import numpy as np
import ml_dtypes


def mxq(x, axis, fmt="e4m3"):
    dtype, down = {"e4m3": (ml_dtypes.float8_e4m3fn, 7), "e5m2": (ml_dtypes.float8_e5m2, 14)}[fmt]
    v = np.moveaxis(np.asarray(x, np.float32).astype(ml_dtypes.bfloat16).astype(np.float64), axis, -1)
    blocks = v.reshape(v.shape[:-1] + (-1, 32))
    amax = np.abs(blocks).max(-1, keepdims=True)
    byte = np.maximum(np.where(amax > 0, np.frexp(amax)[1] - 1 + 127, 0) - down, 1)
    scale = np.exp2(byte - 127.0)
    codes = (blocks / scale).astype(np.float32).astype(dtype).astype(np.float64)
    return np.moveaxis((codes * scale).reshape(v.shape), -1, axis)


WIDE = False


def mx_kscale(k):
    if not WIDE:
        return np.ones(k)
    levels = np.array([10, -10, 5, -5, 0])
    if k % 512:
        return np.exp2(np.random.permutation(np.resize(levels, k // 32))).repeat(32)
    a = np.empty((k // 512, 16))
    for p in range(k // 512):
        a[p, :8] = np.random.permutation(np.resize(levels, 8))
        for g in range(8):
            far = levels[np.abs(levels - a[p, g]) >= 10]
            a[p, g + 8] = far[np.random.randint(len(far))]
    return np.exp2(a.ravel()).repeat(32)


BF16 = ml_dtypes.bfloat16


def bf(x):
    return np.asarray(x, np.float32).astype(BF16)


def f64(x):
    return np.asarray(x).astype(np.float64)


B, N, D, C, H, NS = 2, 1024, 1024, 1024, 16, 10
HD = C // H
D4 = (0.4829629131445341, 0.8365163037378079, 0.2241438680420134, -0.1294095225512604)


def causal_multiscale(x_c, scale_gain):
    g = np.exp(scale_gain - scale_gain.max(0, keepdims=True))
    gains = g / g.sum(0, keepdims=True)
    gains_exp = np.repeat(gains, HD, axis=1)
    out = np.zeros_like(x_c)
    for j in range(NS):
        d = 2 ** j
        xp = np.pad(x_c, ((0, 0), (0, 0), (3 * d, 0)))
        y = (D4[0] * xp[:, :, 0 * d:0 * d + N]
             + D4[1] * xp[:, :, 1 * d:1 * d + N]
             + D4[2] * xp[:, :, 2 * d:2 * d + N]
             + D4[3] * xp[:, :, 3 * d:3 * d + N])
        out = out + gains_exp[j][None, :, None] * y
    return out


def setup_inputs():
    s = mx_kscale(D)
    return {"x": bf(np.random.standard_normal((B, N, D)) * s),
            "k_w": bf(np.random.standard_normal((C, D)) / np.sqrt(D) / s[None, :]),
            "k_b": bf(np.random.standard_normal(C) * 0.2),
            "v_w": bf(np.random.standard_normal((C, D)) / np.sqrt(D) / s[None, :]),
            "v_b": bf(np.random.standard_normal(C) * 0.2),
            "scale_gain": bf(np.random.standard_normal((NS, H)) * 0.5)}


def core(x, k_w, k_b, v_w, v_b, scale_gain):
    xq = mxq(f64(x), 2, "e4m3")
    k = ((xq @ mxq(f64(k_w), 1, "e4m3").T) + f64(k_b)).reshape(B, N, H, HD)
    v = ((xq @ mxq(f64(v_w), 1, "e4m3").T) + f64(v_b)).reshape(B, N, H, HD)
    k_mag = np.sqrt((k * k).sum(-1, keepdims=True))
    field = v * k_mag
    x_c = field.transpose(0, 2, 3, 1).reshape(B, C, N)
    return causal_multiscale(x_c, f64(scale_gain))


def e4m3fn_bytes(y):
    return np.clip(np.asarray(y, np.float64), -448.0, 448.0).astype(np.float32).astype(ml_dtypes.float8_e4m3fn).view(np.uint8)


Y_SCALE = 60.0


def reference(x, k_w, k_b, v_w, v_b, scale_gain):
    out = core(x, k_w, k_b, v_w, v_b, scale_gain)
    return out, e4m3fn_bytes(out * Y_SCALE)

@@ -1,0 +1,165 @@
+from contextlib import ExitStack
+
+import concourse.masks as masks
+import concourse.mybir as mybir
+
+F32 = mybir.dt.float32
+BF16 = mybir.dt.bfloat16
+U32 = mybir.dt.uint32
+U8 = mybir.dt.uint8
+FP8X4 = mybir.dt.float8_e4m3fn_x4
+FP8 = mybir.dt.float8_e4m3fn
+ALU = mybir.AluOpType
+ACT = mybir.ActivationFunctionType
+AX = mybir.AxisListType
+
+B, N, D, C, H, NS = 2, 1024, 1024, 1024, 16, 10
+P = 128
+T0, T1, T2, T3 = 0.4829629131445341, 0.8365163037378079, 0.2241438680420134, -0.1294095225512604
+Y_SCALE = 60.0
+FLOPS = 2 * 2 * B * N * D * C
+
+
+def tile_causalwaveletfieldattentionbyte_pa_kernel(tc, x, k_w, k_b, v_w, v_b, scale_gain, out_0, out_1):
+    nc = tc.nc
+    xf = x.flatten_outer_dims()
+    NT = B * N
+    CT = C // P
+
+    with ExitStack() as ctx:
+        const = ctx.enter_context(tc.tile_pool(name="const", bufs=1))
+        keep = ctx.enter_context(tc.tile_pool(name="keep", bufs=1))
+        rawp = ctx.enter_context(tc.tile_pool(name="rawp", bufs=4))
+        grp = ctx.enter_context(tc.tile_pool(name="grp", bufs=3))
+        work = ctx.enter_context(tc.tile_pool(name="work", bufs=3))
+        fpool = ctx.enter_context(tc.tile_pool(name="fpool", bufs=2))
+        opool = ctx.enter_context(tc.tile_pool(name="opool", bufs=3))
+        tpp = ctx.enter_context(tc.psum_pool(name="tpp", bufs=2))
+        mmp = ctx.enter_context(tc.psum_pool(name="mmp", bufs=2))
+
+        ident_f = const.tile([P, P], F32, name="ident_f")
+        masks.make_identity(nc, ident_f[:])
+        ident_b = const.tile([P, P], BF16, name="ident_b")
+        masks.make_identity(nc, ident_b[:])
+        blk = const.tile([P, P], F32, name="blk")
+        masks.make_block_diagonal(nc, blk[:], 64)
+
+        sg = const.tile([P, NS * H], BF16, name="sg")
+        nc.sync.dma_start(out=sg[:], in_=scale_gain.rearrange("j h -> (j h)").partition_broadcast(P))
+        brow = const.tile([P, P], BF16, name="brow")
+        nc.vector.memset(brow[:], 0.0)
+        nc.sync.dma_start(out=brow[0:8, :], in_=k_b.rearrange("(r c) -> r c", c=P))
+        nc.sync.dma_start(out=brow[8:16, :], in_=v_b.rearrange("(r c) -> r c", c=P))
+
+        lg = const.tile([P, CT, NS], F32, name="lg")
+        sgv = sg[:].rearrange("p (j c t) -> p t c j", j=NS, c=CT, t=2)
+        nc.vector.tensor_copy(out=lg[0:64], in_=sgv[0:64, 0])
+        nc.vector.tensor_copy(out=lg[64:128], in_=sgv[64:128, 1])
+        mx = const.tile([P, CT], F32, name="mx")
+        nc.vector.tensor_reduce(out=mx[:], in_=lg[:], axis=AX.X, op=ALU.max)
+        nc.vector.tensor_tensor(out=lg[:], in0=lg[:], in1=mx[:].unsqueeze(2).to_broadcast([P, CT, NS]), op=ALU.subtract)
+        ex = const.tile([P, CT, NS], F32, name="ex")
+        nc.scalar.activation(out=ex[:], in_=lg[:], func=ACT.Exp)
+        sm = const.tile([P, CT], F32, name="sm")
+        nc.vector.tensor_reduce(out=sm[:], in_=ex[:], axis=AX.X, op=ALU.add)
+        rs = const.tile([P, CT], F32, name="rs")
+        nc.vector.reciprocal(out=rs[:], in_=sm[:])
+        gn = const.tile([P, CT, NS], F32, name="gn")
+        nc.vector.tensor_tensor(out=gn[:], in0=ex[:], in1=rs[:].unsqueeze(2).to_broadcast([P, CT, NS]), op=ALU.mult)
+        g1 = const.tile([P, CT, NS], F32, name="g1")
+        nc.vector.tensor_scalar(out=g1[:], in0=gn[:], scalar1=T1, scalar2=None, op0=ALU.mult)
+        ca = const.tile([P, CT, NS], F32, name="ca")
+        nc.vector.tensor_scalar(out=ca[:], in0=gn[:], scalar1=T2, scalar2=None, op0=ALU.mult)
+        nc.vector.tensor_tensor(out=ca[:, :, 1:NS], in0=ca[:, :, 1:NS], in1=g1[:, :, 0 : NS - 1], op=ALU.add)
+        cb = const.tile([P, CT, NS], F32, name="cb")
+        nc.vector.tensor_scalar(out=cb[:], in0=gn[:], scalar1=T0, scalar2=None, op0=ALU.mult)
+
+        bt = tpp.tile([P, P], BF16, name="bt", tag="tp")
+        nc.tensor.transpose(bt[:], brow[:], ident_b[:])
+        bias = const.tile([P, 16], F32, name="bias")
+        nc.vector.tensor_copy(out=bias[:], in_=bt[:, 0:16])
+
+        x_codes = keep.tile([P, 2, NT], U32, name="x_codes", align_bytes=64)
+        x_scales = keep.tile([P, 2, NT], U8, name="x_scales", align_bytes=64)
+        kw_codes = keep.tile([P, 2, C], U32, name="kw_codes", align_bytes=64)
+        kw_scales = keep.tile([P, 2, C], U8, name="kw_scales", align_bytes=64)
+        vw_codes = keep.tile([P, 2, C], U32, name="vw_codes", align_bytes=64)
+        vw_scales = keep.tile([P, 2, C], U8, name="vw_scales", align_bytes=64)
+
+        def load_quant(rows, codes, scales, col0):
+            raw = rawp.tile([P, D], BF16, name="raw")
+            nc.sync.dma_start(out=raw[:], in_=rows)
+            words = raw[:].bitcast(F32)
+            tp = tpp.tile([P, 2, 2, P], F32, name="tp", tag="tp")
+            for g in range(2):
+                for u in range(2):
+                    nc.tensor.transpose(tp[:, g, u, :], words[:, 256 * g + u : 256 * (g + 1) : 2], ident_f[:])
+            grouped = grp.tile([P, 2, P, 4], BF16, name="grouped", align_bytes=64)
+            nc.vector.tensor_copy(out=grouped[:].bitcast(F32), in_=tp[:].rearrange("p g u r -> p g r u"))
+            for g in range(2):
+                nc.vector.quantize_mx(
+                    out=codes[:, g, col0 : col0 + P].bitcast(FP8X4),
+                    scales=scales[:, g, col0 : col0 + P],
+                    in_=grouped[:, g].rearrange("p r e -> p (r e)"),
+                )
+
+        load_quant(k_w[0:P, :], kw_codes, kw_scales, 0)
+        load_quant(v_w[0:P, :], vw_codes, vw_scales, 0)
+        for t in range(NT // P):
+            load_quant(xf[t * P : (t + 1) * P, :], x_codes, x_scales, t * P)
+        for ct in range(1, CT):
+            load_quant(k_w[ct * P : (ct + 1) * P, :], kw_codes, kw_scales, ct * P)
+            load_quant(v_w[ct * P : (ct + 1) * P, :], vw_codes, vw_scales, ct * P)
+
+        def project(acc, w_codes, w_scales, ct, ch):
+            for g in range(2):
+                nc.tensor.matmul_mx(
+                    out=acc[:],
+                    lhsT=w_codes[:, g, ct * P : (ct + 1) * P].bitcast(FP8X4),
+                    lhsT_scale=w_scales[:, g, ct * P : (ct + 1) * P],
+                    rhs=x_codes[:, g, ch * 512 : (ch + 1) * 512].bitcast(FP8X4),
+                    rhs_scale=x_scales[:, g, ch * 512 : (ch + 1) * 512],
+                    start=(g == 0),
+                    stop=(g == 1),
+                )
+
+        taps = [(2 ** j, ca, j) for j in range(NS)] + [(3 * 2 ** j, cb, j) for j in range(NS - 1)]
+
+        for ct in range(CT):
+            f = fpool.tile([P, NT], F32, name="f")
+            for ch in range(4):
+                kps = mmp.tile([P, 512], F32, name="kps")
+                project(kps, kw_codes, kw_scales, ct, ch)
+                ksq = work.tile([P, 512], F32, name="ksq")
+                nc.scalar.activation(out=ksq[:], in_=kps[:], func=ACT.Square, bias=bias[:, ct : ct + 1], scale=1.0)
+                msq = mmp.tile([P, 512], F32, name="msq")
+                nc.tensor.matmul(msq[:], lhsT=blk[:], rhs=ksq[:], start=True, stop=True)
+                mag = work.tile([P, 512], F32, name="mag")
+                nc.scalar.activation(out=mag[:], in_=msq[:], func=ACT.Sqrt)
+                vps = mmp.tile([P, 512], F32, name="vps")
+                project(vps, vw_codes, vw_scales, ct, ch)
+                nc.vector.scalar_tensor_tensor(
+                    out=f[:, ch * 512 : (ch + 1) * 512],
+                    in0=vps[:],
+                    scalar=bias[:, 8 + ct : 9 + ct],
+                    in1=mag[:],
+                    op0=ALU.add,
+                    op1=ALU.mult,
+                )
+            for b in range(B):
+                fb = f[:, b * N : (b + 1) * N]
+                acc = opool.tile([P, N], F32, name="acc")
+                nc.scalar.activation(out=acc[:], in_=fb, func=ACT.Copy, scale=T3)
+                for s, coef, j in taps:
+                    nc.vector.scalar_tensor_tensor(
+                        out=acc[:, s:N],
+                        in0=fb[:, 0 : N - s],
+                        scalar=coef[:, ct, j : j + 1],
+                        in1=acc[:, s:N],
+                        op0=ALU.mult,
+                        op1=ALU.add,
+                    )
+                nc.sync.dma_start(out=out_0[b, ct * P : (ct + 1) * P, :], in_=acc[:])
+                o8 = opool.tile([P, N], FP8, name="o8")
+                nc.scalar.activation(out=o8[:], in_=acc[:], func=ACT.Copy, scale=Y_SCALE, saturate=False)
+                nc.sync.dma_start(out=out_1[b, ct * P : (ct + 1) * P, :], in_=o8[:].bitcast(U8))

@@ -15,34 +15,34 @@ AX = mybir.AxisListType
 
 B, N, D, C, H, NS = 2, 1024, 1024, 1024, 16, 10
 P = 128
+HD = 64
 T0, T1, T2, T3 = 0.4829629131445341, 0.8365163037378079, 0.2241438680420134, -0.1294095225512604
 Y_SCALE = 60.0
 FLOPS = 2 * 2 * B * N * D * C
+W = 192
+NJ = 7
 
 
 def tile_causalwaveletfieldattentionbyte_pa_kernel(tc, x, k_w, k_b, v_w, v_b, scale_gain, out_0, out_1):
     nc = tc.nc
     xf = x.flatten_outer_dims()
-    NT = B * N
-    CT = C // P
 
     with ExitStack() as ctx:
         const = ctx.enter_context(tc.tile_pool(name="const", bufs=1))
         keep = ctx.enter_context(tc.tile_pool(name="keep", bufs=1))
-        rawp = ctx.enter_context(tc.tile_pool(name="rawp", bufs=4))
-        grp = ctx.enter_context(tc.tile_pool(name="grp", bufs=3))
+        rawp = ctx.enter_context(tc.tile_pool(name="rawp", bufs=6))
+        grp = ctx.enter_context(tc.tile_pool(name="grp", bufs=2))
         work = ctx.enter_context(tc.tile_pool(name="work", bufs=3))
-        fpool = ctx.enter_context(tc.tile_pool(name="fpool", bufs=2))
         opool = ctx.enter_context(tc.tile_pool(name="opool", bufs=3))
-        tpp = ctx.enter_context(tc.psum_pool(name="tpp", bufs=2))
-        mmp = ctx.enter_context(tc.psum_pool(name="mmp", bufs=2))
+        ps = ctx.enter_context(tc.psum_pool(name="ps", bufs=1))
 
         ident_f = const.tile([P, P], F32, name="ident_f")
         masks.make_identity(nc, ident_f[:])
         ident_b = const.tile([P, P], BF16, name="ident_b")
         masks.make_identity(nc, ident_b[:])
         blk = const.tile([P, P], F32, name="blk")
-        masks.make_block_diagonal(nc, blk[:], 64)
+        masks.make_block_diagonal(nc, blk[:], HD)
+        ind2 = blk[:, 0:P:HD]
 
         sg = const.tile([P, NS * H], BF16, name="sg")
         nc.sync.dma_start(out=sg[:], in_=scale_gain.rearrange("j h -> (j h)").partition_broadcast(P))
@@ -51,115 +51,245 @@ def tile_causalwaveletfieldattentionbyte_pa_kernel(tc, x, k_w, k_b, v_w, v_b, sc
         nc.sync.dma_start(out=brow[0:8, :], in_=k_b.rearrange("(r c) -> r c", c=P))
         nc.sync.dma_start(out=brow[8:16, :], in_=v_b.rearrange("(r c) -> r c", c=P))
 
-        lg = const.tile([P, CT, NS], F32, name="lg")
-        sgv = sg[:].rearrange("p (j c t) -> p t c j", j=NS, c=CT, t=2)
-        nc.vector.tensor_copy(out=lg[0:64], in_=sgv[0:64, 0])
-        nc.vector.tensor_copy(out=lg[64:128], in_=sgv[64:128, 1])
-        mx = const.tile([P, CT], F32, name="mx")
+        unit = {}
+        for s in (0, 1, 2, 3, 4, 6, 8, 12, 16, 24, 32, 48, 64):
+            d = const.tile([P, W], F32, name="unit%d" % s)
+            nc.gpsimd.memset(d[:], 0.0)
+            nc.gpsimd.affine_select(
+                out=d[:], in_=d[:], compare_op=ALU.not_equal, fill=1.0,
+                base=s, pattern=[[-1, W]], channel_multiplier=1,
+            )
+            unit[s] = d
+        ybase = const.tile([P, W], F32, name="ybase")
+        nc.vector.tensor_scalar(out=ybase[:], in0=unit[0][:], scalar1=T3, scalar2=None, op0=ALU.mult)
+        yj = []
+        for j in range(NJ):
+            y = const.tile([P, W], F32, name="y%d" % j)
+            nc.vector.tensor_scalar(out=y[:], in0=unit[2 ** j][:], scalar1=T2, scalar2=None, op0=ALU.mult)
+            for mult, tap in ((2, T1), (3, T0)):
+                if mult * 2 ** j <= HD:
+                    nc.vector.scalar_tensor_tensor(
+                        out=y[:], in0=unit[mult * 2 ** j][:], scalar=tap, in1=y[:], op0=ALU.mult, op1=ALU.add,
+                    )
+            yj.append(y)
+
+        lg = const.tile([P, H, NS], F32, name="lg")
+        nc.vector.tensor_copy(out=lg[:], in_=sg[:].rearrange("p (j h) -> p h j", j=NS))
+        mx = const.tile([P, H], F32, name="mx")
         nc.vector.tensor_reduce(out=mx[:], in_=lg[:], axis=AX.X, op=ALU.max)
-        nc.vector.tensor_tensor(out=lg[:], in0=lg[:], in1=mx[:].unsqueeze(2).to_broadcast([P, CT, NS]), op=ALU.subtract)
-        ex = const.tile([P, CT, NS], F32, name="ex")
+        nc.vector.tensor_tensor(out=lg[:], in0=lg[:], in1=mx[:].unsqueeze(2).to_broadcast([P, H, NS]), op=ALU.subtract)
+        ex = const.tile([P, H, NS], F32, name="ex")
         nc.scalar.activation(out=ex[:], in_=lg[:], func=ACT.Exp)
-        sm = const.tile([P, CT], F32, name="sm")
+        sm = const.tile([P, H], F32, name="sm")
         nc.vector.tensor_reduce(out=sm[:], in_=ex[:], axis=AX.X, op=ALU.add)
-        rs = const.tile([P, CT], F32, name="rs")
+        rs = const.tile([P, H], F32, name="rs")
         nc.vector.reciprocal(out=rs[:], in_=sm[:])
-        gn = const.tile([P, CT, NS], F32, name="gn")
-        nc.vector.tensor_tensor(out=gn[:], in0=ex[:], in1=rs[:].unsqueeze(2).to_broadcast([P, CT, NS]), op=ALU.mult)
-        g1 = const.tile([P, CT, NS], F32, name="g1")
+        gn = const.tile([P, H, NS], F32, name="gn")
+        nc.vector.tensor_tensor(out=gn[:], in0=ex[:], in1=rs[:].unsqueeze(2).to_broadcast([P, H, NS]), op=ALU.mult)
+        g1 = const.tile([P, H, NS], F32, name="g1")
         nc.vector.tensor_scalar(out=g1[:], in0=gn[:], scalar1=T1, scalar2=None, op0=ALU.mult)
-        ca = const.tile([P, CT, NS], F32, name="ca")
+        ca = const.tile([P, H, NS], F32, name="ca")
         nc.vector.tensor_scalar(out=ca[:], in0=gn[:], scalar1=T2, scalar2=None, op0=ALU.mult)
         nc.vector.tensor_tensor(out=ca[:, :, 1:NS], in0=ca[:, :, 1:NS], in1=g1[:, :, 0 : NS - 1], op=ALU.add)
-        cb = const.tile([P, CT, NS], F32, name="cb")
+        cb = const.tile([P, H, NS], F32, name="cb")
         nc.vector.tensor_scalar(out=cb[:], in0=gn[:], scalar1=T0, scalar2=None, op0=ALU.mult)
 
-        bt = tpp.tile([P, P], BF16, name="bt", tag="tp")
+        bt = ps.tile([P, P], BF16, name="bt", tag="vt")
         nc.tensor.transpose(bt[:], brow[:], ident_b[:])
         bias = const.tile([P, 16], F32, name="bias")
         nc.vector.tensor_copy(out=bias[:], in_=bt[:, 0:16])
 
-        x_codes = keep.tile([P, 2, NT], U32, name="x_codes", align_bytes=64)
-        x_scales = keep.tile([P, 2, NT], U8, name="x_scales", align_bytes=64)
-        kw_codes = keep.tile([P, 2, C], U32, name="kw_codes", align_bytes=64)
-        kw_scales = keep.tile([P, 2, C], U8, name="kw_scales", align_bytes=64)
-        vw_codes = keep.tile([P, 2, C], U32, name="vw_codes", align_bytes=64)
-        vw_scales = keep.tile([P, 2, C], U8, name="vw_scales", align_bytes=64)
+        counter = [0]
 
-        def load_quant(rows, codes, scales, col0):
+        def to_k_major(rows, grouped_words):
+            i = counter[0]
+            counter[0] = i + 1
             raw = rawp.tile([P, D], BF16, name="raw")
             nc.sync.dma_start(out=raw[:], in_=rows)
             words = raw[:].bitcast(F32)
-            tp = tpp.tile([P, 2, 2, P], F32, name="tp", tag="tp")
+            tp = ps.tile([P, 2, 2, P], F32, name="tp", tag=("pa", "pb", "ft")[i % 3])
             for g in range(2):
                 for u in range(2):
                     nc.tensor.transpose(tp[:, g, u, :], words[:, 256 * g + u : 256 * (g + 1) : 2], ident_f[:])
-            grouped = grp.tile([P, 2, P, 4], BF16, name="grouped", align_bytes=64)
-            nc.vector.tensor_copy(out=grouped[:].bitcast(F32), in_=tp[:].rearrange("p g u r -> p g r u"))
-            for g in range(2):
-                nc.vector.quantize_mx(
-                    out=codes[:, g, col0 : col0 + P].bitcast(FP8X4),
-                    scales=scales[:, g, col0 : col0 + P],
-                    in_=grouped[:, g].rearrange("p r e -> p (r e)"),
-                )
+            if i % 2 == 0:
+                nc.vector.tensor_copy(out=grouped_words, in_=tp[:].rearrange("p g u r -> p g r u"))
+            else:
+                nc.scalar.copy(out=grouped_words, in_=tp[:].rearrange("p g u r -> p g r u"))
 
-        load_quant(k_w[0:P, :], kw_codes, kw_scales, 0)
-        load_quant(v_w[0:P, :], vw_codes, vw_scales, 0)
-        for t in range(NT // P):
-            load_quant(xf[t * P : (t + 1) * P, :], x_codes, x_scales, t * P)
-        for ct in range(1, CT):
-            load_quant(k_w[ct * P : (ct + 1) * P, :], kw_codes, kw_scales, ct * P)
-            load_quant(v_w[ct * P : (ct + 1) * P, :], vw_codes, vw_scales, ct * P)
+        def quantise(grouped, codes, scales):
+            nc.vector.quantize_mx(
+                out=codes[:].rearrange("p g r -> p (g r)").bitcast(FP8X4),
+                scales=scales[:].rearrange("p g r -> p (g r)"),
+                in_=grouped[:].rearrange("p g r e -> p (g r e)"),
+            )
 
-        def project(acc, w_codes, w_scales, ct, ch):
+        wc = {}
+
+        def load_w(name, w, ct):
+            grouped = grp.tile([P, 2, P, 4], BF16, name="gw", align_bytes=64)
+            to_k_major(w[ct * P : (ct + 1) * P, :], grouped[:].bitcast(F32))
+            codes = keep.tile([P, 2, P], U32, name="%sc%d" % (name, ct), align_bytes=64)
+            scales = keep.tile([P, 2, P], U8, name="%ss%d" % (name, ct), align_bytes=64)
+            quantise(grouped, codes, scales)
+            wc[(name, ct)] = (codes, scales)
+
+        xc = []
+
+        def load_x(ch):
+            grouped = grp.tile([P, 2, 512, 4], BF16, name="gx", align_bytes=64)
+            for j in range(4):
+                t = 4 * ch + j
+                to_k_major(xf[t * P : (t + 1) * P, :], grouped[:, :, j * P : (j + 1) * P, :].bitcast(F32))
+            codes = keep.tile([P, 2, 512], U32, name="xc%d" % ch, align_bytes=64)
+            scales = keep.tile([P, 2, 512], U8, name="xs%d" % ch, align_bytes=64)
+            quantise(grouped, codes, scales)
+            xc.append((codes, scales))
+
+        def project(name, ct, ch):
+            acc = ps.tile([P, 512], F32, name="mm", tag="mm", bufs=3)
+            w_codes, w_scales = wc[(name, ct)]
+            x_codes, x_scales = xc[ch]
             for g in range(2):
                 nc.tensor.matmul_mx(
                     out=acc[:],
-                    lhsT=w_codes[:, g, ct * P : (ct + 1) * P].bitcast(FP8X4),
-                    lhsT_scale=w_scales[:, g, ct * P : (ct + 1) * P],
-                    rhs=x_codes[:, g, ch * 512 : (ch + 1) * 512].bitcast(FP8X4),
-                    rhs_scale=x_scales[:, g, ch * 512 : (ch + 1) * 512],
+                    lhsT=w_codes[:, g, :].bitcast(FP8X4),
+                    lhsT_scale=w_scales[:, g, :],
+                    rhs=x_codes[:, g, :].bitcast(FP8X4),
+                    rhs_scale=x_scales[:, g, :],
                     start=(g == 0),
                     stop=(g == 1),
                 )
+            return acc
 
-        taps = [(2 ** j, ca, j) for j in range(NS)] + [(3 * 2 ** j, cb, j) for j in range(NS - 1)]
+        msq = {}
+        mag = {}
+        field = {}
 
-        for ct in range(CT):
-            f = fpool.tile([P, NT], F32, name="f")
-            for ch in range(4):
-                kps = mmp.tile([P, 512], F32, name="kps")
-                project(kps, kw_codes, kw_scales, ct, ch)
-                ksq = work.tile([P, 512], F32, name="ksq")
-                nc.scalar.activation(out=ksq[:], in_=kps[:], func=ACT.Square, bias=bias[:, ct : ct + 1], scale=1.0)
-                msq = mmp.tile([P, 512], F32, name="msq")
-                nc.tensor.matmul(msq[:], lhsT=blk[:], rhs=ksq[:], start=True, stop=True)
-                mag = work.tile([P, 512], F32, name="mag")
-                nc.scalar.activation(out=mag[:], in_=msq[:], func=ACT.Sqrt)
-                vps = mmp.tile([P, 512], F32, name="vps")
-                project(vps, vw_codes, vw_scales, ct, ch)
+        def k_slice(g, c2, ch):
+            ct = 2 * g + c2
+            if g not in msq:
+                msq[g] = ps.tile([P, 16, 4], F32, name="msq", tag="msq")
+            kps = project("k", ct, ch)
+            ksq = work.tile([P, 512], F32, name="ksq")
+            nc.scalar.activation(out=ksq[:], in_=kps[:], func=ACT.Square, bias=bias[:, ct : ct + 1], scale=1.0)
+            for j in range(4):
+                nc.tensor.matmul(
+                    msq[g][:, 4 * ch + j, 2 * c2 : 2 * c2 + 2],
+                    lhsT=ksq[:, j * P : (j + 1) * P], rhs=ind2, start=True, stop=True,
+                )
+
+        def norms(g):
+            mag[g] = keep.tile([P, 16, 4], F32, name="mag%d" % g)
+            nc.scalar.activation(out=mag[g][:], in_=msq[g][:], func=ACT.Sqrt)
+            field[g] = keep.tile([P, 8, 4, 2, HD], F32, name="field%d" % g)
+
+        def v_slice(g, c2, ch):
+            ct = 2 * g + c2
+            vps = project("v", ct, ch)
+            vsb = work.tile([P, 512], F32, name="vsb")
+            nc.scalar.activation(out=vsb[:], in_=vps[:], func=ACT.Identity, bias=bias[:, 8 + ct : 9 + ct], scale=1.0)
+            vt = ps.tile([P, 4, P], F32, name="vt", tag="vt")
+            for j in range(4):
+                nc.tensor.transpose(vt[:, j, :], vsb[:, j * P : (j + 1) * P], ident_f[:])
+            b, i0 = ch // 2, 4 * (ch % 2)
+            nc.vector.tensor_tensor(
+                out=field[g][:, i0 : i0 + 4, 2 * c2 : 2 * c2 + 2, b, :],
+                in0=vt[:].rearrange("p j (h c) -> p j h c", h=2),
+                in1=mag[g][:, 4 * ch : 4 * ch + 4, 2 * c2 : 2 * c2 + 2].unsqueeze(3).to_broadcast([P, 4, 2, HD]),
+                op=ALU.mult,
+            )
+
+        band = {}
+
+        def build_band(h):
+            t = keep.tile([P, W], F32, name="band%d" % h)
+            nc.vector.scalar_tensor_tensor(out=t[:], in0=yj[0][:], scalar=gn[:, h, 0:1], in1=ybase[:], op0=ALU.mult, op1=ALU.add)
+            for j in range(1, NJ):
+                lo = 2 ** j
+                hi = min(W, P + 3 * 2 ** j)
                 nc.vector.scalar_tensor_tensor(
-                    out=f[:, ch * 512 : (ch + 1) * 512],
-                    in0=vps[:],
-                    scalar=bias[:, 8 + ct : 9 + ct],
-                    in1=mag[:],
-                    op0=ALU.add,
-                    op1=ALU.mult,
+                    out=t[:, lo:hi], in0=yj[j][:, lo:hi], scalar=gn[:, h, j : j + 1], in1=t[:, lo:hi], op0=ALU.mult, op1=ALU.add,
+                )
+            band[h] = t
+
+        far_taps = [(96, cb, 5), (128, ca, 7), (192, cb, 6), (256, ca, 8), (384, cb, 7), (512, ca, 9), (768, cb, 8)]
+
+        def head(h):
+            g, hl = divmod(h, 4)
+            banks = (ps.tile([P, 512], F32, name="pa", tag="pa"), ps.tile([P, 512], F32, name="pb", tag="pb"))
+            acc = opool.tile([P, N], F32, name="acc")
+            fts = opool.tile([P, N], F32, name="fts")
+            t = band[h]
+            for half in range(2):
+                ft = ps.tile([P, 4, P], F32, name="ft", tag="ft")
+                for i in range(4 * half, 4 * half + 4):
+                    fi = field[g][:, i, hl].rearrange("p b c -> p (b c)")
+                    if i == 0:
+                        pieces = [(0, W)]
+                    elif i == 3:
+                        pieces = [(0, HD), (HD, P), (P, W)]
+                    elif i == 7:
+                        pieces = [(0, HD), (HD, P)]
+                    else:
+                        pieces = [(0, HD), (HD, W)]
+                    for lo, hi in pieces:
+                        c0 = P * i + lo
+                        nc.tensor.matmul(
+                            banks[c0 // 512][:, c0 % 512 : c0 % 512 + hi - lo],
+                            lhsT=fi, rhs=t[:, lo:hi],
+                            start=(i, lo) in ((0, 0), (3, P)), stop=(c0 + hi - lo) % 512 == 0,
+                        )
+                    nc.tensor.transpose(ft[:, i % 4, :], fi, ident_f[:])
+                nc.scalar.copy(out=acc[:, 512 * half : 512 * (half + 1)], in_=banks[half][:])
+                nc.scalar.copy(out=fts[:, 512 * half : 512 * (half + 1)], in_=ft[:].rearrange("p j n -> p (j n)"))
+            for s, coef, j in far_taps:
+                nc.vector.scalar_tensor_tensor(
+                    out=acc[:, s:N], in0=fts[:, 0 : N - s], scalar=coef[:, h, j : j + 1], in1=acc[:, s:N],
+                    op0=ALU.mult, op1=ALU.add,
                 )
             for b in range(B):
-                fb = f[:, b * N : (b + 1) * N]
-                acc = opool.tile([P, N], F32, name="acc")
-                nc.scalar.activation(out=acc[:], in_=fb, func=ACT.Copy, scale=T3)
-                for s, coef, j in taps:
-                    nc.vector.scalar_tensor_tensor(
-                        out=acc[:, s:N],
-                        in0=fb[:, 0 : N - s],
-                        scalar=coef[:, ct, j : j + 1],
-                        in1=acc[:, s:N],
-                        op0=ALU.mult,
-                        op1=ALU.add,
-                    )
-                nc.sync.dma_start(out=out_0[b, ct * P : (ct + 1) * P, :], in_=acc[:])
+                nc.sync.dma_start(out=out_0[b, h * HD : (h + 1) * HD, :], in_=acc[b * HD : (b + 1) * HD, :])
+
+        def bytes_out(ct):
+            for b in range(B):
+                u = opool.tile([P, N], F32, name="u")
+                nc.gpsimd.dma_start(out=u[:], in_=out_0[b, ct * P : (ct + 1) * P, :])
                 o8 = opool.tile([P, N], FP8, name="o8")
-                nc.scalar.activation(out=o8[:], in_=acc[:], func=ACT.Copy, scale=Y_SCALE, saturate=False)
+                nc.scalar.activation(out=o8[:], in_=u[:], func=ACT.Copy, scale=Y_SCALE, saturate=False)
                 nc.sync.dma_start(out=out_1[b, ct * P : (ct + 1) * P, :], in_=o8[:].bitcast(U8))
+
+        def load_group(g):
+            for c2 in range(2):
+                load_w("k", k_w, 2 * g + c2)
+            for c2 in range(2):
+                load_w("v", v_w, 2 * g + c2)
+
+        load_group(0)
+        for ch in range(4):
+            load_x(ch)
+            for c2 in range(2):
+                k_slice(0, c2, ch)
+        norms(0)
+        for h in range(4):
+            build_band(h)
+        load_group(1)
+        for ch in range(4):
+            for c2 in range(2):
+                v_slice(0, c2, ch)
+        load_group(2)
+        load_group(3)
+
+        for g in range(4):
+            nxt = []
+            if g < 3:
+                nxt = [(k_slice, c2, ch) for ch in range(4) for c2 in range(2)] + [(v_slice, c2, ch) for ch in range(4) for c2 in range(2)]
+            for hl in range(4):
+                if g < 3:
+                    build_band(4 * (g + 1) + hl)
+                head(4 * g + hl)
+                for fn, c2, ch in nxt[4 * hl : 4 * hl + 4]:
+                    fn(g + 1, c2, ch)
+                if g < 3 and hl == 1:
+                    norms(g + 1)
+                if hl % 2 == 1:
+                    bytes_out(2 * g + hl // 2)

@@ -16,11 +16,14 @@ AX = mybir.AxisListType
 B, N, D, C, H, NS = 2, 1024, 1024, 1024, 16, 10
 P = 128
 HD = 64
+CT = C // P
 T0, T1, T2, T3 = 0.4829629131445341, 0.8365163037378079, 0.2241438680420134, -0.1294095225512604
+TAPS = ((1, T2), (2, T1), (3, T0))
 Y_SCALE = 60.0
 FLOPS = 2 * 2 * B * N * D * C
-W = 192
-NJ = 7
+R = 4
+W = 2 * P
+PAD = 8
 
 
 def tile_causalwaveletfieldattentionbyte_pa_kernel(tc, x, k_w, k_b, v_w, v_b, scale_gain, out_0, out_1):
@@ -30,19 +33,19 @@ def tile_causalwaveletfieldattentionbyte_pa_kernel(tc, x, k_w, k_b, v_w, v_b, sc
     with ExitStack() as ctx:
         const = ctx.enter_context(tc.tile_pool(name="const", bufs=1))
         keep = ctx.enter_context(tc.tile_pool(name="keep", bufs=1))
-        rawp = ctx.enter_context(tc.tile_pool(name="rawp", bufs=6))
+        rawx = ctx.enter_context(tc.tile_pool(name="rawx", bufs=8))
+        raww = ctx.enter_context(tc.tile_pool(name="raww", bufs=8))
         grp = ctx.enter_context(tc.tile_pool(name="grp", bufs=2))
         work = ctx.enter_context(tc.tile_pool(name="work", bufs=3))
+        fpool = ctx.enter_context(tc.tile_pool(name="fpool", bufs=3))
+        bpool = ctx.enter_context(tc.tile_pool(name="bpool", bufs=2))
         opool = ctx.enter_context(tc.tile_pool(name="opool", bufs=3))
-        ps = ctx.enter_context(tc.psum_pool(name="ps", bufs=1))
+        ps = ctx.enter_context(tc.psum_pool(name="ps", bufs=2))
 
         ident_f = const.tile([P, P], F32, name="ident_f")
         masks.make_identity(nc, ident_f[:])
         ident_b = const.tile([P, P], BF16, name="ident_b")
         masks.make_identity(nc, ident_b[:])
-        blk = const.tile([P, P], F32, name="blk")
-        masks.make_block_diagonal(nc, blk[:], HD)
-        ind2 = blk[:, 0:P:HD]
 
         sg = const.tile([P, NS * H], BF16, name="sg")
         nc.sync.dma_start(out=sg[:], in_=scale_gain.rearrange("j h -> (j h)").partition_broadcast(P))
@@ -51,27 +54,24 @@ def tile_causalwaveletfieldattentionbyte_pa_kernel(tc, x, k_w, k_b, v_w, v_b, sc
         nc.sync.dma_start(out=brow[0:8, :], in_=k_b.rearrange("(r c) -> r c", c=P))
         nc.sync.dma_start(out=brow[8:16, :], in_=v_b.rearrange("(r c) -> r c", c=P))
 
-        unit = {}
-        for s in (0, 1, 2, 3, 4, 6, 8, 12, 16, 24, 32, 48, 64):
-            d = const.tile([P, W], F32, name="unit%d" % s)
-            nc.gpsimd.memset(d[:], 0.0)
-            nc.gpsimd.affine_select(
-                out=d[:], in_=d[:], compare_op=ALU.not_equal, fill=1.0,
-                base=s, pattern=[[-1, W]], channel_multiplier=1,
-            )
-            unit[s] = d
-        ybase = const.tile([P, W], F32, name="ybase")
-        nc.vector.tensor_scalar(out=ybase[:], in0=unit[0][:], scalar1=T3, scalar2=None, op0=ALU.mult)
-        yj = []
-        for j in range(NJ):
-            y = const.tile([P, W], F32, name="y%d" % j)
-            nc.vector.tensor_scalar(out=y[:], in0=unit[2 ** j][:], scalar1=T2, scalar2=None, op0=ALU.mult)
-            for mult, tap in ((2, T1), (3, T0)):
-                if mult * 2 ** j <= HD:
-                    nc.vector.scalar_tensor_tensor(
-                        out=y[:], in0=unit[mult * 2 ** j][:], scalar=tap, in1=y[:], op0=ALU.mult, op1=ALU.add,
-                    )
-            yj.append(y)
+        raw_w = {}
+
+        def fetch_w(ct):
+            for name, w in (("k", k_w), ("v", v_w)):
+                raw = raww.tile([P, D], BF16, name="raw_w")
+                nc.sync.dma_start(out=raw[:], in_=w[ct * P : (ct + 1) * P, :])
+                raw_w[(name, ct)] = raw
+
+        raw_x = {}
+
+        def fetch_x(ch):
+            for r in range(R):
+                raw = rawx.tile([P, D], BF16, name="raw_x")
+                nc.sync.dma_start(out=raw[:], in_=xf[512 * ch + r : 512 * (ch + 1) : R, :])
+                raw_x[(ch, r)] = raw
+
+        fetch_w(0)
+        fetch_x(0)
 
         lg = const.tile([P, H, NS], F32, name="lg")
         nc.vector.tensor_copy(out=lg[:], in_=sg[:].rearrange("p (j h) -> p h j", j=NS))
@@ -86,6 +86,22 @@ def tile_causalwaveletfieldattentionbyte_pa_kernel(tc, x, k_w, k_b, v_w, v_b, sc
         nc.vector.reciprocal(out=rs[:], in_=sm[:])
         gn = const.tile([P, H, NS], F32, name="gn")
         nc.vector.tensor_tensor(out=gn[:], in0=ex[:], in1=rs[:].unsqueeze(2).to_broadcast([P, H, NS]), op=ALU.mult)
+        gp = const.tile([P, CT, NS], F32, name="gp")
+        gnv = gn[:].rearrange("p (c t) j -> p t c j", t=2)
+        nc.vector.tensor_copy(out=gp[0:HD], in_=gnv[0:HD, 0])
+        nc.vector.tensor_copy(out=gp[HD:P], in_=gnv[HD:P, 1])
+        cp = const.tile([P, CT, 4], F32, name="cp")
+        nc.vector.tensor_scalar(out=cp[:, :, 0:1], in0=gp[:, :, 0:1], scalar1=T2, scalar2=None, op0=ALU.mult)
+        nc.vector.tensor_scalar(out=cp[:, :, 1:2], in0=gp[:, :, 0:1], scalar1=T1, scalar2=None, op0=ALU.mult)
+        nc.vector.scalar_tensor_tensor(out=cp[:, :, 1:2], in0=gp[:, :, 1:2], scalar=T2, in1=cp[:, :, 1:2], op0=ALU.mult, op1=ALU.add)
+        nc.vector.tensor_scalar(out=cp[:, :, 2:4], in0=gp[:, :, 0:2], scalar1=T0, scalar2=None, op0=ALU.mult)
+        near = ((1, 0), (2, 1), (3, 2), (6, 3))
+
+        bt = ps.tile([P, P], BF16, name="bt", tag="mm")
+        nc.tensor.transpose(bt[:], brow[:], ident_b[:])
+        bias = const.tile([P, 16], F32, name="bias")
+        nc.vector.tensor_copy(out=bias[:], in_=bt[:, 0:16])
+
         g1 = const.tile([P, H, NS], F32, name="g1")
         nc.vector.tensor_scalar(out=g1[:], in0=gn[:], scalar1=T1, scalar2=None, op0=ALU.mult)
         ca = const.tile([P, H, NS], F32, name="ca")
@@ -93,60 +109,67 @@ def tile_causalwaveletfieldattentionbyte_pa_kernel(tc, x, k_w, k_b, v_w, v_b, sc
         nc.vector.tensor_tensor(out=ca[:, :, 1:NS], in0=ca[:, :, 1:NS], in1=g1[:, :, 0 : NS - 1], op=ALU.add)
         cb = const.tile([P, H, NS], F32, name="cb")
         nc.vector.tensor_scalar(out=cb[:], in0=gn[:], scalar1=T0, scalar2=None, op0=ALU.mult)
+        row0 = [(2 ** j // R, ca, j) for j in range(2, NS)] + [(3 * 2 ** j // R, cb, j) for j in range(2, NS - 1)]
+        band = {}
+        for h_lo, h_hi in ((0, 4), (4, H)):
+            t = keep.tile([P, h_hi - h_lo, W], F32, name="toep%d" % h_lo)
+            nc.gpsimd.memset(t[:], 0.0)
+            nc.vector.tensor_scalar(out=t[0:1, :, 0:1], in0=gn[0:1, h_lo:h_hi, 0:1], scalar1=0.0, scalar2=T3, op0=ALU.mult, op1=ALU.add)
+            for s, coef, j in row0:
+                nc.vector.tensor_copy(out=t[0:1, :, s : s + 1], in_=coef[0:1, h_lo:h_hi, j : j + 1])
+            for cnt, mults in ((1, (1, 2, 3)), (4, (1, 2, 3)), (16, (1, 2, 3)), (64, (1,))):
+                for m in mults:
+                    a = m * cnt
+                    nc.gpsimd.dma_start(out=t[a : a + cnt, :, a:W], in_=t[0:cnt, :, 0 : W - a])
+            for h in range(h_lo, h_hi):
+                band[h] = t[:, h - h_lo, :]
 
-        bt = ps.tile([P, P], BF16, name="bt", tag="vt")
-        nc.tensor.transpose(bt[:], brow[:], ident_b[:])
-        bias = const.tile([P, 16], F32, name="bias")
-        nc.vector.tensor_copy(out=bias[:], in_=bt[:, 0:16])
+        def build_band(h):
+            return None
 
         counter = [0]
 
-        def to_k_major(rows, grouped_words):
+        def to_k_major(raw, grouped_words):
             i = counter[0]
             counter[0] = i + 1
-            raw = rawp.tile([P, D], BF16, name="raw")
-            nc.sync.dma_start(out=raw[:], in_=rows)
             words = raw[:].bitcast(F32)
-            tp = ps.tile([P, 2, 2, P], F32, name="tp", tag=("pa", "pb", "ft")[i % 3])
+            tp = ps.tile([P, 2, 2, P], F32, name="tp", tag=("tr", "pt", "pb")[i % 3])
             for g in range(2):
                 for u in range(2):
                     nc.tensor.transpose(tp[:, g, u, :], words[:, 256 * g + u : 256 * (g + 1) : 2], ident_f[:])
-            if i % 2 == 0:
-                nc.vector.tensor_copy(out=grouped_words, in_=tp[:].rearrange("p g u r -> p g r u"))
-            else:
-                nc.scalar.copy(out=grouped_words, in_=tp[:].rearrange("p g u r -> p g r u"))
+            nc.scalar.copy(out=grouped_words, in_=tp[:].rearrange("p g u r -> p g r u"))
 
-        def quantise(grouped, codes, scales):
+        def quantise(grouped, codes, scl):
             nc.vector.quantize_mx(
                 out=codes[:].rearrange("p g r -> p (g r)").bitcast(FP8X4),
-                scales=scales[:].rearrange("p g r -> p (g r)"),
+                scales=scl[:].rearrange("p g r -> p (g r)"),
                 in_=grouped[:].rearrange("p g r e -> p (g r e)"),
             )
 
         wc = {}
 
-        def load_w(name, w, ct):
-            grouped = grp.tile([P, 2, P, 4], BF16, name="gw", align_bytes=64)
-            to_k_major(w[ct * P : (ct + 1) * P, :], grouped[:].bitcast(F32))
-            codes = keep.tile([P, 2, P], U32, name="%sc%d" % (name, ct), align_bytes=64)
-            scales = keep.tile([P, 2, P], U8, name="%ss%d" % (name, ct), align_bytes=64)
-            quantise(grouped, codes, scales)
-            wc[(name, ct)] = (codes, scales)
+        def prep_w(ct):
+            for name in ("k", "v"):
+                grouped = grp.tile([P, 2, P, 4], BF16, name="gw", align_bytes=64)
+                to_k_major(raw_w[(name, ct)], grouped[:].bitcast(F32))
+                codes = keep.tile([P, 2, P], U32, name="%sc%d" % (name, ct), align_bytes=64)
+                scl = keep.tile([P, 2, P], U8, name="%ss%d" % (name, ct), align_bytes=64)
+                quantise(grouped, codes, scl)
+                wc[(name, ct)] = (codes, scl)
 
-        xc = []
+        xc = {}
 
-        def load_x(ch):
+        def prep_x(ch):
             grouped = grp.tile([P, 2, 512, 4], BF16, name="gx", align_bytes=64)
-            for j in range(4):
-                t = 4 * ch + j
-                to_k_major(xf[t * P : (t + 1) * P, :], grouped[:, :, j * P : (j + 1) * P, :].bitcast(F32))
+            for r in range(R):
+                to_k_major(raw_x[(ch, r)], grouped[:, :, r * P : (r + 1) * P, :].bitcast(F32))
             codes = keep.tile([P, 2, 512], U32, name="xc%d" % ch, align_bytes=64)
-            scales = keep.tile([P, 2, 512], U8, name="xs%d" % ch, align_bytes=64)
-            quantise(grouped, codes, scales)
-            xc.append((codes, scales))
+            scl = keep.tile([P, 2, 512], U8, name="xs%d" % ch, align_bytes=64)
+            quantise(grouped, codes, scl)
+            xc[ch] = (codes, scl)
 
         def project(name, ct, ch):
-            acc = ps.tile([P, 512], F32, name="mm", tag="mm", bufs=3)
+            acc = ps.tile([P, 512], F32, name="mm", tag="mm")
             w_codes, w_scales = wc[(name, ct)]
             x_codes, x_scales = xc[ch]
             for g in range(2):
@@ -165,131 +188,159 @@ def tile_causalwaveletfieldattentionbyte_pa_kernel(tc, x, k_w, k_b, v_w, v_b, sc
         mag = {}
         field = {}
 
-        def k_slice(g, c2, ch):
-            ct = 2 * g + c2
-            if g not in msq:
-                msq[g] = ps.tile([P, 16, 4], F32, name="msq", tag="msq")
+        def k_mx(ct, ch):
             kps = project("k", ct, ch)
             ksq = work.tile([P, 512], F32, name="ksq")
             nc.scalar.activation(out=ksq[:], in_=kps[:], func=ACT.Square, bias=bias[:, ct : ct + 1], scale=1.0)
-            for j in range(4):
-                nc.tensor.matmul(
-                    msq[g][:, 4 * ch + j, 2 * c2 : 2 * c2 + 2],
-                    lhsT=ksq[:, j * P : (j + 1) * P], rhs=ind2, start=True, stop=True,
-                )
+            return ksq
 
-        def norms(g):
-            mag[g] = keep.tile([P, 16, 4], F32, name="mag%d" % g)
-            nc.scalar.activation(out=mag[g][:], in_=msq[g][:], func=ACT.Sqrt)
-            field[g] = keep.tile([P, 8, 4, 2, HD], F32, name="field%d" % g)
+        def k_tr(ct, ch, ksq):
+            if ct not in msq:
+                msq[ct] = work.tile([P, 4, R, 2], F32, name="msq")
+            kt = ps.tile([P, R, P], F32, name="kt", tag="tr")
+            for r in range(R):
+                nc.tensor.transpose(kt[:, r, :], ksq[:, r * P : (r + 1) * P], ident_f[:])
+            nc.vector.tensor_reduce(out=msq[ct][:, ch], in_=kt[:].rearrange("p r (h c) -> p r h c", h=2), axis=AX.X, op=ALU.add)
 
-        def v_slice(g, c2, ch):
-            ct = 2 * g + c2
+        def norms(ct):
+            mag[ct] = work.tile([P, 4, R, 2], F32, name="mag")
+            nc.scalar.activation(out=mag[ct][:], in_=msq[ct][:], func=ACT.Sqrt)
+            field[ct] = fpool.tile([P, 2, R, B, P], F32, name="field")
+
+        def v_mx(ct, ch):
             vps = project("v", ct, ch)
             vsb = work.tile([P, 512], F32, name="vsb")
             nc.scalar.activation(out=vsb[:], in_=vps[:], func=ACT.Identity, bias=bias[:, 8 + ct : 9 + ct], scale=1.0)
-            vt = ps.tile([P, 4, P], F32, name="vt", tag="vt")
-            for j in range(4):
-                nc.tensor.transpose(vt[:, j, :], vsb[:, j * P : (j + 1) * P], ident_f[:])
-            b, i0 = ch // 2, 4 * (ch % 2)
+            return vsb
+
+        def v_tr(ct, ch, vsb):
+            vt = ps.tile([P, R, P], F32, name="vt", tag="tr")
+            for r in range(R):
+                nc.tensor.transpose(vt[:, r, :], vsb[:, r * P : (r + 1) * P], ident_f[:])
+            b, a = divmod(ch, 2)
             nc.vector.tensor_tensor(
-                out=field[g][:, i0 : i0 + 4, 2 * c2 : 2 * c2 + 2, b, :],
-                in0=vt[:].rearrange("p j (h c) -> p j h c", h=2),
-                in1=mag[g][:, 4 * ch : 4 * ch + 4, 2 * c2 : 2 * c2 + 2].unsqueeze(3).to_broadcast([P, 4, 2, HD]),
+                out=field[ct][:, a, :, b, :].rearrange("p r (h c) -> p r h c", h=2),
+                in0=vt[:].rearrange("p r (h c) -> p r h c", h=2),
+                in1=mag[ct][:, ch].unsqueeze(3).to_broadcast([P, R, 2, HD]),
                 op=ALU.mult,
             )
 
-        band = {}
+        far = {}
 
-        def build_band(h):
-            t = keep.tile([P, W], F32, name="band%d" % h)
-            nc.vector.scalar_tensor_tensor(out=t[:], in0=yj[0][:], scalar=gn[:, h, 0:1], in1=ybase[:], op0=ALU.mult, op1=ALU.add)
-            for j in range(1, NJ):
-                lo = 2 ** j
-                hi = min(W, P + 3 * 2 ** j)
+        def toeplitz(ct, h2):
+            if ct not in far:
+                far[ct] = bpool.tile([P, 2, R, B, P], F32, name="far")
+            t = band[2 * ct + h2]
+            cols = slice(h2 * HD, (h2 + 1) * HD)
+            for a in range(2):
+                pb = ps.tile([P, R, B, HD], F32, name="pb", tag="pb")
+                nc.tensor.matmul(pb[:], lhsT=t[:, 0:P], rhs=field[ct][:, a, :, :, cols], start=True, stop=(a == 0))
+                if a == 1:
+                    nc.tensor.matmul(pb[:], lhsT=t[:, P:W], rhs=field[ct][:, 0, :, :, cols], start=False, stop=True)
+                nc.scalar.copy(out=far[ct][:, a, :, :, cols], in_=pb[:])
+
+        fts = []
+        for i in range(3):
+            t = const.tile([P, PAD + N], F32, name="fts%d" % i)
+            nc.gpsimd.memset(t[:, 0:PAD], 0.0)
+            fts.append(t)
+        accs = {}
+
+        def finish(ct, b, a):
+            ftb = fts[(2 * ct + b) % 3]
+            if a == 0:
+                accs[(ct, b)] = opool.tile([P, N], F32, name="acc")
+            acc = accs[(ct, b)]
+            pt = ps.tile([P, R, P], F32, name="pt", tag="pt")
+            ft = ps.tile([P, R, P], F32, name="ft", tag="tr")
+            for r in range(R):
+                nc.tensor.transpose(ft[:, r, :], field[ct][:, a, r, b, :], ident_f[:])
+            for r in range(R):
+                nc.tensor.transpose(pt[:, r, :], far[ct][:, a, r, b, :], ident_f[:])
+            lo = 512 * a
+            nc.scalar.copy(
+                out=ftb[:, PAD + lo : PAD + lo + 512].rearrange("p (q r) -> p q r", r=R),
+                in_=ft[:].rearrange("p r q -> p q r"),
+            )
+            s, k = near[0]
+            nc.vector.scalar_tensor_tensor(
+                out=acc[:, lo : lo + 512].rearrange("p (q r) -> p q r", r=R),
+                in0=ftb[:, PAD - s + lo : PAD - s + lo + 512].rearrange("p (q r) -> p q r", r=R),
+                scalar=cp[:, ct, k : k + 1],
+                in1=pt[:].rearrange("p r q -> p q r"),
+                op0=ALU.mult, op1=ALU.add,
+            )
+
+        def near_taps(ct, b):
+            ftb = fts[(2 * ct + b) % 3]
+            acc = accs[(ct, b)]
+            for s, k in near[1:]:
                 nc.vector.scalar_tensor_tensor(
-                    out=t[:, lo:hi], in0=yj[j][:, lo:hi], scalar=gn[:, h, j : j + 1], in1=t[:, lo:hi], op0=ALU.mult, op1=ALU.add,
-                )
-            band[h] = t
-
-        far_taps = [(96, cb, 5), (128, ca, 7), (192, cb, 6), (256, ca, 8), (384, cb, 7), (512, ca, 9), (768, cb, 8)]
-
-        def head(h):
-            g, hl = divmod(h, 4)
-            banks = (ps.tile([P, 512], F32, name="pa", tag="pa"), ps.tile([P, 512], F32, name="pb", tag="pb"))
-            acc = opool.tile([P, N], F32, name="acc")
-            fts = opool.tile([P, N], F32, name="fts")
-            t = band[h]
-            for half in range(2):
-                ft = ps.tile([P, 4, P], F32, name="ft", tag="ft")
-                for i in range(4 * half, 4 * half + 4):
-                    fi = field[g][:, i, hl].rearrange("p b c -> p (b c)")
-                    if i == 0:
-                        pieces = [(0, W)]
-                    elif i == 3:
-                        pieces = [(0, HD), (HD, P), (P, W)]
-                    elif i == 7:
-                        pieces = [(0, HD), (HD, P)]
-                    else:
-                        pieces = [(0, HD), (HD, W)]
-                    for lo, hi in pieces:
-                        c0 = P * i + lo
-                        nc.tensor.matmul(
-                            banks[c0 // 512][:, c0 % 512 : c0 % 512 + hi - lo],
-                            lhsT=fi, rhs=t[:, lo:hi],
-                            start=(i, lo) in ((0, 0), (3, P)), stop=(c0 + hi - lo) % 512 == 0,
-                        )
-                    nc.tensor.transpose(ft[:, i % 4, :], fi, ident_f[:])
-                nc.scalar.copy(out=acc[:, 512 * half : 512 * (half + 1)], in_=banks[half][:])
-                nc.scalar.copy(out=fts[:, 512 * half : 512 * (half + 1)], in_=ft[:].rearrange("p j n -> p (j n)"))
-            for s, coef, j in far_taps:
-                nc.vector.scalar_tensor_tensor(
-                    out=acc[:, s:N], in0=fts[:, 0 : N - s], scalar=coef[:, h, j : j + 1], in1=acc[:, s:N],
+                    out=acc[:], in0=ftb[:, PAD - s : PAD - s + N], scalar=cp[:, ct, k : k + 1], in1=acc[:],
                     op0=ALU.mult, op1=ALU.add,
                 )
-            for b in range(B):
-                nc.sync.dma_start(out=out_0[b, h * HD : (h + 1) * HD, :], in_=acc[b * HD : (b + 1) * HD, :])
+            rows = slice(ct * P, (ct + 1) * P)
+            nc.sync.dma_start(out=out_0[b, rows, :], in_=acc[:])
+            o8 = opool.tile([P, N], FP8, name="o8")
+            nc.scalar.activation(out=o8[:], in_=acc[:], func=ACT.Copy, scale=Y_SCALE, saturate=False)
+            nc.sync.dma_start(out=out_1[b, rows, :], in_=o8[:].bitcast(U8))
 
-        def bytes_out(ct):
-            for b in range(B):
-                u = opool.tile([P, N], F32, name="u")
-                nc.gpsimd.dma_start(out=u[:], in_=out_0[b, ct * P : (ct + 1) * P, :])
-                o8 = opool.tile([P, N], FP8, name="o8")
-                nc.scalar.activation(out=o8[:], in_=u[:], func=ACT.Copy, scale=Y_SCALE, saturate=False)
-                nc.sync.dma_start(out=out_1[b, ct * P : (ct + 1) * P, :], in_=o8[:].bitcast(U8))
-
-        def load_group(g):
-            for c2 in range(2):
-                load_w("k", k_w, 2 * g + c2)
-            for c2 in range(2):
-                load_w("v", v_w, 2 * g + c2)
-
-        load_group(0)
-        for ch in range(4):
-            load_x(ch)
-            for c2 in range(2):
-                k_slice(0, c2, ch)
+        prep_w(0)
+        fetch_x(1)
+        prep_x(0)
+        fetch_x(2)
+        prep_x(1)
+        s0 = k_mx(0, 0)
+        fetch_x(3)
+        prep_x(2)
+        k_tr(0, 0, s0)
+        s1 = k_mx(0, 1)
+        fetch_w(1)
+        fetch_w(2)
+        prep_x(3)
+        k_tr(0, 1, s1)
+        s2 = k_mx(0, 2)
+        s3 = k_mx(0, 3)
+        build_band(0)
+        build_band(1)
+        prep_w(1)
+        k_tr(0, 2, s2)
+        k_tr(0, 3, s3)
         norms(0)
-        for h in range(4):
-            build_band(h)
-        load_group(1)
-        for ch in range(4):
-            for c2 in range(2):
-                v_slice(0, c2, ch)
-        load_group(2)
-        load_group(3)
+        for pair in ((0, 1), (2, 3)):
+            sl = [v_mx(0, ch) for ch in pair]
+            for ch, vsb in zip(pair, sl):
+                v_tr(0, ch, vsb)
 
-        for g in range(4):
-            nxt = []
-            if g < 3:
-                nxt = [(k_slice, c2, ch) for ch in range(4) for c2 in range(2)] + [(v_slice, c2, ch) for ch in range(4) for c2 in range(2)]
-            for hl in range(4):
-                if g < 3:
-                    build_band(4 * (g + 1) + hl)
-                head(4 * g + hl)
-                for fn, c2, ch in nxt[4 * hl : 4 * hl + 4]:
-                    fn(g + 1, c2, ch)
-                if g < 3 and hl == 1:
-                    norms(g + 1)
-                if hl % 2 == 1:
-                    bytes_out(2 * g + hl // 2)
+        for ct in range(CT):
+            n = ct + 1
+            more = n < CT
+            if ct + 3 < CT:
+                fetch_w(ct + 3)
+            sl = [k_mx(n, ch) for ch in (0, 1)] if more else []
+            toeplitz(ct, 0)
+            for ch, ksq in enumerate(sl):
+                k_tr(n, ch, ksq)
+            if more:
+                build_band(2 * n)
+            sl = [k_mx(n, ch) for ch in (2, 3)] if more else []
+            toeplitz(ct, 1)
+            for ch, ksq in enumerate(sl):
+                k_tr(n, 2 + ch, ksq)
+            if more:
+                norms(n)
+                build_band(2 * n + 1)
+            sl = [v_mx(n, ch) for ch in (0, 1)] if more else []
+            finish(ct, 0, 0)
+            finish(ct, 0, 1)
+            for ch, vsb in enumerate(sl):
+                v_tr(n, ch, vsb)
+            near_taps(ct, 0)
+            sl = [v_mx(n, ch) for ch in (2, 3)] if more else []
+            finish(ct, 1, 0)
+            finish(ct, 1, 1)
+            for ch, vsb in enumerate(sl):
+                v_tr(n, 2 + ch, vsb)
+            near_taps(ct, 1)
+            if ct + 2 < CT:
+                prep_w(ct + 2)

@@ -24,6 +24,7 @@ FLOPS = 2 * 2 * B * N * D * C
 R = 4
 W = 2 * P
 PAD = 8
+BANKS = {"mm": 4, "pb": 2, "ft": 1, "pt": 1}
 
 
 def tile_causalwaveletfieldattentionbyte_pa_kernel(tc, x, k_w, k_b, v_w, v_b, scale_gain, out_0, out_1):
@@ -36,23 +37,20 @@ def tile_causalwaveletfieldattentionbyte_pa_kernel(tc, x, k_w, k_b, v_w, v_b, sc
         rawx = ctx.enter_context(tc.tile_pool(name="rawx", bufs=8))
         raww = ctx.enter_context(tc.tile_pool(name="raww", bufs=8))
         grp = ctx.enter_context(tc.tile_pool(name="grp", bufs=2))
-        work = ctx.enter_context(tc.tile_pool(name="work", bufs=3))
-        fpool = ctx.enter_context(tc.tile_pool(name="fpool", bufs=3))
-        bpool = ctx.enter_context(tc.tile_pool(name="bpool", bufs=2))
+        work = ctx.enter_context(tc.tile_pool(name="work", bufs=4))
+        fpool = ctx.enter_context(tc.tile_pool(name="fpool", bufs=4))
+        bpool = ctx.enter_context(tc.tile_pool(name="bpool", bufs=3))
         opool = ctx.enter_context(tc.tile_pool(name="opool", bufs=3))
-        ps = ctx.enter_context(tc.psum_pool(name="ps", bufs=2))
+        ps = ctx.enter_context(tc.psum_pool(name="ps", bufs=1))
 
         ident_f = const.tile([P, P], F32, name="ident_f")
         masks.make_identity(nc, ident_f[:])
-        ident_b = const.tile([P, P], BF16, name="ident_b")
-        masks.make_identity(nc, ident_b[:])
 
         sg = const.tile([P, NS * H], BF16, name="sg")
         nc.sync.dma_start(out=sg[:], in_=scale_gain.rearrange("j h -> (j h)").partition_broadcast(P))
-        brow = const.tile([P, P], BF16, name="brow")
-        nc.vector.memset(brow[:], 0.0)
-        nc.sync.dma_start(out=brow[0:8, :], in_=k_b.rearrange("(r c) -> r c", c=P))
-        nc.sync.dma_start(out=brow[8:16, :], in_=v_b.rearrange("(r c) -> r c", c=P))
+
+        kbb = const.tile([P, C], BF16, name="kbb")
+        vbb = const.tile([P, C], BF16, name="vbb")
 
         raw_w = {}
 
@@ -72,6 +70,8 @@ def tile_causalwaveletfieldattentionbyte_pa_kernel(tc, x, k_w, k_b, v_w, v_b, sc
 
         fetch_w(0)
         fetch_x(0)
+        nc.sync.dma_start(out=kbb[:], in_=k_b.partition_broadcast(P))
+        nc.sync.dma_start(out=vbb[:], in_=v_b.partition_broadcast(P))
 
         lg = const.tile([P, H, NS], F32, name="lg")
         nc.vector.tensor_copy(out=lg[:], in_=sg[:].rearrange("p (j h) -> p h j", j=NS))
@@ -96,11 +96,6 @@ def tile_causalwaveletfieldattentionbyte_pa_kernel(tc, x, k_w, k_b, v_w, v_b, sc
         nc.vector.scalar_tensor_tensor(out=cp[:, :, 1:2], in0=gp[:, :, 1:2], scalar=T2, in1=cp[:, :, 1:2], op0=ALU.mult, op1=ALU.add)
         nc.vector.tensor_scalar(out=cp[:, :, 2:4], in0=gp[:, :, 0:2], scalar1=T0, scalar2=None, op0=ALU.mult)
         near = ((1, 0), (2, 1), (3, 2), (6, 3))
-
-        bt = ps.tile([P, P], BF16, name="bt", tag="mm")
-        nc.tensor.transpose(bt[:], brow[:], ident_b[:])
-        bias = const.tile([P, 16], F32, name="bias")
-        nc.vector.tensor_copy(out=bias[:], in_=bt[:, 0:16])
 
         g1 = const.tile([P, H, NS], F32, name="g1")
         nc.vector.tensor_scalar(out=g1[:], in0=gn[:], scalar1=T1, scalar2=None, op0=ALU.mult)
@@ -127,13 +122,9 @@ def tile_causalwaveletfieldattentionbyte_pa_kernel(tc, x, k_w, k_b, v_w, v_b, sc
         def build_band(h):
             return None
 
-        counter = [0]
-
-        def to_k_major(raw, grouped_words):
-            i = counter[0]
-            counter[0] = i + 1
+        def to_k_major(raw, grouped_words, tag):
             words = raw[:].bitcast(F32)
-            tp = ps.tile([P, 2, 2, P], F32, name="tp", tag=("tr", "pt", "pb")[i % 3])
+            tp = ps.tile([P, 2, 2, P], F32, name="tp", tag=tag, bufs=BANKS[tag])
             for g in range(2):
                 for u in range(2):
                     nc.tensor.transpose(tp[:, g, u, :], words[:, 256 * g + u : 256 * (g + 1) : 2], ident_f[:])
@@ -148,10 +139,10 @@ def tile_causalwaveletfieldattentionbyte_pa_kernel(tc, x, k_w, k_b, v_w, v_b, sc
 
         wc = {}
 
-        def prep_w(ct):
-            for name in ("k", "v"):
+        def prep_w(ct, names):
+            for name in names:
                 grouped = grp.tile([P, 2, P, 4], BF16, name="gw", align_bytes=64)
-                to_k_major(raw_w[(name, ct)], grouped[:].bitcast(F32))
+                to_k_major(raw_w[(name, ct)], grouped[:].bitcast(F32), "ft" if name == "k" else "pt")
                 codes = keep.tile([P, 2, P], U32, name="%sc%d" % (name, ct), align_bytes=64)
                 scl = keep.tile([P, 2, P], U8, name="%ss%d" % (name, ct), align_bytes=64)
                 quantise(grouped, codes, scl)
@@ -162,65 +153,74 @@ def tile_causalwaveletfieldattentionbyte_pa_kernel(tc, x, k_w, k_b, v_w, v_b, sc
         def prep_x(ch):
             grouped = grp.tile([P, 2, 512, 4], BF16, name="gx", align_bytes=64)
             for r in range(R):
-                to_k_major(raw_x[(ch, r)], grouped[:, :, r * P : (r + 1) * P, :].bitcast(F32))
+                to_k_major(raw_x[(ch, r)], grouped[:, :, r * P : (r + 1) * P, :].bitcast(F32), ("pb", "ft", "pb", "pt")[r])
             codes = keep.tile([P, 2, 512], U32, name="xc%d" % ch, align_bytes=64)
             scl = keep.tile([P, 2, 512], U8, name="xs%d" % ch, align_bytes=64)
             quantise(grouped, codes, scl)
             xc[ch] = (codes, scl)
 
         def project(name, ct, ch):
-            acc = ps.tile([P, 512], F32, name="mm", tag="mm")
+            acc = ps.tile([P, R, P], F32, name="mm", tag="mm", bufs=BANKS["mm"])
             w_codes, w_scales = wc[(name, ct)]
             x_codes, x_scales = xc[ch]
-            for g in range(2):
-                nc.tensor.matmul_mx(
-                    out=acc[:],
-                    lhsT=w_codes[:, g, :].bitcast(FP8X4),
-                    lhsT_scale=w_scales[:, g, :],
-                    rhs=x_codes[:, g, :].bitcast(FP8X4),
-                    rhs_scale=x_scales[:, g, :],
-                    start=(g == 0),
-                    stop=(g == 1),
-                )
+            for r in range(R):
+                cols = slice(r * P, (r + 1) * P)
+                for g in range(2):
+                    nc.tensor.matmul_mx(
+                        out=acc[:, r, :],
+                        lhsT=x_codes[:, g, cols].bitcast(FP8X4),
+                        lhsT_scale=x_scales[:, g, cols],
+                        rhs=w_codes[:, g, :].bitcast(FP8X4),
+                        rhs_scale=w_scales[:, g, :],
+                        start=(g == 0),
+                        stop=(g == 1),
+                    )
             return acc
 
         msq = {}
         mag = {}
         field = {}
 
-        def k_mx(ct, ch):
-            kps = project("k", ct, ch)
-            ksq = work.tile([P, 512], F32, name="ksq")
-            nc.scalar.activation(out=ksq[:], in_=kps[:], func=ACT.Square, bias=bias[:, ct : ct + 1], scale=1.0)
-            return ksq
+        def with_bias(acc, bb, ct, name):
+            t = work.tile([P, R, P], F32, name=name)
+            nc.vector.tensor_tensor(
+                out=t[:], in0=acc[:], in1=bb[:, ct * P : (ct + 1) * P].unsqueeze(1).to_broadcast([P, R, P]), op=ALU.add,
+            )
+            return t
 
-        def k_tr(ct, ch, ksq):
+        def squares(ct, ch, tk):
             if ct not in msq:
                 msq[ct] = work.tile([P, 4, R, 2], F32, name="msq")
-            kt = ps.tile([P, R, P], F32, name="kt", tag="tr")
             for r in range(R):
-                nc.tensor.transpose(kt[:, r, :], ksq[:, r * P : (r + 1) * P], ident_f[:])
-            nc.vector.tensor_reduce(out=msq[ct][:, ch], in_=kt[:].rearrange("p r (h c) -> p r h c", h=2), axis=AX.X, op=ALU.add)
+                for h2 in range(2):
+                    junk = work.tile([P, HD], F32, name="junk")
+                    nc.scalar.activation(
+                        out=junk[:], in_=tk[:, r, h2 * HD : (h2 + 1) * HD], func=ACT.Square,
+                        accum_out=msq[ct][:, ch, r, h2 : h2 + 1],
+                    )
 
         def norms(ct):
             mag[ct] = work.tile([P, 4, R, 2], F32, name="mag")
             nc.scalar.activation(out=mag[ct][:], in_=msq[ct][:], func=ACT.Sqrt)
+
+        def stage1(ct, chunks):
+            accs1 = [project("k", ct, ch) for ch in chunks]
+            tks = [with_bias(acc, kbb, ct, "tk") for acc in accs1]
+            for ch, tk in zip(chunks, tks):
+                squares(ct, ch, tk)
+
+        def stage2(ct):
             field[ct] = fpool.tile([P, 2, R, B, P], F32, name="field")
+            accs2 = [project("v", ct, ch) for ch in range(4)]
+            tvs = [with_bias(acc, vbb, ct, "tv") for acc in accs2]
+            for ch, tv in enumerate(tvs):
+                v_tr(ct, ch, tv)
 
-        def v_mx(ct, ch):
-            vps = project("v", ct, ch)
-            vsb = work.tile([P, 512], F32, name="vsb")
-            nc.scalar.activation(out=vsb[:], in_=vps[:], func=ACT.Identity, bias=bias[:, 8 + ct : 9 + ct], scale=1.0)
-            return vsb
-
-        def v_tr(ct, ch, vsb):
-            vt = ps.tile([P, R, P], F32, name="vt", tag="tr")
-            for r in range(R):
-                nc.tensor.transpose(vt[:, r, :], vsb[:, r * P : (r + 1) * P], ident_f[:])
+        def v_tr(ct, ch, tv):
             b, a = divmod(ch, 2)
             nc.vector.tensor_tensor(
                 out=field[ct][:, a, :, b, :].rearrange("p r (h c) -> p r h c", h=2),
-                in0=vt[:].rearrange("p r (h c) -> p r h c", h=2),
+                in0=tv[:].rearrange("p r (h c) -> p r h c", h=2),
                 in1=mag[ct][:, ch].unsqueeze(3).to_broadcast([P, R, 2, HD]),
                 op=ALU.mult,
             )
@@ -233,7 +233,7 @@ def tile_causalwaveletfieldattentionbyte_pa_kernel(tc, x, k_w, k_b, v_w, v_b, sc
             t = band[2 * ct + h2]
             cols = slice(h2 * HD, (h2 + 1) * HD)
             for a in range(2):
-                pb = ps.tile([P, R, B, HD], F32, name="pb", tag="pb")
+                pb = ps.tile([P, R, B, HD], F32, name="pb", tag="pb", bufs=BANKS["pb"])
                 nc.tensor.matmul(pb[:], lhsT=t[:, 0:P], rhs=field[ct][:, a, :, :, cols], start=True, stop=(a == 0))
                 if a == 1:
                     nc.tensor.matmul(pb[:], lhsT=t[:, P:W], rhs=field[ct][:, 0, :, :, cols], start=False, stop=True)
@@ -251,8 +251,8 @@ def tile_causalwaveletfieldattentionbyte_pa_kernel(tc, x, k_w, k_b, v_w, v_b, sc
             if a == 0:
                 accs[(ct, b)] = opool.tile([P, N], F32, name="acc")
             acc = accs[(ct, b)]
-            pt = ps.tile([P, R, P], F32, name="pt", tag="pt")
-            ft = ps.tile([P, R, P], F32, name="ft", tag="tr")
+            pt = ps.tile([P, R, P], F32, name="pt", tag="pt", bufs=BANKS["pt"])
+            ft = ps.tile([P, R, P], F32, name="ft", tag="ft", bufs=BANKS["ft"])
             for r in range(R):
                 nc.tensor.transpose(ft[:, r, :], field[ct][:, a, r, b, :], ident_f[:])
             for r in range(R):
@@ -285,62 +285,42 @@ def tile_causalwaveletfieldattentionbyte_pa_kernel(tc, x, k_w, k_b, v_w, v_b, sc
             nc.scalar.activation(out=o8[:], in_=acc[:], func=ACT.Copy, scale=Y_SCALE, saturate=False)
             nc.sync.dma_start(out=out_1[b, rows, :], in_=o8[:].bitcast(U8))
 
-        prep_w(0)
-        fetch_x(1)
-        prep_x(0)
-        fetch_x(2)
-        prep_x(1)
-        s0 = k_mx(0, 0)
-        fetch_x(3)
-        prep_x(2)
-        k_tr(0, 0, s0)
-        s1 = k_mx(0, 1)
-        fetch_w(1)
-        fetch_w(2)
-        prep_x(3)
-        k_tr(0, 1, s1)
-        s2 = k_mx(0, 2)
-        s3 = k_mx(0, 3)
-        build_band(0)
-        build_band(1)
-        prep_w(1)
-        k_tr(0, 2, s2)
-        k_tr(0, 3, s3)
+        prep_w(0, ("k", "v"))
+        for ch in range(4):
+            if ch < 3:
+                fetch_x(ch + 1)
+            prep_x(ch)
+            stage1(0, (ch,))
         norms(0)
-        for pair in ((0, 1), (2, 3)):
-            sl = [v_mx(0, ch) for ch in pair]
-            for ch, vsb in zip(pair, sl):
-                v_tr(0, ch, vsb)
+        for ct in (1, 2, 3):
+            fetch_w(ct)
+        prep_w(1, ("k", "v"))
 
-        for ct in range(CT):
-            n = ct + 1
-            more = n < CT
-            if ct + 3 < CT:
-                fetch_w(ct + 3)
-            sl = [k_mx(n, ch) for ch in (0, 1)] if more else []
-            toeplitz(ct, 0)
-            for ch, ksq in enumerate(sl):
-                k_tr(n, ch, ksq)
-            if more:
-                build_band(2 * n)
-            sl = [k_mx(n, ch) for ch in (2, 3)] if more else []
-            toeplitz(ct, 1)
-            for ch, ksq in enumerate(sl):
-                k_tr(n, 2 + ch, ksq)
-            if more:
-                norms(n)
-                build_band(2 * n + 1)
-            sl = [v_mx(n, ch) for ch in (0, 1)] if more else []
-            finish(ct, 0, 0)
-            finish(ct, 0, 1)
-            for ch, vsb in enumerate(sl):
-                v_tr(n, ch, vsb)
-            near_taps(ct, 0)
-            sl = [v_mx(n, ch) for ch in (2, 3)] if more else []
-            finish(ct, 1, 0)
-            finish(ct, 1, 1)
-            for ch, vsb in enumerate(sl):
-                v_tr(n, 2 + ch, vsb)
-            near_taps(ct, 1)
-            if ct + 2 < CT:
-                prep_w(ct + 2)
+        for i in range(-2, CT + 1):
+            c1, c2, c3, c4 = i + 3, i + 2, i + 1, i
+            if i + 6 < CT:
+                fetch_w(i + 6)
+            if c1 < CT:
+                stage1(c1, (0, 1, 2, 3))
+                norms(c1)
+            if 0 <= c4 - 1:
+                near_taps(c4 - 1, 1)
+            if 0 <= c3 < CT:
+                toeplitz(c3, 0)
+            if 0 <= c4 < CT:
+                finish(c4, 0, 0)
+            if 0 <= c2 < CT:
+                stage2(c2)
+            if 0 <= c4 < CT:
+                finish(c4, 0, 1)
+                near_taps(c4, 0)
+            if 0 <= c3 < CT:
+                toeplitz(c3, 1)
+            if 0 <= c4 < CT:
+                finish(c4, 1, 0)
+            if i + 4 < CT:
+                prep_w(i + 4, ("k",))
+            if 0 <= c4 < CT:
+                finish(c4, 1, 1)
+            if i + 4 < CT:
+                prep_w(i + 4, ("v",))

@@ -14,313 +14,292 @@ ACT = mybir.ActivationFunctionType
 AX = mybir.AxisListType
 
 B, N, D, C, H, NS = 2, 1024, 1024, 1024, 16, 10
-P = 128
-HD = 64
-CT = C // P
 T0, T1, T2, T3 = 0.4829629131445341, 0.8365163037378079, 0.2241438680420134, -0.1294095225512604
-TAPS = ((1, T2), (2, T1), (3, T0))
 Y_SCALE = 60.0
 FLOPS = 2 * 2 * B * N * D * C
+
+P = 128
+HD = C // H
+CT = C // P
+PASSES = D // (4 * P)
 R = 4
-W = 2 * P
-PAD = 8
-BANKS = {"mm": 4, "pb": 2, "ft": 1, "pt": 1}
+CHUNK = R * P
+CHUNKS = B * N // CHUNK
+HALO = 6
+EXT = HALO + R
+NEAR = (1, 2, 3, 6)
+BANKS = {"mx": 4, "toeplitz": 2, "turn": 2}
+FILL = 2
+W_TILES_A_FILL = 3
+SPREAD = 112
 
 
 def tile_causalwaveletfieldattentionbyte_pa_kernel(tc, x, k_w, k_b, v_w, v_b, scale_gain, out_0, out_1):
     nc = tc.nc
-    xf = x.flatten_outer_dims()
+    x_rows = x.flatten_outer_dims()
+    weights = {"k": k_w, "v": v_w}
 
     with ExitStack() as ctx:
         const = ctx.enter_context(tc.tile_pool(name="const", bufs=1))
         keep = ctx.enter_context(tc.tile_pool(name="keep", bufs=1))
-        rawx = ctx.enter_context(tc.tile_pool(name="rawx", bufs=8))
-        raww = ctx.enter_context(tc.tile_pool(name="raww", bufs=8))
-        grp = ctx.enter_context(tc.tile_pool(name="grp", bufs=2))
-        work = ctx.enter_context(tc.tile_pool(name="work", bufs=4))
-        fpool = ctx.enter_context(tc.tile_pool(name="fpool", bufs=4))
-        bpool = ctx.enter_context(tc.tile_pool(name="bpool", bufs=3))
-        opool = ctx.enter_context(tc.tile_pool(name="opool", bufs=3))
-        ps = ctx.enter_context(tc.psum_pool(name="ps", bufs=1))
+        raw_w_pool = ctx.enter_context(tc.tile_pool(name="raw_w_pool", bufs=2 * CT))
+        grouped_w_pool = ctx.enter_context(tc.tile_pool(name="grouped_w_pool", bufs=2))
+        work = ctx.enter_context(tc.tile_pool(name="work", bufs=CHUNKS))
+        out_pool = ctx.enter_context(tc.tile_pool(name="out_pool", bufs=4))
+        psum = ctx.enter_context(tc.psum_pool(name="psum", bufs=1))
 
-        ident_f = const.tile([P, P], F32, name="ident_f")
-        masks.make_identity(nc, ident_f[:])
+        def bank(shape, role):
+            return psum.tile(shape, F32, name=role, tag=role, bufs=BANKS[role])
 
-        sg = const.tile([P, NS * H], BF16, name="sg")
-        nc.sync.dma_start(out=sg[:], in_=scale_gain.rearrange("j h -> (j h)").partition_broadcast(P))
+        identity = const.tile([P, P], F32, name="identity")
+        masks.make_identity(nc, identity[:])
 
-        kbb = const.tile([P, C], BF16, name="kbb")
-        vbb = const.tile([P, C], BF16, name="vbb")
+        logits = const.tile([P, NS * H], BF16, name="logits")
+        nc.sync.dma_start(out=logits[:], in_=scale_gain.rearrange("j h -> (j h)").partition_broadcast(P))
+        bias = {"k": const.tile([P, C], BF16, name="k_bias"), "v": const.tile([P, C], BF16, name="v_bias")}
 
         raw_w = {}
 
-        def fetch_w(ct):
-            for name, w in (("k", k_w), ("v", v_w)):
-                raw = raww.tile([P, D], BF16, name="raw_w")
-                nc.sync.dma_start(out=raw[:], in_=w[ct * P : (ct + 1) * P, :])
+        def fetch_weights(ct):
+            for name in ("k", "v"):
+                raw = raw_w_pool.tile([P, D], BF16, name="raw_w")
+                nc.sync.dma_start(out=raw[:], in_=weights[name][ct * P : (ct + 1) * P, :])
                 raw_w[(name, ct)] = raw
 
-        raw_x = {}
-
-        def fetch_x(ch):
-            for r in range(R):
-                raw = rawx.tile([P, D], BF16, name="raw_x")
-                nc.sync.dma_start(out=raw[:], in_=xf[512 * ch + r : 512 * (ch + 1) : R, :])
-                raw_x[(ch, r)] = raw
-
-        fetch_w(0)
-        fetch_x(0)
-        nc.sync.dma_start(out=kbb[:], in_=k_b.partition_broadcast(P))
-        nc.sync.dma_start(out=vbb[:], in_=v_b.partition_broadcast(P))
-
-        lg = const.tile([P, H, NS], F32, name="lg")
-        nc.vector.tensor_copy(out=lg[:], in_=sg[:].rearrange("p (j h) -> p h j", j=NS))
-        mx = const.tile([P, H], F32, name="mx")
-        nc.vector.tensor_reduce(out=mx[:], in_=lg[:], axis=AX.X, op=ALU.max)
-        nc.vector.tensor_tensor(out=lg[:], in0=lg[:], in1=mx[:].unsqueeze(2).to_broadcast([P, H, NS]), op=ALU.subtract)
-        ex = const.tile([P, H, NS], F32, name="ex")
-        nc.scalar.activation(out=ex[:], in_=lg[:], func=ACT.Exp)
-        sm = const.tile([P, H], F32, name="sm")
-        nc.vector.tensor_reduce(out=sm[:], in_=ex[:], axis=AX.X, op=ALU.add)
-        rs = const.tile([P, H], F32, name="rs")
-        nc.vector.reciprocal(out=rs[:], in_=sm[:])
-        gn = const.tile([P, H, NS], F32, name="gn")
-        nc.vector.tensor_tensor(out=gn[:], in0=ex[:], in1=rs[:].unsqueeze(2).to_broadcast([P, H, NS]), op=ALU.mult)
-        gp = const.tile([P, CT, NS], F32, name="gp")
-        gnv = gn[:].rearrange("p (c t) j -> p t c j", t=2)
-        nc.vector.tensor_copy(out=gp[0:HD], in_=gnv[0:HD, 0])
-        nc.vector.tensor_copy(out=gp[HD:P], in_=gnv[HD:P, 1])
-        cp = const.tile([P, CT, 4], F32, name="cp")
-        nc.vector.tensor_scalar(out=cp[:, :, 0:1], in0=gp[:, :, 0:1], scalar1=T2, scalar2=None, op0=ALU.mult)
-        nc.vector.tensor_scalar(out=cp[:, :, 1:2], in0=gp[:, :, 0:1], scalar1=T1, scalar2=None, op0=ALU.mult)
-        nc.vector.scalar_tensor_tensor(out=cp[:, :, 1:2], in0=gp[:, :, 1:2], scalar=T2, in1=cp[:, :, 1:2], op0=ALU.mult, op1=ALU.add)
-        nc.vector.tensor_scalar(out=cp[:, :, 2:4], in0=gp[:, :, 0:2], scalar1=T0, scalar2=None, op0=ALU.mult)
-        near = ((1, 0), (2, 1), (3, 2), (6, 3))
-
-        g1 = const.tile([P, H, NS], F32, name="g1")
-        nc.vector.tensor_scalar(out=g1[:], in0=gn[:], scalar1=T1, scalar2=None, op0=ALU.mult)
-        ca = const.tile([P, H, NS], F32, name="ca")
-        nc.vector.tensor_scalar(out=ca[:], in0=gn[:], scalar1=T2, scalar2=None, op0=ALU.mult)
-        nc.vector.tensor_tensor(out=ca[:, :, 1:NS], in0=ca[:, :, 1:NS], in1=g1[:, :, 0 : NS - 1], op=ALU.add)
-        cb = const.tile([P, H, NS], F32, name="cb")
-        nc.vector.tensor_scalar(out=cb[:], in0=gn[:], scalar1=T0, scalar2=None, op0=ALU.mult)
-        row0 = [(2 ** j // R, ca, j) for j in range(2, NS)] + [(3 * 2 ** j // R, cb, j) for j in range(2, NS - 1)]
-        band = {}
-        for h_lo, h_hi in ((0, 4), (4, H)):
-            t = keep.tile([P, h_hi - h_lo, W], F32, name="toep%d" % h_lo)
-            nc.gpsimd.memset(t[:], 0.0)
-            nc.vector.tensor_scalar(out=t[0:1, :, 0:1], in0=gn[0:1, h_lo:h_hi, 0:1], scalar1=0.0, scalar2=T3, op0=ALU.mult, op1=ALU.add)
-            for s, coef, j in row0:
-                nc.vector.tensor_copy(out=t[0:1, :, s : s + 1], in_=coef[0:1, h_lo:h_hi, j : j + 1])
-            for cnt, mults in ((1, (1, 2, 3)), (4, (1, 2, 3)), (16, (1, 2, 3)), (64, (1,))):
-                for m in mults:
-                    a = m * cnt
-                    nc.gpsimd.dma_start(out=t[a : a + cnt, :, a:W], in_=t[0:cnt, :, 0 : W - a])
-            for h in range(h_lo, h_hi):
-                band[h] = t[:, h - h_lo, :]
-
-        def build_band(h):
-            return None
-
-        def to_k_major(raw, grouped_words, tag):
+        def turn_rows(raw, role):
             words = raw[:].bitcast(F32)
-            tp = ps.tile([P, 2, 2, P], F32, name="tp", tag=tag, bufs=BANKS[tag])
-            for g in range(2):
+            turned = bank([P, PASSES, 2, P], role)
+            for g in range(PASSES):
                 for u in range(2):
-                    nc.tensor.transpose(tp[:, g, u, :], words[:, 256 * g + u : 256 * (g + 1) : 2], ident_f[:])
-            nc.scalar.copy(out=grouped_words, in_=tp[:].rearrange("p g u r -> p g r u"))
+                    nc.tensor.transpose(turned[:, g, u, :], words[:, 2 * P * g + u : 2 * P * (g + 1) : 2], identity[:])
+            return turned[:].rearrange("p g u n -> p g n u")
 
-        def quantise(grouped, codes, scl):
+        def quantise(grouped, name, width):
+            codes = keep.tile([P, PASSES, width], U32, name="%s_codes" % name, align_bytes=64)
+            scales = keep.tile([P, PASSES, width], U8, name="%s_scales" % name, align_bytes=64)
             nc.vector.quantize_mx(
-                out=codes[:].rearrange("p g r -> p (g r)").bitcast(FP8X4),
-                scales=scl[:].rearrange("p g r -> p (g r)"),
-                in_=grouped[:].rearrange("p g r e -> p (g r e)"),
+                out=codes[:].rearrange("p g c -> p (g c)").bitcast(FP8X4),
+                scales=scales[:].rearrange("p g c -> p (g c)"),
+                in_=grouped[:].rearrange("p g c t -> p (g c t)"),
             )
+            return codes, scales
 
-        wc = {}
+        w_mx = {}
 
-        def prep_w(ct, names):
-            for name in names:
-                grouped = grp.tile([P, 2, P, 4], BF16, name="gw", align_bytes=64)
-                to_k_major(raw_w[(name, ct)], grouped[:].bitcast(F32), "ft" if name == "k" else "pt")
-                codes = keep.tile([P, 2, P], U32, name="%sc%d" % (name, ct), align_bytes=64)
-                scl = keep.tile([P, 2, P], U8, name="%ss%d" % (name, ct), align_bytes=64)
-                quantise(grouped, codes, scl)
-                wc[(name, ct)] = (codes, scl)
+        def prepare_weights(ct, copy):
+            for name in ("k", "v"):
+                grouped = grouped_w_pool.tile([P, PASSES, P, 4], BF16, name="grouped_w", align_bytes=64)
+                copy(out=grouped[:].bitcast(F32), in_=turn_rows(raw_w[(name, ct)], "turn"))
+                w_mx[(name, ct)] = quantise(grouped, "%s%d" % (name, ct), P)
 
-        xc = {}
-
-        def prep_x(ch):
-            grouped = grp.tile([P, 2, 512, 4], BF16, name="gx", align_bytes=64)
-            for r in range(R):
-                to_k_major(raw_x[(ch, r)], grouped[:, :, r * P : (r + 1) * P, :].bitcast(F32), ("pb", "ft", "pb", "pt")[r])
-            codes = keep.tile([P, 2, 512], U32, name="xc%d" % ch, align_bytes=64)
-            scl = keep.tile([P, 2, 512], U8, name="xs%d" % ch, align_bytes=64)
-            quantise(grouped, codes, scl)
-            xc[ch] = (codes, scl)
+        x_mx = {}
 
         def project(name, ct, ch):
-            acc = ps.tile([P, R, P], F32, name="mm", tag="mm", bufs=BANKS["mm"])
-            w_codes, w_scales = wc[(name, ct)]
-            x_codes, x_scales = xc[ch]
+            sums = bank([P, R, P], "mx")
+            x_codes, x_scales = x_mx[ch]
+            w_codes, w_scales = w_mx[(name, ct)]
             for r in range(R):
-                cols = slice(r * P, (r + 1) * P)
-                for g in range(2):
+                tokens = slice(r * P, (r + 1) * P)
+                for g in range(PASSES):
                     nc.tensor.matmul_mx(
-                        out=acc[:, r, :],
-                        lhsT=x_codes[:, g, cols].bitcast(FP8X4),
-                        lhsT_scale=x_scales[:, g, cols],
+                        out=sums[:, r, :],
+                        lhsT=x_codes[:, g, tokens].bitcast(FP8X4),
+                        lhsT_scale=x_scales[:, g, tokens],
                         rhs=w_codes[:, g, :].bitcast(FP8X4),
                         rhs_scale=w_scales[:, g, :],
                         start=(g == 0),
-                        stop=(g == 1),
+                        stop=(g == PASSES - 1),
                     )
-            return acc
+            return sums
 
-        msq = {}
-        mag = {}
-        field = {}
-
-        def with_bias(acc, bb, ct, name):
-            t = work.tile([P, R, P], F32, name=name)
+        def add_bias(sums, name, ct):
+            biased = work.tile([P, R, P], F32, name="%s_biased" % name)
             nc.vector.tensor_tensor(
-                out=t[:], in0=acc[:], in1=bb[:, ct * P : (ct + 1) * P].unsqueeze(1).to_broadcast([P, R, P]), op=ALU.add,
+                out=biased[:], in0=sums[:], op=ALU.add,
+                in1=bias[name][:, ct * P : (ct + 1) * P].unsqueeze(1).to_broadcast([P, R, P]),
             )
-            return t
+            return biased
 
-        def squares(ct, ch, tk):
-            if ct not in msq:
-                msq[ct] = work.tile([P, 4, R, 2], F32, name="msq")
+        def projections(name, ct, chunks):
+            all_sums = [project(name, ct, ch) for ch in chunks]
+            return [add_bias(sums, name, ct) for sums in all_sums]
+
+        norm = {}
+
+        def norms(ct, square_sums):
+            norm[ct] = work.tile([P, CHUNKS, R, 2], F32, name="norm")
+            nc.scalar.activation(out=norm[ct][:], in_=square_sums[:], func=ACT.Sqrt)
+
+        def sum_squares(square_sums, ch, k_biased):
             for r in range(R):
-                for h2 in range(2):
-                    junk = work.tile([P, HD], F32, name="junk")
+                for half in range(2):
+                    squares = work.tile([P, HD], F32, name="squares")
                     nc.scalar.activation(
-                        out=junk[:], in_=tk[:, r, h2 * HD : (h2 + 1) * HD], func=ACT.Square,
-                        accum_out=msq[ct][:, ch, r, h2 : h2 + 1],
+                        out=squares[:], in_=k_biased[:, r, half * HD : (half + 1) * HD], func=ACT.Square,
+                        accum_out=square_sums[:, ch, r, half : half + 1],
                     )
 
-        def norms(ct):
-            mag[ct] = work.tile([P, 4, R, 2], F32, name="mag")
-            nc.scalar.activation(out=mag[ct][:], in_=msq[ct][:], func=ACT.Sqrt)
+        def stage_norms(ct):
+            square_sums = work.tile([P, CHUNKS, R, 2], F32, name="square_sums")
+            for ch, k_biased in enumerate(projections("k", ct, range(CHUNKS))):
+                sum_squares(square_sums, ch, k_biased)
+            norms(ct, square_sums)
 
-        def stage1(ct, chunks):
-            accs1 = [project("k", ct, ch) for ch in chunks]
-            tks = [with_bias(acc, kbb, ct, "tk") for acc in accs1]
-            for ch, tk in zip(chunks, tks):
-                squares(ct, ch, tk)
+        fetch_weights(0)
+        with tc.tile_pool(name="raw_x_pool", bufs=2 * R) as raw_x_pool, tc.tile_pool(name="grouped_x_pool", bufs=2) as grouped_x_pool:
+            raw_x = {}
 
-        def stage2(ct):
-            field[ct] = fpool.tile([P, 2, R, B, P], F32, name="field")
-            accs2 = [project("v", ct, ch) for ch in range(4)]
-            tvs = [with_bias(acc, vbb, ct, "tv") for acc in accs2]
-            for ch, tv in enumerate(tvs):
-                v_tr(ct, ch, tv)
+            def fetch_x(ch):
+                for r in range(R):
+                    raw = raw_x_pool.tile([P, D], BF16, name="raw_x")
+                    nc.sync.dma_start(out=raw[:], in_=x_rows[CHUNK * ch + r : CHUNK * (ch + 1) : R, :])
+                    raw_x[(ch, r)] = raw
 
-        def v_tr(ct, ch, tv):
-            b, a = divmod(ch, 2)
+            fetch_x(0)
+            nc.sync.dma_start(out=bias["k"][:], in_=k_b.partition_broadcast(P))
+            nc.sync.dma_start(out=bias["v"][:], in_=v_b.partition_broadcast(P))
+
+            shifted = const.tile([P, H, NS], F32, name="shifted")
+            nc.vector.tensor_copy(out=shifted[:], in_=logits[:].rearrange("p (j h) -> p h j", j=NS))
+            largest = const.tile([P, H], F32, name="largest")
+            nc.vector.tensor_reduce(out=largest[:], in_=shifted[:], axis=AX.X, op=ALU.max)
             nc.vector.tensor_tensor(
-                out=field[ct][:, a, :, b, :].rearrange("p r (h c) -> p r h c", h=2),
-                in0=tv[:].rearrange("p r (h c) -> p r h c", h=2),
-                in1=mag[ct][:, ch].unsqueeze(3).to_broadcast([P, R, 2, HD]),
-                op=ALU.mult,
+                out=shifted[:], in0=shifted[:], in1=largest[:].unsqueeze(2).to_broadcast([P, H, NS]), op=ALU.subtract,
             )
-
-        far = {}
-
-        def toeplitz(ct, h2):
-            if ct not in far:
-                far[ct] = bpool.tile([P, 2, R, B, P], F32, name="far")
-            t = band[2 * ct + h2]
-            cols = slice(h2 * HD, (h2 + 1) * HD)
-            for a in range(2):
-                pb = ps.tile([P, R, B, HD], F32, name="pb", tag="pb", bufs=BANKS["pb"])
-                nc.tensor.matmul(pb[:], lhsT=t[:, 0:P], rhs=field[ct][:, a, :, :, cols], start=True, stop=(a == 0))
-                if a == 1:
-                    nc.tensor.matmul(pb[:], lhsT=t[:, P:W], rhs=field[ct][:, 0, :, :, cols], start=False, stop=True)
-                nc.scalar.copy(out=far[ct][:, a, :, :, cols], in_=pb[:])
-
-        fts = []
-        for i in range(3):
-            t = const.tile([P, PAD + N], F32, name="fts%d" % i)
-            nc.gpsimd.memset(t[:, 0:PAD], 0.0)
-            fts.append(t)
-        accs = {}
-
-        def finish(ct, b, a):
-            ftb = fts[(2 * ct + b) % 3]
-            if a == 0:
-                accs[(ct, b)] = opool.tile([P, N], F32, name="acc")
-            acc = accs[(ct, b)]
-            pt = ps.tile([P, R, P], F32, name="pt", tag="pt", bufs=BANKS["pt"])
-            ft = ps.tile([P, R, P], F32, name="ft", tag="ft", bufs=BANKS["ft"])
-            for r in range(R):
-                nc.tensor.transpose(ft[:, r, :], field[ct][:, a, r, b, :], ident_f[:])
-            for r in range(R):
-                nc.tensor.transpose(pt[:, r, :], far[ct][:, a, r, b, :], ident_f[:])
-            lo = 512 * a
-            nc.scalar.copy(
-                out=ftb[:, PAD + lo : PAD + lo + 512].rearrange("p (q r) -> p q r", r=R),
-                in_=ft[:].rearrange("p r q -> p q r"),
+            exps = const.tile([P, H, NS], F32, name="exps")
+            nc.scalar.activation(out=exps[:], in_=shifted[:], func=ACT.Exp)
+            total = const.tile([P, H], F32, name="total")
+            nc.vector.tensor_reduce(out=total[:], in_=exps[:], axis=AX.X, op=ALU.add)
+            inverse = const.tile([P, H], F32, name="inverse")
+            nc.vector.reciprocal(out=inverse[:], in_=total[:])
+            gain = const.tile([P, H, NS], F32, name="gain")
+            nc.vector.tensor_tensor(
+                out=gain[:], in0=exps[:], in1=inverse[:].unsqueeze(2).to_broadcast([P, H, NS]), op=ALU.mult,
             )
-            s, k = near[0]
-            nc.vector.scalar_tensor_tensor(
-                out=acc[:, lo : lo + 512].rearrange("p (q r) -> p q r", r=R),
-                in0=ftb[:, PAD - s + lo : PAD - s + lo + 512].rearrange("p (q r) -> p q r", r=R),
-                scalar=cp[:, ct, k : k + 1],
-                in1=pt[:].rearrange("p r q -> p q r"),
-                op0=ALU.mult, op1=ALU.add,
-            )
+            t1_gain = const.tile([P, H, NS], F32, name="t1_gain")
+            nc.vector.tensor_scalar(out=t1_gain[:], in0=gain[:], scalar1=T1, scalar2=None, op0=ALU.mult)
+            pow2 = const.tile([P, H, NS], F32, name="pow2")
+            nc.vector.tensor_scalar(out=pow2[:], in0=gain[:], scalar1=T2, scalar2=None, op0=ALU.mult)
+            nc.vector.tensor_tensor(out=pow2[:, :, 1:NS], in0=pow2[:, :, 1:NS], in1=t1_gain[:, :, 0 : NS - 1], op=ALU.add)
+            triple = const.tile([P, H, NS], F32, name="triple")
+            nc.vector.tensor_scalar(out=triple[:], in0=gain[:], scalar1=T0, scalar2=None, op0=ALU.mult)
+            coefficient = {}
+            for j in range(NS):
+                coefficient[2 ** j] = (pow2, j)
+                coefficient[3 * 2 ** j] = (triple, j)
 
-        def near_taps(ct, b):
-            ftb = fts[(2 * ct + b) % 3]
-            acc = accs[(ct, b)]
-            for s, k in near[1:]:
-                nc.vector.scalar_tensor_tensor(
-                    out=acc[:], in0=ftb[:, PAD - s : PAD - s + N], scalar=cp[:, ct, k : k + 1], in1=acc[:],
-                    op0=ALU.mult, op1=ALU.add,
+            toeplitz = {}
+            for first, last in ((0, 4), (4, H)):
+                rows = keep.tile([P, last - first, 2 * P], F32, name="toeplitz%d" % first)
+                nc.gpsimd.memset(rows[:], 0.0)
+                nc.vector.tensor_scalar(
+                    out=rows[0:1, :, 0:1], in0=gain[0:1, first:last, 0:1], scalar1=0.0, scalar2=T3, op0=ALU.mult, op1=ALU.add,
                 )
-            rows = slice(ct * P, (ct + 1) * P)
-            nc.sync.dma_start(out=out_0[b, rows, :], in_=acc[:])
-            o8 = opool.tile([P, N], FP8, name="o8")
-            nc.scalar.activation(out=o8[:], in_=acc[:], func=ACT.Copy, scale=Y_SCALE, saturate=False)
-            nc.sync.dma_start(out=out_1[b, rows, :], in_=o8[:].bitcast(U8))
+                for shift in sorted(coefficient):
+                    if shift % R == 0 and shift < N:
+                        tile_of, j = coefficient[shift]
+                        nc.vector.tensor_copy(
+                            out=rows[0:1, :, shift // R : shift // R + 1], in_=tile_of[0:1, first:last, j : j + 1],
+                        )
+                for count in (1, 4, 16, 64):
+                    for down in range(count, min(4 * count, P), count):
+                        nc.gpsimd.dma_start(out=rows[down : down + count, :, down : 2 * P], in_=rows[0:count, :, 0 : 2 * P - down])
+                for h in range(first, last):
+                    toeplitz[h] = rows[:, h - first, :]
 
-        prep_w(0, ("k", "v"))
-        for ch in range(4):
-            if ch < 3:
-                fetch_x(ch + 1)
-            prep_x(ch)
-            stage1(0, (ch,))
-        norms(0)
-        for ct in (1, 2, 3):
-            fetch_w(ct)
-        prep_w(1, ("k", "v"))
+            prepare_weights(0, nc.scalar.copy)
+            square_sums_0 = work.tile([P, CHUNKS, R, 2], F32, name="square_sums")
+            for ch in range(CHUNKS):
+                if ch + 1 < CHUNKS:
+                    fetch_x(ch + 1)
+                grouped = grouped_x_pool.tile([P, PASSES, CHUNK, 4], BF16, name="grouped_x", align_bytes=64)
+                for r in range(R):
+                    nc.scalar.copy(
+                        out=grouped[:, :, r * P : (r + 1) * P, :].bitcast(F32),
+                        in_=turn_rows(raw_x[(ch, r)], ("toeplitz", "turn")[r % 2]),
+                    )
+                x_mx[ch] = quantise(grouped, "x%d" % ch, CHUNK)
+                sum_squares(square_sums_0, ch, projections("k", 0, (ch,))[0])
+            norms(0, square_sums_0)
+            for ct in range(1, CT):
+                fetch_weights(ct)
+            prepare_weights(1, nc.scalar.copy)
 
-        for i in range(-2, CT + 1):
-            c1, c2, c3, c4 = i + 3, i + 2, i + 1, i
-            if i + 6 < CT:
-                fetch_w(i + 6)
-            if c1 < CT:
-                stage1(c1, (0, 1, 2, 3))
-                norms(c1)
-            if 0 <= c4 - 1:
-                near_taps(c4 - 1, 1)
-            if 0 <= c3 < CT:
-                toeplitz(c3, 0)
-            if 0 <= c4 < CT:
-                finish(c4, 0, 0)
-            if 0 <= c2 < CT:
-                stage2(c2)
-            if 0 <= c4 < CT:
-                finish(c4, 0, 1)
-                near_taps(c4, 0)
-            if 0 <= c3 < CT:
-                toeplitz(c3, 1)
-            if 0 <= c4 < CT:
-                finish(c4, 1, 0)
-            if i + 4 < CT:
-                prep_w(i + 4, ("k",))
-            if 0 <= c4 < CT:
-                finish(c4, 1, 1)
-            if i + 4 < CT:
-                prep_w(i + 4, ("v",))
+        ext_pool = ctx.enter_context(tc.tile_pool(name="ext_pool", bufs=1))
+        filtered_pool = ctx.enter_context(tc.tile_pool(name="filtered_pool", bufs=3))
+
+        exts = []
+        for i in range(3):
+            ext = ext_pool.tile([P, 2, EXT, B, P], F32, name="ext%d" % i)
+            nc.gpsimd.memset(ext[0:1, 0, 2:HALO, :, :], 0.0)
+            nc.gpsimd.memset(ext[0:2, 0, 0:2, :, :], 0.0)
+            exts.append(ext)
+
+        def stage_field(ct):
+            ext = exts[ct % 3]
+            for ch, v_biased in enumerate(projections("v", ct, range(CHUNKS))):
+                batch, a = divmod(ch, 2)
+                for r in range(R):
+                    for half in range(2):
+                        head = slice(half * HD, (half + 1) * HD)
+                        nc.scalar.activation(
+                            out=ext[:, a, HALO + r, batch, head], in_=v_biased[:, r, head], func=ACT.Copy,
+                            scale=norm[ct][:, ch, r, half : half + 1],
+                        )
+            for up, e_to, e_from in ((1, slice(2, HALO), slice(HALO, EXT)), (2, slice(0, 2), slice(EXT - 2, EXT))):
+                for lo, hi in ((0, SPREAD), (SPREAD, P - up)):
+                    nc.gpsimd.dma_start(out=ext[lo + up : hi + up, :, e_to, :, :], in_=ext[lo:hi, :, e_from, :, :])
+            for up, e_to, e_from in ((1, slice(2, HALO), slice(HALO, EXT)), (2, slice(0, 2), slice(EXT - 2, EXT))):
+                nc.gpsimd.dma_start(out=ext[0:up, 1, e_to, :, :], in_=ext[P - up : P, 0, e_from, :, :])
+
+        filtered = {}
+
+        def stage_filter(ct, half):
+            if half == 0:
+                filtered[ct] = filtered_pool.tile([P, 2, R, B, P], F32, name="filtered")
+            ext = exts[ct % 3]
+            h = 2 * ct + half
+            head = slice(half * HD, (half + 1) * HD)
+            for a in range(2):
+                far = bank([P, R, B, HD], "toeplitz")
+                nc.tensor.matmul(far[:], lhsT=toeplitz[h][:, 0:P], rhs=ext[:, a, HALO:EXT, :, head], start=True, stop=(a == 0))
+                if a == 1:
+                    nc.tensor.matmul(far[:], lhsT=toeplitz[h][:, P : 2 * P], rhs=ext[:, 0, HALO:EXT, :, head], start=False, stop=True)
+                target = filtered[ct][:, a, :, :, head]
+                for shift in NEAR:
+                    tile_of, j = coefficient[shift]
+                    nc.vector.scalar_tensor_tensor(
+                        out=target, in0=ext[:, a, HALO - shift : EXT - shift, :, head], scalar=tile_of[:, h, j : j + 1],
+                        in1=(far[:] if shift == NEAR[0] else target), op0=ALU.mult, op1=ALU.add,
+                    )
+
+        def stage_output(ct, a):
+            channels = slice(ct * P, (ct + 1) * P)
+            tokens = slice(CHUNK * a, CHUNK * (a + 1))
+            for batch in range(B):
+                turned = bank([P, R, P], "turn")
+                for r in range(R):
+                    nc.tensor.transpose(turned[:, r, :], filtered[ct][:, a, r, batch, :], identity[:])
+                result = out_pool.tile([P, CHUNK], F32, name="result")
+                nc.scalar.copy(out=result[:].rearrange("p (q r) -> p q r", r=R), in_=turned[:].rearrange("p r q -> p q r"))
+                nc.sync.dma_start(out=out_0[batch, channels, tokens], in_=result[:])
+                as_fp8 = out_pool.tile([P, CHUNK], FP8, name="as_fp8")
+                nc.scalar.activation(out=as_fp8[:], in_=result[:], func=ACT.Copy, scale=Y_SCALE, saturate=False)
+                nc.sync.dma_start(out=out_1[batch, channels, tokens], in_=as_fp8[:].bitcast(U8))
+
+        for i in range(-FILL, CT):
+            if 0 <= i + 2 < CT:
+                stage_field(i + 2)
+            if 0 <= i + 1 < CT:
+                stage_filter(i + 1, 0)
+            if 0 <= i:
+                stage_output(i, 0)
+            if i + 3 < CT:
+                stage_norms(i + 3)
+            if 0 <= i + 1 < CT:
+                stage_filter(i + 1, 1)
+            if 0 <= i:
+                stage_output(i, 1)
+            if i < 0:
+                for ct in range(2 + W_TILES_A_FILL * (i + FILL), 2 + W_TILES_A_FILL * (i + FILL + 1)):
+                    prepare_weights(ct, nc.vector.tensor_copy)

@@ -30,7 +30,8 @@ EXT = HALO + R
 NEAR = (1, 2, 3, 6)
 BANKS = {"mx": 4, "toeplitz": 2, "turn": 2}
 FILL = 2
-W_TILES_A_FILL = 3
+UNITS = CT + 1
+FILL_UNITS = {-2: (2, 3, 4), -1: (5, 6, 7, 8)}
 SPREAD = 112
 
 
@@ -56,12 +57,15 @@ def tile_causalwaveletfieldattentionbyte_pa_kernel(tc, x, k_w, k_b, v_w, v_b, sc
 
         logits = const.tile([P, NS * H], BF16, name="logits")
         nc.sync.dma_start(out=logits[:], in_=scale_gain.rearrange("j h -> (j h)").partition_broadcast(P))
-        bias = {"k": const.tile([P, C], BF16, name="k_bias"), "v": const.tile([P, C], BF16, name="v_bias")}
+        bias = const.tile([P, UNITS, 2, P], BF16, name="bias")
+
+        def parts(s):
+            return [("k", s)] * (s < CT) + [("v", s - 1)] * (s > 0)
 
         raw_w = {}
 
-        def fetch_weights(ct):
-            for name in ("k", "v"):
+        def fetch_weights(s):
+            for name, ct in parts(s):
                 raw = raw_w_pool.tile([P, D], BF16, name="raw_w")
                 nc.sync.dma_start(out=raw[:], in_=weights[name][ct * P : (ct + 1) * P, :])
                 raw_w[(name, ct)] = raw
@@ -86,64 +90,82 @@ def tile_causalwaveletfieldattentionbyte_pa_kernel(tc, x, k_w, k_b, v_w, v_b, sc
 
         w_mx = {}
 
-        def prepare_weights(ct, copy):
-            for name in ("k", "v"):
-                grouped = grouped_w_pool.tile([P, PASSES, P, 4], BF16, name="grouped_w", align_bytes=64)
-                copy(out=grouped[:].bitcast(F32), in_=turn_rows(raw_w[(name, ct)], "turn"))
-                w_mx[(name, ct)] = quantise(grouped, "%s%d" % (name, ct), P)
+        def prepare_weights(s, copy):
+            width = P * len(parts(s))
+            grouped = grouped_w_pool.tile([P, PASSES, width, 4], BF16, name="grouped_w", align_bytes=64)
+            for n, part in enumerate(parts(s)):
+                copy(out=grouped[:, :, n * P : (n + 1) * P, :].bitcast(F32), in_=turn_rows(raw_w[part], "turn"))
+            w_mx[s] = quantise(grouped, "w%d" % s, width)
 
         x_mx = {}
 
-        def project(name, ct, ch):
-            sums = bank([P, R, P], "mx")
+        def project(s, ch):
+            width = P * len(parts(s))
+            a_bank = R * P // width
             x_codes, x_scales = x_mx[ch]
-            w_codes, w_scales = w_mx[(name, ct)]
-            for r in range(R):
-                tokens = slice(r * P, (r + 1) * P)
-                for g in range(PASSES):
-                    nc.tensor.matmul_mx(
-                        out=sums[:, r, :],
-                        lhsT=x_codes[:, g, tokens].bitcast(FP8X4),
-                        lhsT_scale=x_scales[:, g, tokens],
-                        rhs=w_codes[:, g, :].bitcast(FP8X4),
-                        rhs_scale=w_scales[:, g, :],
-                        start=(g == 0),
-                        stop=(g == PASSES - 1),
-                    )
-            return sums
+            w_codes, w_scales = w_mx[s]
+            banks = []
+            for first in range(0, R, a_bank):
+                sums = bank([P, a_bank, width], "mx")
+                for r in range(first, first + a_bank):
+                    tokens = slice(r * P, (r + 1) * P)
+                    for g in range(PASSES):
+                        nc.tensor.matmul_mx(
+                            out=sums[:, r - first, :],
+                            lhsT=x_codes[:, g, tokens].bitcast(FP8X4),
+                            lhsT_scale=x_scales[:, g, tokens],
+                            rhs=w_codes[:, g, :].bitcast(FP8X4),
+                            rhs_scale=w_scales[:, g, :],
+                            start=(g == 0),
+                            stop=(g == PASSES - 1),
+                        )
+                banks.append((ch, first, sums))
+            return banks
 
-        def add_bias(sums, name, ct):
-            biased = work.tile([P, R, P], F32, name="%s_biased" % name)
+        def add_bias(s, sums):
+            width = P * len(parts(s))
+            a_bank = R * P // width
+            lo = 0 if s < CT else 1
+            biased = work.tile([P, a_bank, width], F32, name="biased", bufs=2 * BANKS["mx"])
             nc.vector.tensor_tensor(
                 out=biased[:], in0=sums[:], op=ALU.add,
-                in1=bias[name][:, ct * P : (ct + 1) * P].unsqueeze(1).to_broadcast([P, R, P]),
+                in1=bias[:, s, lo : lo + width // P, :].rearrange("p t c -> p (t c)").unsqueeze(1).to_broadcast([P, a_bank, width]),
             )
             return biased
 
-        def projections(name, ct, chunks):
-            all_sums = [project(name, ct, ch) for ch in chunks]
-            return [add_bias(sums, name, ct) for sums in all_sums]
-
         norm = {}
+        square_sums = {}
 
-        def norms(ct, square_sums):
-            norm[ct] = work.tile([P, CHUNKS, R, 2], F32, name="norm")
-            nc.scalar.activation(out=norm[ct][:], in_=square_sums[:], func=ACT.Sqrt)
+        def stage_project(s, chunks):
+            if s < CT and s not in square_sums:
+                square_sums[s] = work.tile([P, CHUNKS, R, 2], F32, name="square_sums")
+            banks = []
+            for ch in chunks:
+                banks.extend(project(s, ch))
+            all_biased = [(ch, first, add_bias(s, sums)) for ch, first, sums in banks]
+            width = P * len(parts(s))
+            for ch, first, biased in all_biased:
+                batch, a = divmod(ch, 2)
+                for n in range(R * P // width):
+                    r = first + n
+                    for half in range(2):
+                        head = slice(half * HD, (half + 1) * HD)
+                        if s < CT:
+                            squares = work.tile([P, HD], F32, name="squares")
+                            nc.scalar.activation(
+                                out=squares[:], in_=biased[:, n, head], func=ACT.Square,
+                                accum_out=square_sums[s][:, ch, r, half : half + 1],
+                            )
+                        if s > 0:
+                            v_head = slice(width - P + half * HD, width - P + (half + 1) * HD)
+                            nc.scalar.activation(
+                                out=exts[(s - 1) % 3][:, a, HALO + r, batch, head], in_=biased[:, n, v_head], func=ACT.Copy,
+                                scale=norm[s - 1][:, ch, r, half : half + 1],
+                            )
 
-        def sum_squares(square_sums, ch, k_biased):
-            for r in range(R):
-                for half in range(2):
-                    squares = work.tile([P, HD], F32, name="squares")
-                    nc.scalar.activation(
-                        out=squares[:], in_=k_biased[:, r, half * HD : (half + 1) * HD], func=ACT.Square,
-                        accum_out=square_sums[:, ch, r, half : half + 1],
-                    )
-
-        def stage_norms(ct):
-            square_sums = work.tile([P, CHUNKS, R, 2], F32, name="square_sums")
-            for ch, k_biased in enumerate(projections("k", ct, range(CHUNKS))):
-                sum_squares(square_sums, ch, k_biased)
-            norms(ct, square_sums)
+        def norms(s):
+            norm[s] = work.tile([P, CHUNKS, R, 2], F32, name="norm")
+            nc.scalar.activation(out=norm[s][:], in_=square_sums[s][:], func=ACT.Sqrt)
 
         fetch_weights(0)
         with tc.tile_pool(name="raw_x_pool", bufs=2 * R) as raw_x_pool, tc.tile_pool(name="grouped_x_pool", bufs=2) as grouped_x_pool:
@@ -156,8 +178,8 @@ def tile_causalwaveletfieldattentionbyte_pa_kernel(tc, x, k_w, k_b, v_w, v_b, sc
                     raw_x[(ch, r)] = raw
 
             fetch_x(0)
-            nc.sync.dma_start(out=bias["k"][:], in_=k_b.partition_broadcast(P))
-            nc.sync.dma_start(out=bias["v"][:], in_=v_b.partition_broadcast(P))
+            nc.sync.dma_start(out=bias[:, 0:CT, 0, :], in_=k_b.partition_broadcast(P).rearrange("q (s c) -> q s c", c=P))
+            nc.sync.dma_start(out=bias[:, 1:UNITS, 1, :], in_=v_b.partition_broadcast(P).rearrange("q (s c) -> q s c", c=P))
 
             shifted = const.tile([P, H, NS], F32, name="shifted")
             nc.vector.tensor_copy(out=shifted[:], in_=logits[:].rearrange("p (j h) -> p h j", j=NS))
@@ -208,7 +230,6 @@ def tile_causalwaveletfieldattentionbyte_pa_kernel(tc, x, k_w, k_b, v_w, v_b, sc
                     toeplitz[h] = rows[:, h - first, :]
 
             prepare_weights(0, nc.scalar.copy)
-            square_sums_0 = work.tile([P, CHUNKS, R, 2], F32, name="square_sums")
             for ch in range(CHUNKS):
                 if ch + 1 < CHUNKS:
                     fetch_x(ch + 1)
@@ -219,10 +240,10 @@ def tile_causalwaveletfieldattentionbyte_pa_kernel(tc, x, k_w, k_b, v_w, v_b, sc
                         in_=turn_rows(raw_x[(ch, r)], ("toeplitz", "turn")[r % 2]),
                     )
                 x_mx[ch] = quantise(grouped, "x%d" % ch, CHUNK)
-                sum_squares(square_sums_0, ch, projections("k", 0, (ch,))[0])
-            norms(0, square_sums_0)
-            for ct in range(1, CT):
-                fetch_weights(ct)
+                stage_project(0, (ch,))
+            norms(0)
+            for s in range(1, UNITS):
+                fetch_weights(s)
             prepare_weights(1, nc.scalar.copy)
 
         ext_pool = ctx.enter_context(tc.tile_pool(name="ext_pool", bufs=1))
@@ -235,17 +256,8 @@ def tile_causalwaveletfieldattentionbyte_pa_kernel(tc, x, k_w, k_b, v_w, v_b, sc
             nc.gpsimd.memset(ext[0:2, 0, 0:2, :, :], 0.0)
             exts.append(ext)
 
-        def stage_field(ct):
+        def halo(ct):
             ext = exts[ct % 3]
-            for ch, v_biased in enumerate(projections("v", ct, range(CHUNKS))):
-                batch, a = divmod(ch, 2)
-                for r in range(R):
-                    for half in range(2):
-                        head = slice(half * HD, (half + 1) * HD)
-                        nc.scalar.activation(
-                            out=ext[:, a, HALO + r, batch, head], in_=v_biased[:, r, head], func=ACT.Copy,
-                            scale=norm[ct][:, ch, r, half : half + 1],
-                        )
             for up, e_to, e_from in ((1, slice(2, HALO), slice(HALO, EXT)), (2, slice(0, 2), slice(EXT - 2, EXT))):
                 for lo, hi in ((0, SPREAD), (SPREAD, P - up)):
                     nc.gpsimd.dma_start(out=ext[lo + up : hi + up, :, e_to, :, :], in_=ext[lo:hi, :, e_from, :, :])
@@ -254,23 +266,28 @@ def tile_causalwaveletfieldattentionbyte_pa_kernel(tc, x, k_w, k_b, v_w, v_b, sc
 
         filtered = {}
 
-        def stage_filter(ct, half):
-            if half == 0:
+        def stage_filter(ct, a):
+            if a == 0:
                 filtered[ct] = filtered_pool.tile([P, 2, R, B, P], F32, name="filtered")
             ext = exts[ct % 3]
-            h = 2 * ct + half
-            head = slice(half * HD, (half + 1) * HD)
-            for a in range(2):
+            fars = []
+            for half in range(2):
+                h = 2 * ct + half
+                head = slice(half * HD, (half + 1) * HD)
                 far = bank([P, R, B, HD], "toeplitz")
                 nc.tensor.matmul(far[:], lhsT=toeplitz[h][:, 0:P], rhs=ext[:, a, HALO:EXT, :, head], start=True, stop=(a == 0))
                 if a == 1:
                     nc.tensor.matmul(far[:], lhsT=toeplitz[h][:, P : 2 * P], rhs=ext[:, 0, HALO:EXT, :, head], start=False, stop=True)
-                target = filtered[ct][:, a, :, :, head]
-                for shift in NEAR:
-                    tile_of, j = coefficient[shift]
+                fars.append(far)
+            for shift in NEAR:
+                tile_of, j = coefficient[shift]
+                for half in range(2):
+                    h = 2 * ct + half
+                    head = slice(half * HD, (half + 1) * HD)
+                    target = filtered[ct][:, a, :, :, head]
                     nc.vector.scalar_tensor_tensor(
                         out=target, in0=ext[:, a, HALO - shift : EXT - shift, :, head], scalar=tile_of[:, h, j : j + 1],
-                        in1=(far[:] if shift == NEAR[0] else target), op0=ALU.mult, op1=ALU.add,
+                        in1=(fars[half][:] if shift == NEAR[0] else target), op0=ALU.mult, op1=ALU.add,
                     )
 
         def stage_output(ct, a):
@@ -281,25 +298,31 @@ def tile_causalwaveletfieldattentionbyte_pa_kernel(tc, x, k_w, k_b, v_w, v_b, sc
                 for r in range(R):
                     nc.tensor.transpose(turned[:, r, :], filtered[ct][:, a, r, batch, :], identity[:])
                 result = out_pool.tile([P, CHUNK], F32, name="result")
-                nc.scalar.copy(out=result[:].rearrange("p (q r) -> p q r", r=R), in_=turned[:].rearrange("p r q -> p q r"))
-                nc.sync.dma_start(out=out_0[batch, channels, tokens], in_=result[:])
                 as_fp8 = out_pool.tile([P, CHUNK], FP8, name="as_fp8")
-                nc.scalar.activation(out=as_fp8[:], in_=result[:], func=ACT.Copy, scale=Y_SCALE, saturate=False)
+                if (ct, a, batch) == (CT - 1, 1, 1):
+                    nc.vector.tensor_copy(out=result[:].rearrange("p (q r) -> p q r", r=R), in_=turned[:].rearrange("p r q -> p q r"))
+                    nc.vector.tensor_scalar(out=as_fp8[:], in0=result[:], scalar1=Y_SCALE, scalar2=None, op0=ALU.mult, saturate=False)
+                else:
+                    nc.scalar.copy(out=result[:].rearrange("p (q r) -> p q r", r=R), in_=turned[:].rearrange("p r q -> p q r"))
+                    nc.scalar.activation(out=as_fp8[:], in_=result[:], func=ACT.Copy, scale=Y_SCALE, saturate=False)
+                nc.sync.dma_start(out=out_0[batch, channels, tokens], in_=result[:])
                 nc.sync.dma_start(out=out_1[batch, channels, tokens], in_=as_fp8[:].bitcast(U8))
 
         for i in range(-FILL, CT):
-            if 0 <= i + 2 < CT:
-                stage_field(i + 2)
+            s = i + 3
+            if s < UNITS:
+                stage_project(s, (0, 1))
+                stage_project(s, (2, 3))
+                if s < CT:
+                    norms(s)
+                halo(s - 1)
             if 0 <= i + 1 < CT:
                 stage_filter(i + 1, 0)
             if 0 <= i:
                 stage_output(i, 0)
-            if i + 3 < CT:
-                stage_norms(i + 3)
             if 0 <= i + 1 < CT:
                 stage_filter(i + 1, 1)
             if 0 <= i:
                 stage_output(i, 1)
-            if i < 0:
-                for ct in range(2 + W_TILES_A_FILL * (i + FILL), 2 + W_TILES_A_FILL * (i + FILL + 1)):
-                    prepare_weights(ct, nc.vector.tensor_copy)
+            for unit in FILL_UNITS.get(i, ()):
+                prepare_weights(unit, nc.vector.tensor_copy)

@@ -29,9 +29,9 @@ HALO = 6
 EXT = HALO + R
 NEAR = (1, 2, 3, 6)
 BANKS = {"mx": 4, "toeplitz": 2, "turn": 2}
-FILL = 2
+FILL = 3
 UNITS = CT + 1
-FILL_UNITS = {-2: (2, 3, 4), -1: (5, 6, 7, 8)}
+FILL_UNITS = {-3: (2, 3, 4), -2: (5, 6, 7), -1: (8,)}
 SPREAD = 112
 
 
@@ -309,13 +309,6 @@ def tile_causalwaveletfieldattentionbyte_pa_kernel(tc, x, k_w, k_b, v_w, v_b, sc
                 nc.sync.dma_start(out=out_1[batch, channels, tokens], in_=as_fp8[:].bitcast(U8))
 
         for i in range(-FILL, CT):
-            s = i + 3
-            if s < UNITS:
-                stage_project(s, (0, 1))
-                stage_project(s, (2, 3))
-                if s < CT:
-                    norms(s)
-                halo(s - 1)
             if 0 <= i + 1 < CT:
                 stage_filter(i + 1, 0)
             if 0 <= i:
@@ -324,5 +317,12 @@ def tile_causalwaveletfieldattentionbyte_pa_kernel(tc, x, k_w, k_b, v_w, v_b, sc
                 stage_filter(i + 1, 1)
             if 0 <= i:
                 stage_output(i, 1)
+            s = i + 4
+            if s < UNITS:
+                stage_project(s, (0, 1))
+                stage_project(s, (2, 3))
+                if s < CT:
+                    norms(s)
+                halo(s - 1)
             for unit in FILL_UNITS.get(i, ()):
                 prepare_weights(unit, nc.vector.tensor_copy)

@@ -266,19 +266,22 @@ def tile_causalwaveletfieldattentionbyte_pa_kernel(tc, x, k_w, k_b, v_w, v_b, sc
 
         filtered = {}
 
-        def stage_filter(ct, a):
+        fars = {}
+
+        def far_shifts(ct, a, half):
+            ext = exts[ct % 3]
+            h = 2 * ct + half
+            head = slice(half * HD, (half + 1) * HD)
+            far = bank([P, R, B, HD], "toeplitz")
+            nc.tensor.matmul(far[:], lhsT=toeplitz[h][:, 0:P], rhs=ext[:, a, HALO:EXT, :, head], start=True, stop=(a == 0))
+            if a == 1:
+                nc.tensor.matmul(far[:], lhsT=toeplitz[h][:, P : 2 * P], rhs=ext[:, 0, HALO:EXT, :, head], start=False, stop=True)
+            fars[half] = far
+
+        def near_shifts(ct, a):
             if a == 0:
                 filtered[ct] = filtered_pool.tile([P, 2, R, B, P], F32, name="filtered")
             ext = exts[ct % 3]
-            fars = []
-            for half in range(2):
-                h = 2 * ct + half
-                head = slice(half * HD, (half + 1) * HD)
-                far = bank([P, R, B, HD], "toeplitz")
-                nc.tensor.matmul(far[:], lhsT=toeplitz[h][:, 0:P], rhs=ext[:, a, HALO:EXT, :, head], start=True, stop=(a == 0))
-                if a == 1:
-                    nc.tensor.matmul(far[:], lhsT=toeplitz[h][:, P : 2 * P], rhs=ext[:, 0, HALO:EXT, :, head], start=False, stop=True)
-                fars.append(far)
             for shift in NEAR:
                 tile_of, j = coefficient[shift]
                 for half in range(2):
@@ -309,18 +312,20 @@ def tile_causalwaveletfieldattentionbyte_pa_kernel(tc, x, k_w, k_b, v_w, v_b, sc
                 nc.sync.dma_start(out=out_1[batch, channels, tokens], in_=as_fp8[:].bitcast(U8))
 
         for i in range(-FILL, CT):
-            if 0 <= i + 1 < CT:
-                stage_filter(i + 1, 0)
-            if 0 <= i:
-                stage_output(i, 0)
-            if 0 <= i + 1 < CT:
-                stage_filter(i + 1, 1)
-            if 0 <= i:
-                stage_output(i, 1)
+            if i == 1:
+                ctx.enter_context(tc.manual_schedule(engines={mybir.EngineType.PE}))
             s = i + 4
+            for a in range(2):
+                if 0 <= i + 1 < CT:
+                    far_shifts(i + 1, a, 0)
+                if 0 <= i:
+                    stage_output(i, a)
+                if 0 <= i + 1 < CT:
+                    far_shifts(i + 1, a, 1)
+                    near_shifts(i + 1, a)
+                if s < UNITS:
+                    stage_project(s, (2 * a, 2 * a + 1))
             if s < UNITS:
-                stage_project(s, (0, 1))
-                stage_project(s, (2, 3))
                 if s < CT:
                     norms(s)
                 halo(s - 1)

@@ -28,47 +28,49 @@ CHUNKS = B * N // CHUNK
 HALO = 6
 EXT = HALO + R
 NEAR = (1, 2, 3, 6)
-BANKS = {"mx": 4, "toeplitz": 2, "turn": 2}
-FILL = 3
-UNITS = CT + 1
-FILL_UNITS = {-3: (2, 3, 4), -2: (5, 6, 7), -1: (8,)}
-SPREAD = 112
+BANKS = {"v": 2, "toeplitz": 2, "swing": 4}
+STEPS = B * CT
+LEAD = 3
+GROUP = 8
+PARTIAL = (2, 4)
+PAIR = 2
+SPREAD = 126
 
 
 def tile_causalwaveletfieldattentionbyte_pa_kernel(tc, x, k_w, k_b, v_w, v_b, scale_gain, out_0, out_1):
     nc = tc.nc
     x_rows = x.flatten_outer_dims()
-    weights = {"k": k_w, "v": v_w}
-
     with ExitStack() as ctx:
         const = ctx.enter_context(tc.tile_pool(name="const", bufs=1))
         keep = ctx.enter_context(tc.tile_pool(name="keep", bufs=1))
-        raw_w_pool = ctx.enter_context(tc.tile_pool(name="raw_w_pool", bufs=2 * CT))
-        grouped_w_pool = ctx.enter_context(tc.tile_pool(name="grouped_w_pool", bufs=2))
-        work = ctx.enter_context(tc.tile_pool(name="work", bufs=CHUNKS))
+        square_pool = ctx.enter_context(tc.tile_pool(name="square_pool", bufs=1))
+        work = ctx.enter_context(tc.tile_pool(name="work", bufs=4))
         out_pool = ctx.enter_context(tc.tile_pool(name="out_pool", bufs=4))
+        ext_pool = ctx.enter_context(tc.tile_pool(name="ext_pool", bufs=1))
+        filtered_pool = ctx.enter_context(tc.tile_pool(name="filtered_pool", bufs=3))
         psum = ctx.enter_context(tc.psum_pool(name="psum", bufs=1))
 
         def bank(shape, role):
             return psum.tile(shape, F32, name=role, tag=role, bufs=BANKS[role])
+
+        ctx.enter_context(tc.manual_schedule(engines={mybir.EngineType.Pool, mybir.EngineType.PE, mybir.EngineType.DVE, mybir.EngineType.Activation}))
 
         identity = const.tile([P, P], F32, name="identity")
         masks.make_identity(nc, identity[:])
 
         logits = const.tile([P, NS * H], BF16, name="logits")
         nc.sync.dma_start(out=logits[:], in_=scale_gain.rearrange("j h -> (j h)").partition_broadcast(P))
-        bias = const.tile([P, UNITS, 2, P], BF16, name="bias")
+        k_bias = const.tile([P, GROUP], BF16, name="k_bias")
+        nc.sync.dma_start(out=k_bias[:], in_=k_b.rearrange("(p t) -> p t", t=GROUP))
+        v_bias = const.tile([P, C], BF16, name="v_bias")
 
-        def parts(s):
-            return [("k", s)] * (s < CT) + [("v", s - 1)] * (s > 0)
-
+        k_rows = k_w.rearrange("(p t) k -> t p k", t=GROUP)
         raw_w = {}
 
-        def fetch_weights(s):
-            for name, ct in parts(s):
-                raw = raw_w_pool.tile([P, D], BF16, name="raw_w")
-                nc.sync.dma_start(out=raw[:], in_=weights[name][ct * P : (ct + 1) * P, :])
-                raw_w[(name, ct)] = raw
+        def fetch_w(name, ct):
+            raw = raw_w_pool.tile([P, D], BF16, name="raw_w")
+            nc.sync.dma_start(out=raw[:], in_=k_rows[ct] if name == "k" else v_w[ct * P : (ct + 1) * P, :])
+            raw_w[(name, ct)] = raw
 
         def turn_rows(raw, role):
             words = raw[:].bitcast(F32)
@@ -89,98 +91,272 @@ def tile_causalwaveletfieldattentionbyte_pa_kernel(tc, x, k_w, k_b, v_w, v_b, sc
             return codes, scales
 
         w_mx = {}
+        grouped_w = {}
 
-        def prepare_weights(s, copy):
-            width = P * len(parts(s))
-            grouped = grouped_w_pool.tile([P, PASSES, width, 4], BF16, name="grouped_w", align_bytes=64)
-            for n, part in enumerate(parts(s)):
-                copy(out=grouped[:, :, n * P : (n + 1) * P, :].bitcast(F32), in_=turn_rows(raw_w[part], "turn"))
-            w_mx[s] = quantise(grouped, "w%d" % s, width)
+        def turn_w(name, ct, copy):
+            pair, n = divmod(ct, PAIR)
+            if n == 0:
+                grouped_w[(name, pair)] = grouped_w_pool.tile([P, PASSES, PAIR * P, 4], BF16, name="grouped_w", align_bytes=64)
+            copy(out=grouped_w[(name, pair)][:, :, n * P : (n + 1) * P, :].bitcast(F32), in_=turn_rows(raw_w[(name, ct)], "swing"))
+
+        def quantise_w(name, pair):
+            codes, scales = quantise(grouped_w[(name, pair)], "%s%d" % (name, pair), PAIR * P)
+            for n in range(PAIR):
+                w_mx[(name, PAIR * pair + n)] = (codes[:, :, n * P : (n + 1) * P], scales[:, :, n * P : (n + 1) * P])
 
         x_mx = {}
-
-        def project(s, ch):
-            width = P * len(parts(s))
-            a_bank = R * P // width
-            x_codes, x_scales = x_mx[ch]
-            w_codes, w_scales = w_mx[s]
-            banks = []
-            for first in range(0, R, a_bank):
-                sums = bank([P, a_bank, width], "mx")
-                for r in range(first, first + a_bank):
-                    tokens = slice(r * P, (r + 1) * P)
-                    for g in range(PASSES):
-                        nc.tensor.matmul_mx(
-                            out=sums[:, r - first, :],
-                            lhsT=x_codes[:, g, tokens].bitcast(FP8X4),
-                            lhsT_scale=x_scales[:, g, tokens],
-                            rhs=w_codes[:, g, :].bitcast(FP8X4),
-                            rhs_scale=w_scales[:, g, :],
-                            start=(g == 0),
-                            stop=(g == PASSES - 1),
-                        )
-                banks.append((ch, first, sums))
-            return banks
-
-        def add_bias(s, sums):
-            width = P * len(parts(s))
-            a_bank = R * P // width
-            lo = 0 if s < CT else 1
-            biased = work.tile([P, a_bank, width], F32, name="biased", bufs=2 * BANKS["mx"])
-            nc.vector.tensor_tensor(
-                out=biased[:], in0=sums[:], op=ALU.add,
-                in1=bias[:, s, lo : lo + width // P, :].rearrange("p t c -> p (t c)").unsqueeze(1).to_broadcast([P, a_bank, width]),
-            )
-            return biased
-
         norm = {}
+
+        def multiply(out, stationary, moving):
+            for g in range(PASSES):
+                nc.tensor.matmul_mx(
+                    out=out,
+                    lhsT=stationary[0][:, g, :].bitcast(FP8X4),
+                    lhsT_scale=stationary[1][:, g, :],
+                    rhs=moving[0][:, g, :].bitcast(FP8X4),
+                    rhs_scale=moving[1][:, g, :],
+                    start=(g == 0),
+                    stop=(g == PASSES - 1),
+                )
+
+        sums = {}
+        squares = {}
+
+        def square_k(ch, t):
+            k_sums = bank([P, CHUNK], "swing")
+            multiply(k_sums[:], w_mx[("k", t)], x_mx[ch])
+            square = square_pool.tile([P, CHUNK], F32, name="square", bufs=10)
+            nc.scalar.activation(out=square[:], in_=k_sums[:], func=ACT.Square, bias=k_bias[:, t : t + 1])
+            squares[(ch, t)] = square
+
+        def add_squares(ch, t):
+            n = t % PARTIAL[ch % 2]
+            if t == n:
+                sums[(ch, n)] = squares[(ch, t)]
+            else:
+                total = sums[(ch, n)]
+                nc.vector.tensor_tensor(out=total[:], in0=total[:], in1=squares[(ch, t)][:], op=ALU.add)
+
         square_sums = {}
 
-        def stage_project(s, chunks):
-            if s < CT and s not in square_sums:
-                square_sums[s] = work.tile([P, CHUNKS, R, 2], F32, name="square_sums")
-            banks = []
-            for ch in chunks:
-                banks.extend(project(s, ch))
-            all_biased = [(ch, first, add_bias(s, sums)) for ch, first, sums in banks]
-            width = P * len(parts(s))
-            for ch, first, biased in all_biased:
-                batch, a = divmod(ch, 2)
-                for n in range(R * P // width):
-                    r = first + n
-                    for half in range(2):
-                        head = slice(half * HD, (half + 1) * HD)
-                        if s < CT:
-                            squares = work.tile([P, HD], F32, name="squares")
-                            nc.scalar.activation(
-                                out=squares[:], in_=biased[:, n, head], func=ACT.Square,
-                                accum_out=square_sums[s][:, ch, r, half : half + 1],
-                            )
-                        if s > 0:
-                            v_head = slice(width - P + half * HD, width - P + (half + 1) * HD)
-                            nc.scalar.activation(
-                                out=exts[(s - 1) % 3][:, a, HALO + r, batch, head], in_=biased[:, n, v_head], func=ACT.Copy,
-                                scale=norm[s - 1][:, ch, r, half : half + 1],
-                            )
+        def turn_sums(ch):
+            turned = bank([P, R, P], "swing")
+            for r in range(R):
+                for n in range(PARTIAL[ch % 2]):
+                    nc.tensor.matmul(
+                        turned[:, r, :], lhsT=sums[(ch, n)][:, r * P : (r + 1) * P], rhs=identity[:], is_transpose=True,
+                        start=(n == 0), stop=(n == PARTIAL[ch % 2] - 1),
+                    )
+            square_sums[ch] = turned
 
-        def norms(s):
-            norm[s] = work.tile([P, CHUNKS, R, 2], F32, name="norm")
-            nc.scalar.activation(out=norm[s][:], in_=square_sums[s][:], func=ACT.Sqrt)
+        def root(ch):
+            summed = work.tile([P, R * H], F32, name="summed")
+            nc.vector.tensor_reduce(
+                out=summed[:], in_=square_sums[ch][:].rearrange("q r (h i) -> q (r h) i", i=P // H), axis=AX.X, op=ALU.add,
+            )
+            norm[ch] = keep.tile([P, R, H], F32, name="norm%d" % ch)
+            nc.scalar.activation(out=norm[ch][:].rearrange("q r h -> q (r h)"), in_=summed[:], func=ACT.Sqrt)
 
-        fetch_weights(0)
-        with tc.tile_pool(name="raw_x_pool", bufs=2 * R) as raw_x_pool, tc.tile_pool(name="grouped_x_pool", bufs=2) as grouped_x_pool:
-            raw_x = {}
+        exts = {}
 
-            def fetch_x(ch):
+        def field_tile(g):
+            if g < CT:
+                exts[g] = ext_pool.tile([P, EXT, B, P], F32, name="ext%d" % g)
+                fill = nc.vector if g < 2 else nc.gpsimd
+                fill.memset(exts[g][0:1, 2:HALO, :, :], 0.0)
+                fill.memset(exts[g][0:2, 0:2, :, :], 0.0)
+            else:
+                exts[g] = late_pool.tile([P, EXT, B, P], F32, name="ext_late")
+
+        v_sums = {}
+        biased = {}
+
+        def project_v(g):
+            a, ct = divmod(g, CT)
+            for batch in range(B):
+                ch = 2 * batch + a
+                v_sums[batch] = bank([P, R, P], "v")
                 for r in range(R):
-                    raw = raw_x_pool.tile([P, D], BF16, name="raw_x")
-                    nc.sync.dma_start(out=raw[:], in_=x_rows[CHUNK * ch + r : CHUNK * (ch + 1) : R, :])
-                    raw_x[(ch, r)] = raw
+                    tokens = slice(r * P, (r + 1) * P)
+                    multiply(v_sums[batch][:, r, :], (x_mx[ch][0][:, :, tokens], x_mx[ch][1][:, :, tokens]), w_mx[("v", ct)])
 
-            fetch_x(0)
-            nc.sync.dma_start(out=bias[:, 0:CT, 0, :], in_=k_b.partition_broadcast(P).rearrange("q (s c) -> q s c", c=P))
-            nc.sync.dma_start(out=bias[:, 1:UNITS, 1, :], in_=v_b.partition_broadcast(P).rearrange("q (s c) -> q s c", c=P))
+        def add_bias(g):
+            ct = g % CT
+            for batch in range(B):
+                biased[batch] = work.tile([P, R, P], F32, name="biased")
+                nc.vector.tensor_tensor(
+                    out=biased[batch][:], in0=v_sums[batch][:], op=ALU.add,
+                    in1=v_bias[:, ct * P : (ct + 1) * P].unsqueeze(1).to_broadcast([P, R, P]),
+                )
 
+        def write_field(g, batch):
+            a, ct = divmod(g, CT)
+            for r in range(R):
+                for half in range(2):
+                    head = slice(half * HD, (half + 1) * HD)
+                    h = 2 * ct + half
+                    nc.scalar.activation(
+                        out=exts[g][:, HALO + r, batch, head], in_=biased[batch][:, r, head], func=ACT.Copy,
+                        scale=norm[2 * batch + a][:, r, h : h + 1],
+                    )
+
+        def halo(g):
+            ext = exts[g]
+            for up, e_to, e_from in ((1, slice(2, HALO), slice(HALO, EXT)), (2, slice(0, 2), slice(EXT - 2, EXT))):
+                for lo, hi in ((0, SPREAD), (SPREAD, P - up)):
+                    if lo < hi:
+                        queue = nc.gpsimd if lo == 0 else nc.sync
+                        queue.dma_start(out=ext[lo + up : hi + up, e_to, :, :], in_=ext[lo:hi, e_from, :, :])
+                if g >= CT:
+                    nc.sync.dma_start(out=ext[0:up, e_to, :, :], in_=exts[g - CT][P - up : P, e_from, :, :])
+
+        filtered = {}
+        fars = {}
+
+        def far_shifts(g, half):
+            a, ct = divmod(g, CT)
+            h = 2 * ct + half
+            head = slice(half * HD, (half + 1) * HD)
+            far = bank([P, R, B, HD], "toeplitz")
+            nc.tensor.matmul(far[:], lhsT=toeplitz[h][:, 0:P], rhs=exts[g][:, HALO:EXT, :, head], start=True, stop=(a == 0))
+            if a == 1:
+                nc.tensor.matmul(far[:], lhsT=toeplitz[h][:, P : 2 * P], rhs=exts[ct][:, HALO:EXT, :, head], start=False, stop=True)
+            fars[(g, half)] = far
+
+        def near_shifts(g):
+            filtered[g] = filtered_pool.tile([P, R, B, P], F32, name="filtered")
+            pieces = (slice(0, 1), slice(1, B)) if g == STEPS - 1 else (slice(0, B),)
+            for batches in pieces:
+                for shift in NEAR:
+                    tile_of, j = coefficient[shift]
+                    for half in range(2):
+                        h = 2 * (g % CT) + half
+                        head = slice(half * HD, (half + 1) * HD)
+                        target = filtered[g][:, :, batches, head]
+                        nc.vector.scalar_tensor_tensor(
+                            out=target, in0=exts[g][:, HALO - shift : EXT - shift, batches, head], scalar=tile_of[:, h, j : j + 1],
+                            in1=(fars[(g, half)][:, :, batches, :] if shift == NEAR[0] else target), op0=ALU.mult, op1=ALU.add,
+                        )
+
+        turned_out = {}
+        results = {}
+
+        def turn_out(g, batch):
+            turned_out[batch] = bank([P, R, P], "swing")
+            for r in range(R):
+                nc.tensor.transpose(turned_out[batch][:, r, :], filtered[g][:, r, batch, :], identity[:])
+
+        def copy_out(g, batch):
+            a, ct = divmod(g, CT)
+            results[batch] = out_pool.tile([P, CHUNK], F32, name="result")
+            copy = nc.vector.tensor_copy if (g, batch) == (STEPS - 1, 1) else nc.scalar.copy
+            copy(out=results[batch][:].rearrange("p (q r) -> p q r", r=R), in_=turned_out[batch][:].rearrange("p r q -> p q r"))
+            nc.sync.dma_start(out=out_0[batch, ct * P : (ct + 1) * P, CHUNK * a : CHUNK * (a + 1)], in_=results[batch][:])
+
+        def cast_out(g, batch):
+            a, ct = divmod(g, CT)
+            as_fp8 = out_pool.tile([P, CHUNK], FP8, name="as_fp8")
+            if (g, batch) == (STEPS - 1, 1):
+                nc.vector.tensor_scalar(out=as_fp8[:], in0=results[batch][:], scalar1=Y_SCALE, scalar2=None, op0=ALU.mult, saturate=False)
+            else:
+                nc.scalar.activation(out=as_fp8[:], in_=results[batch][:], func=ACT.Copy, scale=Y_SCALE, saturate=False)
+            nc.sync.dma_start(out=out_1[batch, ct * P : (ct + 1) * P, CHUNK * a : CHUNK * (a + 1)], in_=as_fp8[:].bitcast(U8))
+
+        pending = []
+
+        def step(i):
+            tasks = beside.get(i, ())
+            todo = list(pending)
+            pending.clear()
+            if i + 3 < STEPS:
+                if i + 3 >= CT:
+                    field_tile(i + 3)
+                add_bias(i + 3)
+            last_norm = ("norm", 3) in tasks
+            if 0 <= i:
+                turn_out(i, 0)
+                turn_out(i, 1)
+                copy_out(i, 0)
+                copy_out(i, 1)
+            if i + 3 < STEPS:
+                write_field(i + 3, 0)
+                if not last_norm:
+                    write_field(i + 3, 1)
+                    halo(i + 3)
+                    if 3 < i + 5 < CT:
+                        field_tile(i + 5)
+            if 0 <= i:
+                cast_out(i, 0)
+                cast_out(i, 1)
+            if i + 4 < STEPS:
+                project_v(i + 4)
+            if 0 <= i + 1 < STEPS:
+                near_shifts(i + 1)
+            if 0 <= i + 2 < STEPS:
+                far_shifts(i + 2, 0)
+                far_shifts(i + 2, 1)
+            if last_norm:
+                turn_sums(3)
+                root(3)
+                write_field(i + 3, 1)
+                halo(i + 3)
+            for task in todo:
+                if task[0] == "qw":
+                    quantise_w(task[1], task[2])
+                elif task[0] == "qx":
+                    x_mx[task[1]] = quantise(grouped_x[task[1]], "x%d" % task[1], CHUNK)
+                elif task[0] == "add":
+                    add_squares(task[1], task[2])
+                elif task[0] == "root":
+                    root(task[1])
+            for task in tasks:
+                if task[0] == "k":
+                    for t in task[2]:
+                        square_k(task[1], t)
+                        pending.append(("add", task[1], t))
+            for task in tasks:
+                if task[0] == "w":
+                    turn_w("v", task[1], nc.scalar.copy)
+                    if task[1] % PAIR:
+                        pending.append(("qw", "v", task[1] // PAIR))
+                elif task[0] == "x":
+                    turn_x(task[1], task[2])
+                    if task[2] == R - 1:
+                        pending.append(("qx", task[1]))
+            if ("norm", 1) in tasks:
+                turn_sums(1)
+                pending.append(("root", 1))
+
+        with tc.tile_pool(name="raw_x_pool", bufs=4) as raw_x_pool, tc.tile_pool(name="grouped_x_pool", bufs=2) as grouped_x_pool, tc.tile_pool(name="raw_w_pool", bufs=5) as raw_w_pool, tc.tile_pool(name="grouped_w_pool", bufs=2) as grouped_w_pool:
+            raw_x = {}
+            grouped_x = {}
+
+            def fetch_x(ch, r):
+                raw = raw_x_pool.tile([P, D], BF16, name="raw_x")
+                nc.sync.dma_start(out=raw[:], in_=x_rows[CHUNK * ch + r : CHUNK * (ch + 1) : R, :])
+                raw_x[(ch, r)] = raw
+
+            def turn_x(ch, r):
+                if r == 0:
+                    grouped_x[ch] = grouped_x_pool.tile([P, PASSES, CHUNK, 4], BF16, name="grouped_x", align_bytes=64)
+                nc.scalar.copy(
+                    out=grouped_x[ch][:, :, r * P : (r + 1) * P, :].bitcast(F32),
+                    in_=turn_rows(raw_x[(ch, r)], "toeplitz" if ch % 2 == 0 else "swing"),
+                )
+
+            for n in range(R):
+                fetch_x(0, n)
+                fetch_w("k", n)
+            for t in range(R, GROUP):
+                fetch_w("k", t)
+            for r in range(R):
+                fetch_x(2, r)
+            nc.sync.dma_start(out=v_bias[:], in_=v_b.partition_broadcast(P))
+            for ct in range(PAIR):
+                fetch_w("v", ct)
+
+            for g in range(2):
+                field_tile(g)
             shifted = const.tile([P, H, NS], F32, name="shifted")
             nc.vector.tensor_copy(out=shifted[:], in_=logits[:].rearrange("p (j h) -> p h j", j=NS))
             largest = const.tile([P, H], F32, name="largest")
@@ -211,123 +387,107 @@ def tile_causalwaveletfieldattentionbyte_pa_kernel(tc, x, k_w, k_b, v_w, v_b, sc
                 coefficient[3 * 2 ** j] = (triple, j)
 
             toeplitz = {}
-            for first, last in ((0, 4), (4, H)):
-                rows = keep.tile([P, last - first, 2 * P], F32, name="toeplitz%d" % first)
-                nc.gpsimd.memset(rows[:], 0.0)
-                nc.vector.tensor_scalar(
-                    out=rows[0:1, :, 0:1], in0=gain[0:1, first:last, 0:1], scalar1=0.0, scalar2=T3, op0=ALU.mult, op1=ALU.add,
-                )
-                for shift in sorted(coefficient):
-                    if shift % R == 0 and shift < N:
-                        tile_of, j = coefficient[shift]
-                        nc.vector.tensor_copy(
-                            out=rows[0:1, :, shift // R : shift // R + 1], in_=tile_of[0:1, first:last, j : j + 1],
-                        )
-                for count in (1, 4, 16, 64):
-                    for down in range(count, min(4 * count, P), count):
-                        nc.gpsimd.dma_start(out=rows[down : down + count, :, down : 2 * P], in_=rows[0:count, :, 0 : 2 * P - down])
-                for h in range(first, last):
-                    toeplitz[h] = rows[:, h - first, :]
+            rows = keep.tile([P, H, 2 * P], F32, name="toeplitz_rows")
+            nc.gpsimd.memset(rows[:], 0.0)
+            field_tile(2)
+            nc.vector.tensor_scalar(
+                out=rows[0:1, :, 0:1], in0=gain[0:1, :, 0:1], scalar1=0.0, scalar2=T3, op0=ALU.mult, op1=ALU.add,
+            )
+            for shift in sorted(coefficient):
+                if shift % R == 0 and shift < N:
+                    tile_of, j = coefficient[shift]
+                    nc.vector.tensor_copy(out=rows[0:1, :, shift // R : shift // R + 1], in_=tile_of[0:1, :, j : j + 1])
+            for count in (1, 4, 16, 64):
+                for down in range(count, min(4 * count, P), count):
+                    nc.gpsimd.dma_start(out=rows[down : down + count, :, down : 2 * P], in_=rows[0:count, :, 0 : 2 * P - down])
+            for h in range(H):
+                toeplitz[h] = rows[:, h, :]
 
-            prepare_weights(0, nc.scalar.copy)
-            for ch in range(CHUNKS):
-                if ch + 1 < CHUNKS:
-                    fetch_x(ch + 1)
-                grouped = grouped_x_pool.tile([P, PASSES, CHUNK, 4], BF16, name="grouped_x", align_bytes=64)
-                for r in range(R):
-                    nc.scalar.copy(
-                        out=grouped[:, :, r * P : (r + 1) * P, :].bitcast(F32),
-                        in_=turn_rows(raw_x[(ch, r)], ("toeplitz", "turn")[r % 2]),
-                    )
-                x_mx[ch] = quantise(grouped, "x%d" % ch, CHUNK)
-                stage_project(0, (ch,))
-            norms(0)
-            for s in range(1, UNITS):
-                fetch_weights(s)
-            prepare_weights(1, nc.scalar.copy)
 
-        ext_pool = ctx.enter_context(tc.tile_pool(name="ext_pool", bufs=1))
-        filtered_pool = ctx.enter_context(tc.tile_pool(name="filtered_pool", bufs=3))
+            for r in range(R):
+                turn_x(0, r)
+                turn_w("k", r, nc.scalar.copy)
+            quantise_w("k", 0)
+            x_mx[0] = quantise(grouped_x[0], "x0", CHUNK)
+            turn_w("k", 4, nc.vector.tensor_copy)
+            turn_w("k", 5, nc.vector.tensor_copy)
+            quantise_w("k", 1)
+            quantise_w("k", 2)
+            root_of_one = const.tile([P, 1], F32, name="root_of_one")
+            nc.scalar.activation(out=root_of_one[:], in_=identity[:, 0:1], func=ACT.Sqrt)
+            square_k(0, 0)
+            square_k(0, 1)
+            turn_w("k", 6, nc.vector.tensor_copy)
+            turn_w("k", 7, nc.vector.tensor_copy)
+            quantise_w("k", 3)
+            turn_x(2, 0)
+            turn_x(2, 1)
+            square_k(0, 2)
+            square_k(0, 3)
+            for t in range(4):
+                add_squares(0, t)
+            turn_x(2, 2)
+            turn_x(2, 3)
+            square_k(0, 4)
+            square_k(0, 5)
+            x_mx[2] = quantise(grouped_x[2], "x2", CHUNK)
+            add_squares(0, 4)
+            add_squares(0, 5)
+            square_k(0, 6)
+            square_k(0, 7)
+            for r in range(R):
+                fetch_x(1, r)
+            for ct in range(PAIR, CT):
+                fetch_w("v", ct)
+            for r in range(R):
+                fetch_x(3, r)
+            square_k(2, 0)
+            square_k(2, 1)
+            add_squares(0, 6)
+            add_squares(0, 7)
+            for n in range(PAIR):
+                turn_w("v", n, nc.vector.tensor_copy)
+            turn_sums(0)
+            square_k(2, 2)
+            square_k(2, 3)
+            root(0)
+            quantise_w("v", 0)
+            add_squares(2, 0)
+            add_squares(2, 1)
+            add_squares(2, 2)
+            add_squares(2, 3)
+            square_k(2, 4)
+            square_k(2, 5)
+            add_squares(2, 4)
+            add_squares(2, 5)
+            square_k(2, 6)
+            square_k(2, 7)
+            for n in range(PAIR):
+                turn_w("v", PAIR + n, nc.vector.tensor_copy)
+            project_v(0)
+            add_squares(2, 6)
+            add_squares(2, 7)
+            turn_sums(2)
+            add_bias(0)
+            write_field(0, 0)
+            root(2)
+            write_field(0, 1)
+            halo(0)
+            field_tile(3)
+            quantise_w("v", 1)
+            project_v(1)
 
-        exts = []
-        for i in range(3):
-            ext = ext_pool.tile([P, 2, EXT, B, P], F32, name="ext%d" % i)
-            nc.gpsimd.memset(ext[0:1, 0, 2:HALO, :, :], 0.0)
-            nc.gpsimd.memset(ext[0:2, 0, 0:2, :, :], 0.0)
-            exts.append(ext)
-
-        def halo(ct):
-            ext = exts[ct % 3]
-            for up, e_to, e_from in ((1, slice(2, HALO), slice(HALO, EXT)), (2, slice(0, 2), slice(EXT - 2, EXT))):
-                for lo, hi in ((0, SPREAD), (SPREAD, P - up)):
-                    nc.gpsimd.dma_start(out=ext[lo + up : hi + up, :, e_to, :, :], in_=ext[lo:hi, :, e_from, :, :])
-            for up, e_to, e_from in ((1, slice(2, HALO), slice(HALO, EXT)), (2, slice(0, 2), slice(EXT - 2, EXT))):
-                nc.gpsimd.dma_start(out=ext[0:up, 1, e_to, :, :], in_=ext[P - up : P, 0, e_from, :, :])
-
-        filtered = {}
-
-        fars = {}
-
-        def far_shifts(ct, a, half):
-            ext = exts[ct % 3]
-            h = 2 * ct + half
-            head = slice(half * HD, (half + 1) * HD)
-            far = bank([P, R, B, HD], "toeplitz")
-            nc.tensor.matmul(far[:], lhsT=toeplitz[h][:, 0:P], rhs=ext[:, a, HALO:EXT, :, head], start=True, stop=(a == 0))
-            if a == 1:
-                nc.tensor.matmul(far[:], lhsT=toeplitz[h][:, P : 2 * P], rhs=ext[:, 0, HALO:EXT, :, head], start=False, stop=True)
-            fars[half] = far
-
-        def near_shifts(ct, a):
-            if a == 0:
-                filtered[ct] = filtered_pool.tile([P, 2, R, B, P], F32, name="filtered")
-            ext = exts[ct % 3]
-            for shift in NEAR:
-                tile_of, j = coefficient[shift]
-                for half in range(2):
-                    h = 2 * ct + half
-                    head = slice(half * HD, (half + 1) * HD)
-                    target = filtered[ct][:, a, :, :, head]
-                    nc.vector.scalar_tensor_tensor(
-                        out=target, in0=ext[:, a, HALO - shift : EXT - shift, :, head], scalar=tile_of[:, h, j : j + 1],
-                        in1=(fars[half][:] if shift == NEAR[0] else target), op0=ALU.mult, op1=ALU.add,
-                    )
-
-        def stage_output(ct, a):
-            channels = slice(ct * P, (ct + 1) * P)
-            tokens = slice(CHUNK * a, CHUNK * (a + 1))
-            for batch in range(B):
-                turned = bank([P, R, P], "turn")
-                for r in range(R):
-                    nc.tensor.transpose(turned[:, r, :], filtered[ct][:, a, r, batch, :], identity[:])
-                result = out_pool.tile([P, CHUNK], F32, name="result")
-                as_fp8 = out_pool.tile([P, CHUNK], FP8, name="as_fp8")
-                if (ct, a, batch) == (CT - 1, 1, 1):
-                    nc.vector.tensor_copy(out=result[:].rearrange("p (q r) -> p q r", r=R), in_=turned[:].rearrange("p r q -> p q r"))
-                    nc.vector.tensor_scalar(out=as_fp8[:], in0=result[:], scalar1=Y_SCALE, scalar2=None, op0=ALU.mult, saturate=False)
-                else:
-                    nc.scalar.copy(out=result[:].rearrange("p (q r) -> p q r", r=R), in_=turned[:].rearrange("p r q -> p q r"))
-                    nc.scalar.activation(out=as_fp8[:], in_=result[:], func=ACT.Copy, scale=Y_SCALE, saturate=False)
-                nc.sync.dma_start(out=out_0[batch, channels, tokens], in_=result[:])
-                nc.sync.dma_start(out=out_1[batch, channels, tokens], in_=as_fp8[:].bitcast(U8))
-
-        for i in range(-FILL, CT):
-            if i == 1:
-                ctx.enter_context(tc.manual_schedule(engines={mybir.EngineType.PE}))
-            s = i + 4
-            for a in range(2):
-                if 0 <= i + 1 < CT:
-                    far_shifts(i + 1, a, 0)
-                if 0 <= i:
-                    stage_output(i, a)
-                if 0 <= i + 1 < CT:
-                    far_shifts(i + 1, a, 1)
-                    near_shifts(i + 1, a)
-                if s < UNITS:
-                    stage_project(s, (2 * a, 2 * a + 1))
-            if s < UNITS:
-                if s < CT:
-                    norms(s)
-                halo(s - 1)
-            for unit in FILL_UNITS.get(i, ()):
-                prepare_weights(unit, nc.vector.tensor_copy)
+            beside = {
+                -2: [("w", 4), ("w", 5), ("x", 1, 0), ("x", 1, 1), ("x", 1, 2), ("x", 1, 3)],
+                -1: [("x", 3, 0), ("x", 3, 1), ("w", 6), ("w", 7)],
+                0: [("k", 1, range(0, 4)), ("x", 3, 2), ("x", 3, 3)],
+                1: [("k", 1, range(4, 8))],
+                2: [("k", 3, range(0, 4)), ("norm", 1)],
+                3: [("k", 3, range(4, 8))],
+                5: [("norm", 3)],
+            }
+            for i in range(-2, 2):
+                step(i)
+        late_pool = ctx.enter_context(tc.tile_pool(name="late_pool", bufs=4))
+        for i in range(2, STEPS):
+            step(i)

@@ -268,28 +268,28 @@ def tile_causalwaveletfieldattentionbyte_pa_kernel(tc, x, k_w, k_b, v_w, v_b, sc
             tasks = beside.get(i, ())
             todo = list(pending)
             pending.clear()
-            if i + 3 < STEPS:
-                if i + 3 >= CT:
-                    field_tile(i + 3)
-                add_bias(i + 3)
+            if i + 4 < STEPS:
+                if i + 4 >= CT:
+                    field_tile(i + 4)
+                add_bias(i + 4)
             last_norm = ("norm", 3) in tasks
             if 0 <= i:
                 turn_out(i, 0)
                 turn_out(i, 1)
                 copy_out(i, 0)
                 copy_out(i, 1)
-            if i + 3 < STEPS:
-                write_field(i + 3, 0)
+            if i + 4 < STEPS:
+                write_field(i + 4, 0)
                 if not last_norm:
-                    write_field(i + 3, 1)
-                    halo(i + 3)
-                    if 3 < i + 5 < CT:
-                        field_tile(i + 5)
+                    write_field(i + 4, 1)
+                    halo(i + 4)
+                    if 3 < i + 6 < CT:
+                        field_tile(i + 6)
             if 0 <= i:
                 cast_out(i, 0)
                 cast_out(i, 1)
-            if i + 4 < STEPS:
-                project_v(i + 4)
+            if i + 5 < STEPS:
+                project_v(i + 5)
             if 0 <= i + 1 < STEPS:
                 near_shifts(i + 1)
             if 0 <= i + 2 < STEPS:
@@ -298,8 +298,8 @@ def tile_causalwaveletfieldattentionbyte_pa_kernel(tc, x, k_w, k_b, v_w, v_b, sc
             if last_norm:
                 turn_sums(3)
                 root(3)
-                write_field(i + 3, 1)
-                halo(i + 3)
+                write_field(i + 4, 1)
+                halo(i + 4)
             for task in todo:
                 if task[0] == "qw":
                     quantise_w(task[1], task[2])
@@ -478,16 +478,16 @@ def tile_causalwaveletfieldattentionbyte_pa_kernel(tc, x, k_w, k_b, v_w, v_b, sc
             project_v(1)
 
             beside = {
-                -2: [("w", 4), ("w", 5), ("x", 1, 0), ("x", 1, 1), ("x", 1, 2), ("x", 1, 3)],
-                -1: [("x", 3, 0), ("x", 3, 1), ("w", 6), ("w", 7)],
-                0: [("k", 1, range(0, 4)), ("x", 3, 2), ("x", 3, 3)],
-                1: [("k", 1, range(4, 8))],
-                2: [("k", 3, range(0, 4)), ("norm", 1)],
-                3: [("k", 3, range(4, 8))],
-                5: [("norm", 3)],
+                -3: [("w", 4), ("w", 5), ("x", 1, 0), ("x", 1, 1), ("x", 1, 2), ("x", 1, 3)],
+                -2: [("x", 3, 0), ("x", 3, 1), ("w", 6), ("w", 7)],
+                -1: [("k", 1, range(0, 4)), ("x", 3, 2), ("x", 3, 3)],
+                0: [("k", 1, range(4, 8))],
+                1: [("k", 3, range(0, 4)), ("norm", 1)],
+                2: [("k", 3, range(4, 8))],
+                4: [("norm", 3)],
             }
-            for i in range(-2, 2):
+            for i in range(-3, 1):
                 step(i)
         late_pool = ctx.enter_context(tc.tile_pool(name="late_pool", bufs=4))
-        for i in range(2, STEPS):
+        for i in range(1, STEPS):
             step(i)

@@ -397,11 +397,17 @@ def tile_causalwaveletfieldattentionbyte_pa_kernel(tc, x, k_w, k_b, v_w, v_b, sc
                 if shift % R == 0 and shift < N:
                     tile_of, j = coefficient[shift]
                     nc.vector.tensor_copy(out=rows[0:1, :, shift // R : shift // R + 1], in_=tile_of[0:1, :, j : j + 1])
-            for count in (1, 4, 16, 64):
-                for down in range(count, min(4 * count, P), count):
-                    nc.gpsimd.dma_start(out=rows[down : down + count, :, down : 2 * P], in_=rows[0:count, :, 0 : 2 * P - down])
             for h in range(H):
                 toeplitz[h] = rows[:, h, :]
+
+            def copy_rows(queue, heads, count):
+                for down in range(count, min(4 * count, P), count):
+                    queue.dma_start(out=rows[down : down + count, heads, down : 2 * P], in_=rows[0:count, heads, 0 : 2 * P - down])
+
+            first_heads, other_heads = slice(0, 4), slice(4, H)
+            for count in (1, 4, 16, 64):
+                copy_rows(nc.gpsimd, first_heads, count)
+            copy_rows(nc.sync, other_heads, 1)
 
 
             for r in range(R):
@@ -435,10 +441,15 @@ def tile_causalwaveletfieldattentionbyte_pa_kernel(tc, x, k_w, k_b, v_w, v_b, sc
             add_squares(0, 5)
             square_k(0, 6)
             square_k(0, 7)
+            for ct in range(PAIR, 2 * PAIR):
+                fetch_w("v", ct)
+            copy_rows(nc.sync, other_heads, 4)
             for r in range(R):
                 fetch_x(1, r)
-            for ct in range(PAIR, CT):
+            copy_rows(nc.sync, other_heads, 16)
+            for ct in range(2 * PAIR, CT):
                 fetch_w("v", ct)
+            copy_rows(nc.sync, other_heads, 64)
             for r in range(R):
                 fetch_x(3, r)
             square_k(2, 0)

@@ -32,7 +32,7 @@ BANKS = {"v": 2, "toeplitz": 2, "swing": 4}
 STEPS = B * CT
 LEAD = 3
 GROUP = 8
-PARTIAL = (2, 4)
+PARTIAL = (2, 4, 2, 8)
 PAIR = 2
 SPREAD = 126
 
@@ -128,13 +128,12 @@ def tile_causalwaveletfieldattentionbyte_pa_kernel(tc, x, k_w, k_b, v_w, v_b, sc
             square = square_pool.tile([P, CHUNK], F32, name="square", bufs=10)
             nc.scalar.activation(out=square[:], in_=k_sums[:], func=ACT.Square, bias=k_bias[:, t : t + 1])
             squares[(ch, t)] = square
+            if t < PARTIAL[ch]:
+                sums[(ch, t)] = square
 
         def add_squares(ch, t):
-            n = t % PARTIAL[ch % 2]
-            if t == n:
-                sums[(ch, n)] = squares[(ch, t)]
-            else:
-                total = sums[(ch, n)]
+            if t >= PARTIAL[ch]:
+                total = sums[(ch, t % PARTIAL[ch])]
                 nc.vector.tensor_tensor(out=total[:], in0=total[:], in1=squares[(ch, t)][:], op=ALU.add)
 
         square_sums = {}
@@ -142,10 +141,10 @@ def tile_causalwaveletfieldattentionbyte_pa_kernel(tc, x, k_w, k_b, v_w, v_b, sc
         def turn_sums(ch):
             turned = bank([P, R, P], "swing")
             for r in range(R):
-                for n in range(PARTIAL[ch % 2]):
+                for n in range(PARTIAL[ch]):
                     nc.tensor.matmul(
                         turned[:, r, :], lhsT=sums[(ch, n)][:, r * P : (r + 1) * P], rhs=identity[:], is_transpose=True,
-                        start=(n == 0), stop=(n == PARTIAL[ch % 2] - 1),
+                        start=(n == 0), stop=(n == PARTIAL[ch] - 1),
                     )
             square_sums[ch] = turned
 
@@ -205,10 +204,9 @@ def tile_causalwaveletfieldattentionbyte_pa_kernel(tc, x, k_w, k_b, v_w, v_b, sc
             for up, e_to, e_from in ((1, slice(2, HALO), slice(HALO, EXT)), (2, slice(0, 2), slice(EXT - 2, EXT))):
                 for lo, hi in ((0, SPREAD), (SPREAD, P - up)):
                     if lo < hi:
-                        queue = nc.gpsimd if lo == 0 else nc.sync
-                        queue.dma_start(out=ext[lo + up : hi + up, e_to, :, :], in_=ext[lo:hi, e_from, :, :])
+                        nc.gpsimd.dma_start(out=ext[lo + up : hi + up, e_to, :, :], in_=ext[lo:hi, e_from, :, :])
                 if g >= CT:
-                    nc.sync.dma_start(out=ext[0:up, e_to, :, :], in_=exts[g - CT][P - up : P, e_from, :, :])
+                    nc.gpsimd.dma_start(out=ext[0:up, e_to, :, :], in_=exts[g - CT][P - up : P, e_from, :, :])
 
         filtered = {}
         fars = {}
@@ -269,51 +267,27 @@ def tile_causalwaveletfieldattentionbyte_pa_kernel(tc, x, k_w, k_b, v_w, v_b, sc
             todo = list(pending)
             pending.clear()
             if i + 4 < STEPS:
-                if i + 4 >= CT:
-                    field_tile(i + 4)
-                add_bias(i + 4)
-            last_norm = ("norm", 3) in tasks
+                project_v(i + 4)
+            field = i + 3
+            if 0 < field < STEPS:
+                if field >= CT:
+                    field_tile(field)
+                write_field(field, 0)
+                write_field(field, 1)
+                halo(field)
+                if 3 < field + 2 < CT:
+                    field_tile(field + 2)
+            if 0 <= i + 1 < STEPS:
+                near_shifts(i + 1)
+            if 0 <= i + 2 < STEPS:
+                far_shifts(i + 2, 0)
+                if i < 0:
+                    far_shifts(i + 2, 1)
             if 0 <= i:
                 turn_out(i, 0)
                 turn_out(i, 1)
                 copy_out(i, 0)
                 copy_out(i, 1)
-            if i + 4 < STEPS:
-                write_field(i + 4, 0)
-                if not last_norm:
-                    write_field(i + 4, 1)
-                    halo(i + 4)
-                    if 3 < i + 6 < CT:
-                        field_tile(i + 6)
-            if 0 <= i:
-                cast_out(i, 0)
-                cast_out(i, 1)
-            if i + 5 < STEPS:
-                project_v(i + 5)
-            if 0 <= i + 1 < STEPS:
-                near_shifts(i + 1)
-            if 0 <= i + 2 < STEPS:
-                far_shifts(i + 2, 0)
-                far_shifts(i + 2, 1)
-            if last_norm:
-                turn_sums(3)
-                root(3)
-                write_field(i + 4, 1)
-                halo(i + 4)
-            for task in todo:
-                if task[0] == "qw":
-                    quantise_w(task[1], task[2])
-                elif task[0] == "qx":
-                    x_mx[task[1]] = quantise(grouped_x[task[1]], "x%d" % task[1], CHUNK)
-                elif task[0] == "add":
-                    add_squares(task[1], task[2])
-                elif task[0] == "root":
-                    root(task[1])
-            for task in tasks:
-                if task[0] == "k":
-                    for t in task[2]:
-                        square_k(task[1], t)
-                        pending.append(("add", task[1], t))
             for task in tasks:
                 if task[0] == "w":
                     turn_w("v", task[1], nc.scalar.copy)
@@ -323,9 +297,30 @@ def tile_causalwaveletfieldattentionbyte_pa_kernel(tc, x, k_w, k_b, v_w, v_b, sc
                     turn_x(task[1], task[2])
                     if task[2] == R - 1:
                         pending.append(("qx", task[1]))
-            if ("norm", 1) in tasks:
-                turn_sums(1)
-                pending.append(("root", 1))
+                elif task[0] == "norm":
+                    turn_sums(task[1])
+            if 0 <= i and i + 2 < STEPS:
+                far_shifts(i + 2, 1)
+            if 0 <= i:
+                cast_out(i, 0)
+                cast_out(i, 1)
+            if i + 4 < STEPS:
+                add_bias(i + 4)
+            for task in todo:
+                if task[0] == "qw":
+                    quantise_w(task[1], task[2])
+                elif task[0] == "qx":
+                    x_mx[task[1]] = quantise(grouped_x[task[1]], "x%d" % task[1], CHUNK)
+                elif task[0] == "add":
+                    add_squares(task[1], task[2])
+            for task in tasks:
+                if task[0] == "norm":
+                    root(task[1])
+            for task in tasks:
+                if task[0] == "k":
+                    for t in task[2]:
+                        square_k(task[1], t)
+                        pending.append(("add", task[1], t))
 
         with tc.tile_pool(name="raw_x_pool", bufs=4) as raw_x_pool, tc.tile_pool(name="grouped_x_pool", bufs=2) as grouped_x_pool, tc.tile_pool(name="raw_w_pool", bufs=5) as raw_w_pool, tc.tile_pool(name="grouped_w_pool", bufs=2) as grouped_w_pool:
             raw_x = {}
@@ -486,19 +481,19 @@ def tile_causalwaveletfieldattentionbyte_pa_kernel(tc, x, k_w, k_b, v_w, v_b, sc
             halo(0)
             field_tile(3)
             quantise_w("v", 1)
-            project_v(1)
 
             beside = {
-                -3: [("w", 4), ("w", 5), ("x", 1, 0), ("x", 1, 1), ("x", 1, 2), ("x", 1, 3)],
-                -2: [("x", 3, 0), ("x", 3, 1), ("w", 6), ("w", 7)],
-                -1: [("k", 1, range(0, 4)), ("x", 3, 2), ("x", 3, 3)],
-                0: [("k", 1, range(4, 8))],
-                1: [("k", 3, range(0, 4)), ("norm", 1)],
-                2: [("k", 3, range(4, 8))],
+                -3: [("w", 4), ("w", 5), ("x", 1, 0), ("x", 1, 1)],
+                -2: [("x", 1, 2), ("x", 1, 3)],
+                -1: [("x", 3, 0), ("x", 3, 1), ("w", 6), ("w", 7)],
+                0: [("x", 3, 2), ("x", 3, 3), ("k", 1, range(0, 4))],
+                1: [("k", 1, range(4, 8))],
+                2: [("k", 3, range(0, 4))],
+                3: [("norm", 1), ("k", 3, range(4, 8))],
                 4: [("norm", 3)],
             }
-            for i in range(-3, 1):
+            for i in range(-3, 2):
                 step(i)
         late_pool = ctx.enter_context(tc.tile_pool(name="late_pool", bufs=4))
-        for i in range(1, STEPS):
+        for i in range(2, STEPS):
             step(i)

@@ -43,7 +43,6 @@ def tile_causalwaveletfieldattentionbyte_pa_kernel(tc, x, k_w, k_b, v_w, v_b, sc
     with ExitStack() as ctx:
         const = ctx.enter_context(tc.tile_pool(name="const", bufs=1))
         keep = ctx.enter_context(tc.tile_pool(name="keep", bufs=1))
-        square_pool = ctx.enter_context(tc.tile_pool(name="square_pool", bufs=1))
         work = ctx.enter_context(tc.tile_pool(name="work", bufs=4))
         out_pool = ctx.enter_context(tc.tile_pool(name="out_pool", bufs=4))
         ext_pool = ctx.enter_context(tc.tile_pool(name="ext_pool", bufs=1))
@@ -101,6 +100,7 @@ def tile_causalwaveletfieldattentionbyte_pa_kernel(tc, x, k_w, k_b, v_w, v_b, sc
 
         def quantise_w(name, pair):
             codes, scales = quantise(grouped_w[(name, pair)], "%s%d" % (name, pair), PAIR * P)
+            w_mx[(name + "_pair", pair)] = (codes, scales)
             for n in range(PAIR):
                 w_mx[(name, PAIR * pair + n)] = (codes[:, :, n * P : (n + 1) * P], scales[:, :, n * P : (n + 1) * P])
 
@@ -170,43 +170,58 @@ def tile_causalwaveletfieldattentionbyte_pa_kernel(tc, x, k_w, k_b, v_w, v_b, sc
         v_sums = {}
         biased = {}
 
-        def project_v(g):
-            a, ct = divmod(g, CT)
-            for batch in range(B):
-                ch = 2 * batch + a
-                v_sums[batch] = bank([P, R, P], "v")
-                for r in range(R):
-                    tokens = slice(r * P, (r + 1) * P)
-                    multiply(v_sums[batch][:, r, :], (x_mx[ch][0][:, :, tokens], x_mx[ch][1][:, :, tokens]), w_mx[("v", ct)])
+        def project_v(unit):
+            pair, batch = divmod(unit, B)
+            a, ct = divmod(PAIR * pair, CT)
+            ch = 2 * batch + a
+            for j in range(R // 2):
+                v_sums[j] = bank([P, 2, PAIR * P], "v")
+                for n in range(2):
+                    tokens = slice((2 * j + n) * P, (2 * j + n + 1) * P)
+                    multiply(
+                        v_sums[j][:, n, :], (x_mx[ch][0][:, :, tokens], x_mx[ch][1][:, :, tokens]), w_mx[("v_pair", ct // PAIR)],
+                    )
 
-        def add_bias(g):
-            ct = g % CT
-            for batch in range(B):
-                biased[batch] = work.tile([P, R, P], F32, name="biased")
+        def add_bias(unit):
+            ct = unit // B * PAIR % CT
+            for j in range(R // 2):
+                biased[(unit, j)] = work.tile([P, 2, PAIR * P], F32, name="biased")
                 nc.vector.tensor_tensor(
-                    out=biased[batch][:], in0=v_sums[batch][:], op=ALU.add,
-                    in1=v_bias[:, ct * P : (ct + 1) * P].unsqueeze(1).to_broadcast([P, R, P]),
+                    out=biased[(unit, j)][:], in0=v_sums[j][:], op=ALU.add,
+                    in1=v_bias[:, ct * P : (ct + PAIR) * P].unsqueeze(1).to_broadcast([P, 2, PAIR * P]),
                 )
 
-        def write_field(g, batch):
-            a, ct = divmod(g, CT)
+        def write_field(unit, of_pair=range(PAIR)):
+            pair, batch = divmod(unit, B)
+            a, ct = divmod(PAIR * pair, CT)
+            if batch == 0 and a == 1:
+                field_tile(PAIR * pair)
+                field_tile(PAIR * pair + 1)
             for r in range(R):
-                for half in range(2):
-                    head = slice(half * HD, (half + 1) * HD)
-                    h = 2 * ct + half
+                for c in range(2 * of_pair[0], 2 * of_pair[-1] + 2):
+                    g = PAIR * pair + c // 2
+                    head = slice(c % 2 * HD, (c % 2 + 1) * HD)
+                    h = 2 * ct + c
                     nc.scalar.activation(
-                        out=exts[g][:, HALO + r, batch, head], in_=biased[batch][:, r, head], func=ACT.Copy,
-                        scale=norm[2 * batch + a][:, r, h : h + 1],
+                        out=exts[g][:, HALO + r, batch, head], in_=biased[(unit, r // 2)][:, r % 2, c * HD : (c + 1) * HD],
+                        func=ACT.Copy, scale=norm[2 * batch + a][:, r, h : h + 1],
                     )
+            if batch == 1:
+                for n in of_pair:
+                    g = PAIR * pair + n
+                    halo(g)
+                    if a == 0 and 3 <= g + 2 < CT:
+                        field_tile(g + 2)
 
         def halo(g):
             ext = exts[g]
             for up, e_to, e_from in ((1, slice(2, HALO), slice(HALO, EXT)), (2, slice(0, 2), slice(EXT - 2, EXT))):
                 for lo, hi in ((0, SPREAD), (SPREAD, P - up)):
                     if lo < hi:
-                        nc.gpsimd.dma_start(out=ext[lo + up : hi + up, e_to, :, :], in_=ext[lo:hi, e_from, :, :])
+                        queue = nc.gpsimd if lo == 0 or g < CT else nc.sync
+                        queue.dma_start(out=ext[lo + up : hi + up, e_to, :, :], in_=ext[lo:hi, e_from, :, :])
                 if g >= CT:
-                    nc.gpsimd.dma_start(out=ext[0:up, e_to, :, :], in_=exts[g - CT][P - up : P, e_from, :, :])
+                    nc.sync.dma_start(out=ext[0:up, e_to, :, :], in_=exts[g - CT][P - up : P, e_from, :, :])
 
         filtered = {}
         fars = {}
@@ -262,21 +277,29 @@ def tile_causalwaveletfieldattentionbyte_pa_kernel(tc, x, k_w, k_b, v_w, v_b, sc
 
         pending = []
 
+        def background_turns(tasks):
+            for task in tasks:
+                if task[0] == "w":
+                    turn_w("v", task[1], nc.scalar.copy)
+                    if task[1] % PAIR:
+                        pending.append(("qw", "v", task[1] // PAIR))
+                elif task[0] == "x":
+                    turn_x(task[1], task[2])
+                    if task[2] == R - 1:
+                        pending.append(("qx", task[1]))
+
         def step(i):
             tasks = beside.get(i, ())
             todo = list(pending)
             pending.clear()
-            if i + 4 < STEPS:
-                project_v(i + 4)
-            field = i + 3
-            if 0 < field < STEPS:
-                if field >= CT:
-                    field_tile(field)
-                write_field(field, 0)
-                write_field(field, 1)
-                halo(field)
-                if 3 < field + 2 < CT:
-                    field_tile(field + 2)
+            if i == -3:
+                background_turns(tasks)
+            if i + 5 < STEPS:
+                project_v(i + 5)
+            fields = {STEPS // 2 - 4: (), STEPS // 2 - 3: (STEPS // 2, STEPS // 2 + 1)}.get(i, (i + 4,))
+            for unit in fields:
+                if 2 <= unit < STEPS:
+                    write_field(unit)
             if 0 <= i + 1 < STEPS:
                 near_shifts(i + 1)
             if 0 <= i + 2 < STEPS:
@@ -288,24 +311,18 @@ def tile_causalwaveletfieldattentionbyte_pa_kernel(tc, x, k_w, k_b, v_w, v_b, sc
                 turn_out(i, 1)
                 copy_out(i, 0)
                 copy_out(i, 1)
+            if i > -3:
+                background_turns(tasks)
             for task in tasks:
-                if task[0] == "w":
-                    turn_w("v", task[1], nc.scalar.copy)
-                    if task[1] % PAIR:
-                        pending.append(("qw", "v", task[1] // PAIR))
-                elif task[0] == "x":
-                    turn_x(task[1], task[2])
-                    if task[2] == R - 1:
-                        pending.append(("qx", task[1]))
-                elif task[0] == "norm":
+                if task[0] == "norm":
                     turn_sums(task[1])
             if 0 <= i and i + 2 < STEPS:
                 far_shifts(i + 2, 1)
             if 0 <= i:
                 cast_out(i, 0)
                 cast_out(i, 1)
-            if i + 4 < STEPS:
-                add_bias(i + 4)
+            if i + 5 < STEPS:
+                add_bias(i + 5)
             for task in todo:
                 if task[0] == "qw":
                     quantise_w(task[1], task[2])
@@ -322,7 +339,7 @@ def tile_causalwaveletfieldattentionbyte_pa_kernel(tc, x, k_w, k_b, v_w, v_b, sc
                         square_k(task[1], t)
                         pending.append(("add", task[1], t))
 
-        with tc.tile_pool(name="raw_x_pool", bufs=4) as raw_x_pool, tc.tile_pool(name="grouped_x_pool", bufs=2) as grouped_x_pool, tc.tile_pool(name="raw_w_pool", bufs=5) as raw_w_pool, tc.tile_pool(name="grouped_w_pool", bufs=2) as grouped_w_pool:
+        with tc.tile_pool(name="raw_x_pool", bufs=4) as raw_x_pool, tc.tile_pool(name="grouped_x_pool", bufs=2) as grouped_x_pool, tc.tile_pool(name="raw_w_pool", bufs=5) as raw_w_pool, tc.tile_pool(name="grouped_w_pool", bufs=2) as grouped_w_pool, tc.tile_pool(name="square_pool", bufs=1) as square_pool:
             raw_x = {}
             grouped_x = {}
 
@@ -475,11 +492,13 @@ def tile_causalwaveletfieldattentionbyte_pa_kernel(tc, x, k_w, k_b, v_w, v_b, sc
             add_squares(2, 7)
             turn_sums(2)
             add_bias(0)
-            write_field(0, 0)
+            write_field(0, (0,))
+            project_v(1)
             root(2)
-            write_field(0, 1)
-            halo(0)
-            field_tile(3)
+            add_bias(1)
+            write_field(1, (0,))
+            write_field(0, (1,))
+            write_field(1, (1,))
             quantise_w("v", 1)
 
             beside = {
@@ -492,8 +511,8 @@ def tile_causalwaveletfieldattentionbyte_pa_kernel(tc, x, k_w, k_b, v_w, v_b, sc
                 3: [("norm", 1), ("k", 3, range(4, 8))],
                 4: [("norm", 3)],
             }
-            for i in range(-3, 2):
+            for i in range(-3, 5):
                 step(i)
-        late_pool = ctx.enter_context(tc.tile_pool(name="late_pool", bufs=4))
-        for i in range(2, STEPS):
+        late_pool = ctx.enter_context(tc.tile_pool(name="late_pool", bufs=5))
+        for i in range(5, STEPS):
             step(i)

@@ -28,11 +28,12 @@ CHUNKS = B * N // CHUNK
 HALO = 6
 EXT = HALO + R
 NEAR = (1, 2, 3, 6)
-BANKS = {"v": 2, "toeplitz": 2, "swing": 4}
+BANKS = {"toeplitz": 3, "swing": 5}
 STEPS = B * CT
 LEAD = 3
 GROUP = 8
 PARTIAL = (2, 4, 2, 8)
+DIRECT = (0, 0, 2, 0)
 PAIR = 2
 SPREAD = 126
 
@@ -130,9 +131,11 @@ def tile_causalwaveletfieldattentionbyte_pa_kernel(tc, x, k_w, k_b, v_w, v_b, sc
             squares[(ch, t)] = square
             if t < PARTIAL[ch]:
                 sums[(ch, t)] = square
+            if t >= GROUP - DIRECT[ch]:
+                sums[(ch, PARTIAL[ch] + t - (GROUP - DIRECT[ch]))] = square
 
         def add_squares(ch, t):
-            if t >= PARTIAL[ch]:
+            if PARTIAL[ch] <= t < GROUP - DIRECT[ch]:
                 total = sums[(ch, t % PARTIAL[ch])]
                 nc.vector.tensor_tensor(out=total[:], in0=total[:], in1=squares[(ch, t)][:], op=ALU.add)
 
@@ -141,10 +144,10 @@ def tile_causalwaveletfieldattentionbyte_pa_kernel(tc, x, k_w, k_b, v_w, v_b, sc
         def turn_sums(ch):
             turned = bank([P, R, P], "swing")
             for r in range(R):
-                for n in range(PARTIAL[ch]):
+                for n in range(PARTIAL[ch] + DIRECT[ch]):
                     nc.tensor.matmul(
                         turned[:, r, :], lhsT=sums[(ch, n)][:, r * P : (r + 1) * P], rhs=identity[:], is_transpose=True,
-                        start=(n == 0), stop=(n == PARTIAL[ch] - 1),
+                        start=(n == 0), stop=(n == PARTIAL[ch] + DIRECT[ch] - 1),
                     )
             square_sums[ch] = turned
 
@@ -175,7 +178,7 @@ def tile_causalwaveletfieldattentionbyte_pa_kernel(tc, x, k_w, k_b, v_w, v_b, sc
             a, ct = divmod(PAIR * pair, CT)
             ch = 2 * batch + a
             for j in range(R // 2):
-                v_sums[j] = bank([P, 2, PAIR * P], "v")
+                v_sums[j] = bank([P, 2, PAIR * P], "swing")
                 for n in range(2):
                     tokens = slice((2 * j + n) * P, (2 * j + n + 1) * P)
                     multiply(
@@ -363,7 +366,6 @@ def tile_causalwaveletfieldattentionbyte_pa_kernel(tc, x, k_w, k_b, v_w, v_b, sc
                 fetch_w("k", t)
             for r in range(R):
                 fetch_x(2, r)
-            nc.sync.dma_start(out=v_bias[:], in_=v_b.partition_broadcast(P))
             for ct in range(PAIR):
                 fetch_w("v", ct)
 
@@ -458,6 +460,7 @@ def tile_causalwaveletfieldattentionbyte_pa_kernel(tc, x, k_w, k_b, v_w, v_b, sc
             copy_rows(nc.sync, other_heads, 4)
             for r in range(R):
                 fetch_x(1, r)
+            nc.sync.dma_start(out=v_bias[:], in_=v_b.partition_broadcast(P))
             copy_rows(nc.sync, other_heads, 16)
             for ct in range(2 * PAIR, CT):
                 fetch_w("v", ct)

@@ -28,11 +28,11 @@ CHUNKS = B * N // CHUNK
 HALO = 6
 EXT = HALO + R
 NEAR = (1, 2, 3, 6)
-BANKS = {"toeplitz": 3, "swing": 5}
+BANKS = {"swing": 8}
 STEPS = B * CT
 LEAD = 3
 GROUP = 8
-PARTIAL = (2, 4, 2, 8)
+PARTIAL = (1, 4, 1, 8)
 DIRECT = (0, 0, 2, 0)
 PAIR = 2
 SPREAD = 126
@@ -59,9 +59,7 @@ def tile_causalwaveletfieldattentionbyte_pa_kernel(tc, x, k_w, k_b, v_w, v_b, sc
         masks.make_identity(nc, identity[:])
 
         logits = const.tile([P, NS * H], BF16, name="logits")
-        nc.sync.dma_start(out=logits[:], in_=scale_gain.rearrange("j h -> (j h)").partition_broadcast(P))
         k_bias = const.tile([P, GROUP], BF16, name="k_bias")
-        nc.sync.dma_start(out=k_bias[:], in_=k_b.rearrange("(p t) -> p t", t=GROUP))
         v_bias = const.tile([P, C], BF16, name="v_bias")
 
         k_rows = k_w.rearrange("(p t) k -> t p k", t=GROUP)
@@ -233,7 +231,7 @@ def tile_causalwaveletfieldattentionbyte_pa_kernel(tc, x, k_w, k_b, v_w, v_b, sc
             a, ct = divmod(g, CT)
             h = 2 * ct + half
             head = slice(half * HD, (half + 1) * HD)
-            far = bank([P, R, B, HD], "toeplitz")
+            far = bank([P, R, B, HD], "swing")
             nc.tensor.matmul(far[:], lhsT=toeplitz[h][:, 0:P], rhs=exts[g][:, HALO:EXT, :, head], start=True, stop=(a == 0))
             if a == 1:
                 nc.tensor.matmul(far[:], lhsT=toeplitz[h][:, P : 2 * P], rhs=exts[ct][:, HALO:EXT, :, head], start=False, stop=True)
@@ -351,19 +349,21 @@ def tile_causalwaveletfieldattentionbyte_pa_kernel(tc, x, k_w, k_b, v_w, v_b, sc
                 nc.sync.dma_start(out=raw[:], in_=x_rows[CHUNK * ch + r : CHUNK * (ch + 1) : R, :])
                 raw_x[(ch, r)] = raw
 
-            def turn_x(ch, r):
+            def turn_x(ch, r, copy=nc.scalar.copy):
                 if r == 0:
                     grouped_x[ch] = grouped_x_pool.tile([P, PASSES, CHUNK, 4], BF16, name="grouped_x", align_bytes=64)
-                nc.scalar.copy(
+                copy(
                     out=grouped_x[ch][:, :, r * P : (r + 1) * P, :].bitcast(F32),
-                    in_=turn_rows(raw_x[(ch, r)], "toeplitz" if ch % 2 == 0 else "swing"),
+                    in_=turn_rows(raw_x[(ch, r)], "swing"),
                 )
 
-            for n in range(R):
-                fetch_x(0, n)
-                fetch_w("k", n)
-            for t in range(R, GROUP):
+            fetch_x(0, 0)
+            nc.sync.dma_start(out=logits[:], in_=scale_gain.rearrange("j h -> (j h)").partition_broadcast(P))
+            for r in range(1, R):
+                fetch_x(0, r)
+            for t in range(GROUP):
                 fetch_w("k", t)
+            nc.sync.dma_start(out=k_bias[:], in_=k_b.rearrange("(p t) -> p t", t=GROUP))
             for r in range(R):
                 fetch_x(2, r)
             for ct in range(PAIR):
@@ -426,9 +426,10 @@ def tile_causalwaveletfieldattentionbyte_pa_kernel(tc, x, k_w, k_b, v_w, v_b, sc
 
             for r in range(R):
                 turn_x(0, r)
-                turn_w("k", r, nc.scalar.copy)
-            quantise_w("k", 0)
+            for t in range(R):
+                turn_w("k", t, nc.scalar.copy)
             x_mx[0] = quantise(grouped_x[0], "x0", CHUNK)
+            quantise_w("k", 0)
             turn_w("k", 4, nc.vector.tensor_copy)
             turn_w("k", 5, nc.vector.tensor_copy)
             quantise_w("k", 1)
@@ -447,7 +448,7 @@ def tile_causalwaveletfieldattentionbyte_pa_kernel(tc, x, k_w, k_b, v_w, v_b, sc
             for t in range(4):
                 add_squares(0, t)
             turn_x(2, 2)
-            turn_x(2, 3)
+            turn_x(2, 3, nc.vector.tensor_copy)
             square_k(0, 4)
             square_k(0, 5)
             x_mx[2] = quantise(grouped_x[2], "x2", CHUNK)
@@ -473,10 +474,8 @@ def tile_causalwaveletfieldattentionbyte_pa_kernel(tc, x, k_w, k_b, v_w, v_b, sc
             add_squares(0, 7)
             for n in range(PAIR):
                 turn_w("v", n, nc.vector.tensor_copy)
-            turn_sums(0)
             square_k(2, 2)
             square_k(2, 3)
-            root(0)
             quantise_w("v", 0)
             add_squares(2, 0)
             add_squares(2, 1)
@@ -488,8 +487,10 @@ def tile_causalwaveletfieldattentionbyte_pa_kernel(tc, x, k_w, k_b, v_w, v_b, sc
             add_squares(2, 5)
             square_k(2, 6)
             square_k(2, 7)
+            turn_sums(0)
+            root(0)
             for n in range(PAIR):
-                turn_w("v", PAIR + n, nc.vector.tensor_copy)
+                turn_w("v", PAIR + n, nc.scalar.copy)
             project_v(0)
             add_squares(2, 6)
             add_squares(2, 7)

@@ -32,8 +32,8 @@ BANKS = {"swing": 8}
 STEPS = B * CT
 LEAD = 3
 GROUP = 8
-PARTIAL = (1, 4, 1, 8)
-DIRECT = (0, 0, 2, 0)
+PARTIAL = (2, 4, 2, 8)
+DIRECT = (0, 0, 1, 0)
 PAIR = 2
 SPREAD = 126
 
@@ -124,7 +124,7 @@ def tile_causalwaveletfieldattentionbyte_pa_kernel(tc, x, k_w, k_b, v_w, v_b, sc
         def square_k(ch, t):
             k_sums = bank([P, CHUNK], "swing")
             multiply(k_sums[:], w_mx[("k", t)], x_mx[ch])
-            square = square_pool.tile([P, CHUNK], F32, name="square", bufs=10)
+            square = square_pool.tile([P, CHUNK], F32, name="square", bufs=8)
             nc.scalar.activation(out=square[:], in_=k_sums[:], func=ACT.Square, bias=k_bias[:, t : t + 1])
             squares[(ch, t)] = square
             if t < PARTIAL[ch]:
@@ -162,7 +162,7 @@ def tile_causalwaveletfieldattentionbyte_pa_kernel(tc, x, k_w, k_b, v_w, v_b, sc
         def field_tile(g):
             if g < CT:
                 exts[g] = ext_pool.tile([P, EXT, B, P], F32, name="ext%d" % g)
-                fill = nc.vector if g < 2 else nc.gpsimd
+                fill = nc.vector if g == 0 else nc.gpsimd
                 fill.memset(exts[g][0:1, 2:HALO, :, :], 0.0)
                 fill.memset(exts[g][0:2, 0:2, :, :], 0.0)
             else:
@@ -340,7 +340,7 @@ def tile_causalwaveletfieldattentionbyte_pa_kernel(tc, x, k_w, k_b, v_w, v_b, sc
                         square_k(task[1], t)
                         pending.append(("add", task[1], t))
 
-        with tc.tile_pool(name="raw_x_pool", bufs=4) as raw_x_pool, tc.tile_pool(name="grouped_x_pool", bufs=2) as grouped_x_pool, tc.tile_pool(name="raw_w_pool", bufs=5) as raw_w_pool, tc.tile_pool(name="grouped_w_pool", bufs=2) as grouped_w_pool, tc.tile_pool(name="square_pool", bufs=1) as square_pool:
+        with tc.tile_pool(name="raw_x_pool", bufs=4) as raw_x_pool, tc.tile_pool(name="grouped_x_pool", bufs=2) as grouped_x_pool, tc.tile_pool(name="raw_w_pool", bufs=8) as raw_w_pool, tc.tile_pool(name="grouped_w_pool", bufs=2) as grouped_w_pool, tc.tile_pool(name="square_pool", bufs=1) as square_pool:
             raw_x = {}
             grouped_x = {}
 
@@ -369,8 +369,7 @@ def tile_causalwaveletfieldattentionbyte_pa_kernel(tc, x, k_w, k_b, v_w, v_b, sc
             for ct in range(PAIR):
                 fetch_w("v", ct)
 
-            for g in range(2):
-                field_tile(g)
+            field_tile(0)
             shifted = const.tile([P, H, NS], F32, name="shifted")
             nc.vector.tensor_copy(out=shifted[:], in_=logits[:].rearrange("p (j h) -> p h j", j=NS))
             largest = const.tile([P, H], F32, name="largest")
@@ -421,6 +420,7 @@ def tile_causalwaveletfieldattentionbyte_pa_kernel(tc, x, k_w, k_b, v_w, v_b, sc
             first_heads, other_heads = slice(0, 4), slice(4, H)
             for count in (1, 4, 16, 64):
                 copy_rows(nc.gpsimd, first_heads, count)
+            field_tile(1)
             copy_rows(nc.sync, other_heads, 1)
 
 

@@ -53,7 +53,7 @@ def tile_causalwaveletfieldattentionbyte_pa_kernel(tc, x, k_w, k_b, v_w, v_b, sc
         def bank(shape, role):
             return psum.tile(shape, F32, name=role, tag=role, bufs=BANKS[role])
 
-        ctx.enter_context(tc.manual_schedule(engines={mybir.EngineType.Pool, mybir.EngineType.PE, mybir.EngineType.DVE, mybir.EngineType.Activation}))
+        ctx.enter_context(tc.manual_schedule(engines={mybir.EngineType.Pool, mybir.EngineType.PE, mybir.EngineType.DVE, mybir.EngineType.Activation, mybir.EngineType.SP}))
 
         identity = const.tile([P, P], F32, name="identity")
         masks.make_identity(nc, identity[:])
@@ -124,7 +124,7 @@ def tile_causalwaveletfieldattentionbyte_pa_kernel(tc, x, k_w, k_b, v_w, v_b, sc
         def square_k(ch, t):
             k_sums = bank([P, CHUNK], "swing")
             multiply(k_sums[:], w_mx[("k", t)], x_mx[ch])
-            square = square_pool.tile([P, CHUNK], F32, name="square", bufs=8)
+            square = square_pool.tile([P, CHUNK], F32, name="square", bufs=9)
             nc.scalar.activation(out=square[:], in_=k_sums[:], func=ACT.Square, bias=k_bias[:, t : t + 1])
             squares[(ch, t)] = square
             if t < PARTIAL[ch]:
@@ -340,7 +340,7 @@ def tile_causalwaveletfieldattentionbyte_pa_kernel(tc, x, k_w, k_b, v_w, v_b, sc
                         square_k(task[1], t)
                         pending.append(("add", task[1], t))
 
-        with tc.tile_pool(name="raw_x_pool", bufs=4) as raw_x_pool, tc.tile_pool(name="grouped_x_pool", bufs=2) as grouped_x_pool, tc.tile_pool(name="raw_w_pool", bufs=8) as raw_w_pool, tc.tile_pool(name="grouped_w_pool", bufs=2) as grouped_w_pool, tc.tile_pool(name="square_pool", bufs=1) as square_pool:
+        with tc.tile_pool(name="raw_x_pool", bufs=4) as raw_x_pool, tc.tile_pool(name="grouped_x_pool", bufs=2) as grouped_x_pool, tc.tile_pool(name="raw_w_pool", bufs=7) as raw_w_pool, tc.tile_pool(name="grouped_w_pool", bufs=2) as grouped_w_pool, tc.tile_pool(name="square_pool", bufs=1) as square_pool:
             raw_x = {}
             grouped_x = {}
 
@@ -364,10 +364,8 @@ def tile_causalwaveletfieldattentionbyte_pa_kernel(tc, x, k_w, k_b, v_w, v_b, sc
             for t in range(GROUP):
                 fetch_w("k", t)
             nc.sync.dma_start(out=k_bias[:], in_=k_b.rearrange("(p t) -> p t", t=GROUP))
-            for r in range(R):
+            for r in range(2):
                 fetch_x(2, r)
-            for ct in range(PAIR):
-                fetch_w("v", ct)
 
             field_tile(0)
             shifted = const.tile([P, H, NS], F32, name="shifted")
@@ -402,7 +400,6 @@ def tile_causalwaveletfieldattentionbyte_pa_kernel(tc, x, k_w, k_b, v_w, v_b, sc
             toeplitz = {}
             rows = keep.tile([P, H, 2 * P], F32, name="toeplitz_rows")
             nc.gpsimd.memset(rows[:], 0.0)
-            field_tile(2)
             nc.vector.tensor_scalar(
                 out=rows[0:1, :, 0:1], in0=gain[0:1, :, 0:1], scalar1=0.0, scalar2=T3, op0=ALU.mult, op1=ALU.add,
             )
@@ -417,11 +414,18 @@ def tile_causalwaveletfieldattentionbyte_pa_kernel(tc, x, k_w, k_b, v_w, v_b, sc
                 for down in range(count, min(4 * count, P), count):
                     queue.dma_start(out=rows[down : down + count, heads, down : 2 * P], in_=rows[0:count, heads, 0 : 2 * P - down])
 
-            first_heads, other_heads = slice(0, 4), slice(4, H)
-            for count in (1, 4, 16, 64):
-                copy_rows(nc.gpsimd, first_heads, count)
+            first_heads, other_heads = slice(0, 6), slice(6, H)
+            copy_rows(nc.sync, first_heads, 1)
+            for r in range(2, R):
+                fetch_x(2, r)
+            for ct in range(PAIR):
+                fetch_w("v", ct)
+            copy_rows(nc.sync, first_heads, 4)
+            copy_rows(nc.gpsimd, other_heads, 1)
             field_tile(1)
-            copy_rows(nc.sync, other_heads, 1)
+            copy_rows(nc.gpsimd, other_heads, 4)
+            field_tile(2)
+            copy_rows(nc.gpsimd, other_heads, 16)
 
 
             for r in range(R):
@@ -458,14 +462,13 @@ def tile_causalwaveletfieldattentionbyte_pa_kernel(tc, x, k_w, k_b, v_w, v_b, sc
             square_k(0, 7)
             for ct in range(PAIR, 2 * PAIR):
                 fetch_w("v", ct)
-            copy_rows(nc.sync, other_heads, 4)
+            copy_rows(nc.sync, first_heads, 16)
             for r in range(R):
                 fetch_x(1, r)
             nc.sync.dma_start(out=v_bias[:], in_=v_b.partition_broadcast(P))
-            copy_rows(nc.sync, other_heads, 16)
+            copy_rows(nc.sync, first_heads, 64)
             for ct in range(2 * PAIR, CT):
                 fetch_w("v", ct)
-            copy_rows(nc.sync, other_heads, 64)
             for r in range(R):
                 fetch_x(3, r)
             square_k(2, 0)
@@ -503,6 +506,7 @@ def tile_causalwaveletfieldattentionbyte_pa_kernel(tc, x, k_w, k_b, v_w, v_b, sc
             write_field(1, (0,))
             write_field(0, (1,))
             write_field(1, (1,))
+            copy_rows(nc.gpsimd, other_heads, 64)
             quantise_w("v", 1)
 
             beside = {

from contextlib import ExitStack

import concourse.masks as masks
import concourse.mybir as mybir

F32 = mybir.dt.float32
BF16 = mybir.dt.bfloat16
U32 = mybir.dt.uint32
U8 = mybir.dt.uint8
FP8X4 = mybir.dt.float8_e4m3fn_x4
FP8 = mybir.dt.float8_e4m3fn
ALU = mybir.AluOpType
ACT = mybir.ActivationFunctionType
AX = mybir.AxisListType

B, N, D, C, H, NS = 2, 1024, 1024, 1024, 16, 10
T0, T1, T2, T3 = 0.4829629131445341, 0.8365163037378079, 0.2241438680420134, -0.1294095225512604
Y_SCALE = 60.0
FLOPS = 2 * 2 * B * N * D * C

P = 128
HD = C // H
CT = C // P
PASSES = D // (4 * P)
R = 4
CHUNK = R * P
CHUNKS = B * N // CHUNK
HALO = 6
EXT = HALO + R
NEAR = (1, 2, 3, 6)
BANKS = {"swing": 8}
STEPS = B * CT
LEAD = 3
GROUP = 8
PARTIAL = (2, 4, 2, 8)
DIRECT = (0, 0, 1, 0)
PAIR = 2
SPREAD = 126


def tile_causalwaveletfieldattentionbyte_pa_kernel(tc, x, k_w, k_b, v_w, v_b, scale_gain, out_0, out_1):
    nc = tc.nc
    x_rows = x.flatten_outer_dims()
    with ExitStack() as ctx:
        const = ctx.enter_context(tc.tile_pool(name="const", bufs=1))
        keep = ctx.enter_context(tc.tile_pool(name="keep", bufs=1))
        work = ctx.enter_context(tc.tile_pool(name="work", bufs=4))
        out_pool = ctx.enter_context(tc.tile_pool(name="out_pool", bufs=4))
        ext_pool = ctx.enter_context(tc.tile_pool(name="ext_pool", bufs=1))
        filtered_pool = ctx.enter_context(tc.tile_pool(name="filtered_pool", bufs=3))
        psum = ctx.enter_context(tc.psum_pool(name="psum", bufs=1))

        def bank(shape, role):
            return psum.tile(shape, F32, name=role, tag=role, bufs=BANKS[role])

        ctx.enter_context(tc.manual_schedule(engines={mybir.EngineType.Pool, mybir.EngineType.PE, mybir.EngineType.DVE, mybir.EngineType.Activation, mybir.EngineType.SP}))

        identity = const.tile([P, P], F32, name="identity")
        masks.make_identity(nc, identity[:])

        logits = const.tile([P, NS * H], BF16, name="logits")
        k_bias = const.tile([P, GROUP], BF16, name="k_bias")
        v_bias = const.tile([P, C], BF16, name="v_bias")

        k_rows = k_w.rearrange("(p t) k -> t p k", t=GROUP)
        raw_w = {}

        def fetch_w(name, ct):
            raw = raw_w_pool.tile([P, D], BF16, name="raw_w")
            nc.sync.dma_start(out=raw[:], in_=k_rows[ct] if name == "k" else v_w[ct * P : (ct + 1) * P, :])
            raw_w[(name, ct)] = raw

        def turn_rows(raw, role):
            words = raw[:].bitcast(F32)
            turned = bank([P, PASSES, 2, P], role)
            for g in range(PASSES):
                for u in range(2):
                    nc.tensor.transpose(turned[:, g, u, :], words[:, 2 * P * g + u : 2 * P * (g + 1) : 2], identity[:])
            return turned[:].rearrange("p g u n -> p g n u")

        def quantise(grouped, name, width):
            codes = keep.tile([P, PASSES, width], U32, name="%s_codes" % name, align_bytes=64)
            scales = keep.tile([P, PASSES, width], U8, name="%s_scales" % name, align_bytes=64)
            nc.vector.quantize_mx(
                out=codes[:].rearrange("p g c -> p (g c)").bitcast(FP8X4),
                scales=scales[:].rearrange("p g c -> p (g c)"),
                in_=grouped[:].rearrange("p g c t -> p (g c t)"),
            )
            return codes, scales

        w_mx = {}
        grouped_w = {}

        def turn_w(name, ct, copy):
            pair, n = divmod(ct, PAIR)
            if n == 0:
                grouped_w[(name, pair)] = grouped_w_pool.tile([P, PASSES, PAIR * P, 4], BF16, name="grouped_w", align_bytes=64)
            copy(out=grouped_w[(name, pair)][:, :, n * P : (n + 1) * P, :].bitcast(F32), in_=turn_rows(raw_w[(name, ct)], "swing"))

        def quantise_w(name, pair):
            codes, scales = quantise(grouped_w[(name, pair)], "%s%d" % (name, pair), PAIR * P)
            w_mx[(name + "_pair", pair)] = (codes, scales)
            for n in range(PAIR):
                w_mx[(name, PAIR * pair + n)] = (codes[:, :, n * P : (n + 1) * P], scales[:, :, n * P : (n + 1) * P])

        x_mx = {}
        norm = {}

        def multiply(out, stationary, moving):
            for g in range(PASSES):
                nc.tensor.matmul_mx(
                    out=out,
                    lhsT=stationary[0][:, g, :].bitcast(FP8X4),
                    lhsT_scale=stationary[1][:, g, :],
                    rhs=moving[0][:, g, :].bitcast(FP8X4),
                    rhs_scale=moving[1][:, g, :],
                    start=(g == 0),
                    stop=(g == PASSES - 1),
                )

        sums = {}
        squares = {}

        def square_k(ch, t):
            k_sums = bank([P, CHUNK], "swing")
            multiply(k_sums[:], w_mx[("k", t)], x_mx[ch])
            square = square_pool.tile([P, CHUNK], F32, name="square", bufs=9)
            nc.scalar.activation(out=square[:], in_=k_sums[:], func=ACT.Square, bias=k_bias[:, t : t + 1])
            squares[(ch, t)] = square
            if t < PARTIAL[ch]:
                sums[(ch, t)] = square
            if t >= GROUP - DIRECT[ch]:
                sums[(ch, PARTIAL[ch] + t - (GROUP - DIRECT[ch]))] = square

        def add_squares(ch, t):
            if PARTIAL[ch] <= t < GROUP - DIRECT[ch]:
                total = sums[(ch, t % PARTIAL[ch])]
                nc.vector.tensor_tensor(out=total[:], in0=total[:], in1=squares[(ch, t)][:], op=ALU.add)

        square_sums = {}

        def turn_sums(ch):
            turned = bank([P, R, P], "swing")
            for r in range(R):
                for n in range(PARTIAL[ch] + DIRECT[ch]):
                    nc.tensor.matmul(
                        turned[:, r, :], lhsT=sums[(ch, n)][:, r * P : (r + 1) * P], rhs=identity[:], is_transpose=True,
                        start=(n == 0), stop=(n == PARTIAL[ch] + DIRECT[ch] - 1),
                    )
            square_sums[ch] = turned

        def root(ch):
            summed = work.tile([P, R * H], F32, name="summed")
            nc.vector.tensor_reduce(
                out=summed[:], in_=square_sums[ch][:].rearrange("q r (h i) -> q (r h) i", i=P // H), axis=AX.X, op=ALU.add,
            )
            norm[ch] = keep.tile([P, R, H], F32, name="norm%d" % ch)
            nc.scalar.activation(out=norm[ch][:].rearrange("q r h -> q (r h)"), in_=summed[:], func=ACT.Sqrt)

        exts = {}

        def field_tile(g):
            if g < CT:
                exts[g] = ext_pool.tile([P, EXT, B, P], F32, name="ext%d" % g)
                fill = nc.vector if g == 0 else nc.gpsimd
                fill.memset(exts[g][0:1, 2:HALO, :, :], 0.0)
                fill.memset(exts[g][0:2, 0:2, :, :], 0.0)
            else:
                exts[g] = late_pool.tile([P, EXT, B, P], F32, name="ext_late")

        v_sums = {}
        biased = {}

        def project_v(unit):
            pair, batch = divmod(unit, B)
            a, ct = divmod(PAIR * pair, CT)
            ch = 2 * batch + a
            for j in range(R // 2):
                v_sums[j] = bank([P, 2, PAIR * P], "swing")
                for n in range(2):
                    tokens = slice((2 * j + n) * P, (2 * j + n + 1) * P)
                    multiply(
                        v_sums[j][:, n, :], (x_mx[ch][0][:, :, tokens], x_mx[ch][1][:, :, tokens]), w_mx[("v_pair", ct // PAIR)],
                    )

        def add_bias(unit):
            ct = unit // B * PAIR % CT
            for j in range(R // 2):
                biased[(unit, j)] = work.tile([P, 2, PAIR * P], F32, name="biased")
                nc.vector.tensor_tensor(
                    out=biased[(unit, j)][:], in0=v_sums[j][:], op=ALU.add,
                    in1=v_bias[:, ct * P : (ct + PAIR) * P].unsqueeze(1).to_broadcast([P, 2, PAIR * P]),
                )

        def write_field(unit, of_pair=range(PAIR)):
            pair, batch = divmod(unit, B)
            a, ct = divmod(PAIR * pair, CT)
            if batch == 0 and a == 1:
                field_tile(PAIR * pair)
                field_tile(PAIR * pair + 1)
            for r in range(R):
                for c in range(2 * of_pair[0], 2 * of_pair[-1] + 2):
                    g = PAIR * pair + c // 2
                    head = slice(c % 2 * HD, (c % 2 + 1) * HD)
                    h = 2 * ct + c
                    nc.scalar.activation(
                        out=exts[g][:, HALO + r, batch, head], in_=biased[(unit, r // 2)][:, r % 2, c * HD : (c + 1) * HD],
                        func=ACT.Copy, scale=norm[2 * batch + a][:, r, h : h + 1],
                    )
            if batch == 1:
                for n in of_pair:
                    g = PAIR * pair + n
                    halo(g)
                    if a == 0 and 3 <= g + 2 < CT:
                        field_tile(g + 2)

        def halo(g):
            ext = exts[g]
            for up, e_to, e_from in ((1, slice(2, HALO), slice(HALO, EXT)), (2, slice(0, 2), slice(EXT - 2, EXT))):
                for lo, hi in ((0, SPREAD), (SPREAD, P - up)):
                    if lo < hi:
                        queue = nc.gpsimd if lo == 0 or g < CT else nc.sync
                        queue.dma_start(out=ext[lo + up : hi + up, e_to, :, :], in_=ext[lo:hi, e_from, :, :])
                if g >= CT:
                    nc.sync.dma_start(out=ext[0:up, e_to, :, :], in_=exts[g - CT][P - up : P, e_from, :, :])

        filtered = {}
        fars = {}

        def far_shifts(g, half):
            a, ct = divmod(g, CT)
            h = 2 * ct + half
            head = slice(half * HD, (half + 1) * HD)
            far = bank([P, R, B, HD], "swing")
            nc.tensor.matmul(far[:], lhsT=toeplitz[h][:, 0:P], rhs=exts[g][:, HALO:EXT, :, head], start=True, stop=(a == 0))
            if a == 1:
                nc.tensor.matmul(far[:], lhsT=toeplitz[h][:, P : 2 * P], rhs=exts[ct][:, HALO:EXT, :, head], start=False, stop=True)
            fars[(g, half)] = far

        def near_shifts(g):
            filtered[g] = filtered_pool.tile([P, R, B, P], F32, name="filtered")
            pieces = (slice(0, 1), slice(1, B)) if g == STEPS - 1 else (slice(0, B),)
            for batches in pieces:
                for shift in NEAR:
                    tile_of, j = coefficient[shift]
                    for half in range(2):
                        h = 2 * (g % CT) + half
                        head = slice(half * HD, (half + 1) * HD)
                        target = filtered[g][:, :, batches, head]
                        nc.vector.scalar_tensor_tensor(
                            out=target, in0=exts[g][:, HALO - shift : EXT - shift, batches, head], scalar=tile_of[:, h, j : j + 1],
                            in1=(fars[(g, half)][:, :, batches, :] if shift == NEAR[0] else target), op0=ALU.mult, op1=ALU.add,
                        )

        turned_out = {}
        results = {}

        def turn_out(g, batch):
            turned_out[batch] = bank([P, R, P], "swing")
            for r in range(R):
                nc.tensor.transpose(turned_out[batch][:, r, :], filtered[g][:, r, batch, :], identity[:])

        def copy_out(g, batch):
            a, ct = divmod(g, CT)
            results[batch] = out_pool.tile([P, CHUNK], F32, name="result")
            copy = nc.vector.tensor_copy if (g, batch) == (STEPS - 1, 1) else nc.scalar.copy
            copy(out=results[batch][:].rearrange("p (q r) -> p q r", r=R), in_=turned_out[batch][:].rearrange("p r q -> p q r"))
            nc.sync.dma_start(out=out_0[batch, ct * P : (ct + 1) * P, CHUNK * a : CHUNK * (a + 1)], in_=results[batch][:])

        def cast_out(g, batch):
            a, ct = divmod(g, CT)
            as_fp8 = out_pool.tile([P, CHUNK], FP8, name="as_fp8")
            if (g, batch) == (STEPS - 1, 1):
                nc.vector.tensor_scalar(out=as_fp8[:], in0=results[batch][:], scalar1=Y_SCALE, scalar2=None, op0=ALU.mult, saturate=False)
            else:
                nc.scalar.activation(out=as_fp8[:], in_=results[batch][:], func=ACT.Copy, scale=Y_SCALE, saturate=False)
            nc.sync.dma_start(out=out_1[batch, ct * P : (ct + 1) * P, CHUNK * a : CHUNK * (a + 1)], in_=as_fp8[:].bitcast(U8))

        pending = []

        def background_turns(tasks):
            for task in tasks:
                if task[0] == "w":
                    turn_w("v", task[1], nc.scalar.copy)
                    if task[1] % PAIR:
                        pending.append(("qw", "v", task[1] // PAIR))
                elif task[0] == "x":
                    turn_x(task[1], task[2])
                    if task[2] == R - 1:
                        pending.append(("qx", task[1]))

        def step(i):
            tasks = beside.get(i, ())
            todo = list(pending)
            pending.clear()
            if i == -3:
                background_turns(tasks)
            if i + 5 < STEPS:
                project_v(i + 5)
            fields = {STEPS // 2 - 4: (), STEPS // 2 - 3: (STEPS // 2, STEPS // 2 + 1)}.get(i, (i + 4,))
            for unit in fields:
                if 2 <= unit < STEPS:
                    write_field(unit)
            if 0 <= i + 1 < STEPS:
                near_shifts(i + 1)
            if 0 <= i + 2 < STEPS:
                far_shifts(i + 2, 0)
                if i < 0:
                    far_shifts(i + 2, 1)
            if 0 <= i:
                turn_out(i, 0)
                turn_out(i, 1)
                copy_out(i, 0)
                copy_out(i, 1)
            if i > -3:
                background_turns(tasks)
            for task in tasks:
                if task[0] == "norm":
                    turn_sums(task[1])
            if 0 <= i and i + 2 < STEPS:
                far_shifts(i + 2, 1)
            if 0 <= i:
                cast_out(i, 0)
                cast_out(i, 1)
            if i + 5 < STEPS:
                add_bias(i + 5)
            for task in todo:
                if task[0] == "qw":
                    quantise_w(task[1], task[2])
                elif task[0] == "qx":
                    x_mx[task[1]] = quantise(grouped_x[task[1]], "x%d" % task[1], CHUNK)
                elif task[0] == "add":
                    add_squares(task[1], task[2])
            for task in tasks:
                if task[0] == "norm":
                    root(task[1])
            for task in tasks:
                if task[0] == "k":
                    for t in task[2]:
                        square_k(task[1], t)
                        pending.append(("add", task[1], t))

        with tc.tile_pool(name="raw_x_pool", bufs=4) as raw_x_pool, tc.tile_pool(name="grouped_x_pool", bufs=2) as grouped_x_pool, tc.tile_pool(name="raw_w_pool", bufs=7) as raw_w_pool, tc.tile_pool(name="grouped_w_pool", bufs=2) as grouped_w_pool, tc.tile_pool(name="square_pool", bufs=1) as square_pool:
            raw_x = {}
            grouped_x = {}

            def fetch_x(ch, r):
                raw = raw_x_pool.tile([P, D], BF16, name="raw_x")
                nc.sync.dma_start(out=raw[:], in_=x_rows[CHUNK * ch + r : CHUNK * (ch + 1) : R, :])
                raw_x[(ch, r)] = raw

            def turn_x(ch, r, copy=nc.scalar.copy):
                if r == 0:
                    grouped_x[ch] = grouped_x_pool.tile([P, PASSES, CHUNK, 4], BF16, name="grouped_x", align_bytes=64)
                copy(
                    out=grouped_x[ch][:, :, r * P : (r + 1) * P, :].bitcast(F32),
                    in_=turn_rows(raw_x[(ch, r)], "swing"),
                )

            fetch_x(0, 0)
            nc.sync.dma_start(out=logits[:], in_=scale_gain.rearrange("j h -> (j h)").partition_broadcast(P))
            for r in range(1, R):
                fetch_x(0, r)
            for t in range(GROUP):
                fetch_w("k", t)
            nc.sync.dma_start(out=k_bias[:], in_=k_b.rearrange("(p t) -> p t", t=GROUP))
            for r in range(2):
                fetch_x(2, r)

            field_tile(0)
            shifted = const.tile([P, H, NS], F32, name="shifted")
            nc.vector.tensor_copy(out=shifted[:], in_=logits[:].rearrange("p (j h) -> p h j", j=NS))
            largest = const.tile([P, H], F32, name="largest")
            nc.vector.tensor_reduce(out=largest[:], in_=shifted[:], axis=AX.X, op=ALU.max)
            nc.vector.tensor_tensor(
                out=shifted[:], in0=shifted[:], in1=largest[:].unsqueeze(2).to_broadcast([P, H, NS]), op=ALU.subtract,
            )
            exps = const.tile([P, H, NS], F32, name="exps")
            nc.scalar.activation(out=exps[:], in_=shifted[:], func=ACT.Exp)
            total = const.tile([P, H], F32, name="total")
            nc.vector.tensor_reduce(out=total[:], in_=exps[:], axis=AX.X, op=ALU.add)
            inverse = const.tile([P, H], F32, name="inverse")
            nc.vector.reciprocal(out=inverse[:], in_=total[:])
            gain = const.tile([P, H, NS], F32, name="gain")
            nc.vector.tensor_tensor(
                out=gain[:], in0=exps[:], in1=inverse[:].unsqueeze(2).to_broadcast([P, H, NS]), op=ALU.mult,
            )
            t1_gain = const.tile([P, H, NS], F32, name="t1_gain")
            nc.vector.tensor_scalar(out=t1_gain[:], in0=gain[:], scalar1=T1, scalar2=None, op0=ALU.mult)
            pow2 = const.tile([P, H, NS], F32, name="pow2")
            nc.vector.tensor_scalar(out=pow2[:], in0=gain[:], scalar1=T2, scalar2=None, op0=ALU.mult)
            nc.vector.tensor_tensor(out=pow2[:, :, 1:NS], in0=pow2[:, :, 1:NS], in1=t1_gain[:, :, 0 : NS - 1], op=ALU.add)
            triple = const.tile([P, H, NS], F32, name="triple")
            nc.vector.tensor_scalar(out=triple[:], in0=gain[:], scalar1=T0, scalar2=None, op0=ALU.mult)
            coefficient = {}
            for j in range(NS):
                coefficient[2 ** j] = (pow2, j)
                coefficient[3 * 2 ** j] = (triple, j)

            toeplitz = {}
            rows = keep.tile([P, H, 2 * P], F32, name="toeplitz_rows")
            nc.gpsimd.memset(rows[:], 0.0)
            nc.vector.tensor_scalar(
                out=rows[0:1, :, 0:1], in0=gain[0:1, :, 0:1], scalar1=0.0, scalar2=T3, op0=ALU.mult, op1=ALU.add,
            )
            for shift in sorted(coefficient):
                if shift % R == 0 and shift < N:
                    tile_of, j = coefficient[shift]
                    nc.vector.tensor_copy(out=rows[0:1, :, shift // R : shift // R + 1], in_=tile_of[0:1, :, j : j + 1])
            for h in range(H):
                toeplitz[h] = rows[:, h, :]

            def copy_rows(queue, heads, count):
                for down in range(count, min(4 * count, P), count):
                    queue.dma_start(out=rows[down : down + count, heads, down : 2 * P], in_=rows[0:count, heads, 0 : 2 * P - down])

            first_heads, other_heads = slice(0, 6), slice(6, H)
            copy_rows(nc.sync, first_heads, 1)
            for r in range(2, R):
                fetch_x(2, r)
            for ct in range(PAIR):
                fetch_w("v", ct)
            copy_rows(nc.sync, first_heads, 4)
            copy_rows(nc.gpsimd, other_heads, 1)
            field_tile(1)
            copy_rows(nc.gpsimd, other_heads, 4)
            field_tile(2)
            copy_rows(nc.gpsimd, other_heads, 16)


            for r in range(R):
                turn_x(0, r)
            for t in range(R):
                turn_w("k", t, nc.scalar.copy)
            x_mx[0] = quantise(grouped_x[0], "x0", CHUNK)
            quantise_w("k", 0)
            turn_w("k", 4, nc.vector.tensor_copy)
            turn_w("k", 5, nc.vector.tensor_copy)
            quantise_w("k", 1)
            quantise_w("k", 2)
            root_of_one = const.tile([P, 1], F32, name="root_of_one")
            nc.scalar.activation(out=root_of_one[:], in_=identity[:, 0:1], func=ACT.Sqrt)
            square_k(0, 0)
            square_k(0, 1)
            turn_w("k", 6, nc.vector.tensor_copy)
            turn_w("k", 7, nc.vector.tensor_copy)
            quantise_w("k", 3)
            turn_x(2, 0)
            turn_x(2, 1)
            square_k(0, 2)
            square_k(0, 3)
            for t in range(4):
                add_squares(0, t)
            turn_x(2, 2)
            turn_x(2, 3, nc.vector.tensor_copy)
            square_k(0, 4)
            square_k(0, 5)
            x_mx[2] = quantise(grouped_x[2], "x2", CHUNK)
            add_squares(0, 4)
            add_squares(0, 5)
            square_k(0, 6)
            square_k(0, 7)
            for ct in range(PAIR, 2 * PAIR):
                fetch_w("v", ct)
            copy_rows(nc.sync, first_heads, 16)
            for r in range(R):
                fetch_x(1, r)
            nc.sync.dma_start(out=v_bias[:], in_=v_b.partition_broadcast(P))
            copy_rows(nc.sync, first_heads, 64)
            for ct in range(2 * PAIR, CT):
                fetch_w("v", ct)
            for r in range(R):
                fetch_x(3, r)
            square_k(2, 0)
            square_k(2, 1)
            add_squares(0, 6)
            add_squares(0, 7)
            for n in range(PAIR):
                turn_w("v", n, nc.vector.tensor_copy)
            square_k(2, 2)
            square_k(2, 3)
            quantise_w("v", 0)
            add_squares(2, 0)
            add_squares(2, 1)
            add_squares(2, 2)
            add_squares(2, 3)
            square_k(2, 4)
            square_k(2, 5)
            add_squares(2, 4)
            add_squares(2, 5)
            square_k(2, 6)
            square_k(2, 7)
            turn_sums(0)
            root(0)
            for n in range(PAIR):
                turn_w("v", PAIR + n, nc.scalar.copy)
            project_v(0)
            add_squares(2, 6)
            add_squares(2, 7)
            turn_sums(2)
            add_bias(0)
            write_field(0, (0,))
            project_v(1)
            root(2)
            add_bias(1)
            write_field(1, (0,))
            write_field(0, (1,))
            write_field(1, (1,))
            copy_rows(nc.gpsimd, other_heads, 64)
            quantise_w("v", 1)

            beside = {
                -3: [("w", 4), ("w", 5), ("x", 1, 0), ("x", 1, 1)],
                -2: [("x", 1, 2), ("x", 1, 3)],
                -1: [("x", 3, 0), ("x", 3, 1), ("w", 6), ("w", 7)],
                0: [("x", 3, 2), ("x", 3, 3), ("k", 1, range(0, 4))],
                1: [("k", 1, range(4, 8))],
                2: [("k", 3, range(0, 4))],
                3: [("norm", 1), ("k", 3, range(4, 8))],
                4: [("norm", 3)],
            }
            for i in range(-3, 5):
                step(i)
        late_pool = ctx.enter_context(tc.tile_pool(name="late_pool", bufs=5))
        for i in range(5, STEPS):
            step(i)
